import numpy as np
import ml_dtypes


def mxq(x, axis, fmt="e4m3"):
    dtype, down = {"e4m3": (ml_dtypes.float8_e4m3fn, 7), "e5m2": (ml_dtypes.float8_e5m2, 14)}[fmt]
    v = np.moveaxis(np.asarray(x, np.float32).astype(ml_dtypes.bfloat16).astype(np.float64), axis, -1)
    blocks = v.reshape(v.shape[:-1] + (-1, 32))
    amax = np.abs(blocks).max(-1, keepdims=True)
    byte = np.maximum(np.where(amax > 0, np.frexp(amax)[1] - 1 + 127, 0) - down, 1)
    scale = np.exp2(byte - 127.0)
    codes = (blocks / scale).astype(np.float32).astype(dtype).astype(np.float64)
    return np.moveaxis((codes * scale).reshape(v.shape), -1, axis)


WIDE = False


def mx_kscale(k):
    if not WIDE:
        return np.ones(k)
    levels = np.array([30, -30])
    if k % 512:
        return np.exp2(np.random.permutation(np.resize(levels, k // 32))).repeat(32)
    a = np.empty((k // 512, 16))
    for p in range(k // 512):
        a[p, :8] = np.random.permutation(np.resize(levels, 8))
        for g in range(8):
            far = levels[np.abs(levels - a[p, g]) >= 10]
            a[p, g + 8] = far[np.random.randint(len(far))]
    return np.exp2(a.ravel()).repeat(32)


BF16 = ml_dtypes.bfloat16


def bf(x):
    return np.asarray(x, np.float32).astype(BF16)


def f64(x):
    return np.asarray(x).astype(np.float64)


B, T, D, DH, H, W = 1, 1024, 512, 512, 4, 512
ROPE_BASE = 10000.0
EPS = 1.1920929e-07


def rope(u):
    freqs = ROPE_BASE ** (-2.0 * np.arange(DH // 2) / DH)
    theta = np.arange(T)[:, None] * freqs[None, :]
    cos, sin = np.cos(theta), np.sin(theta)
    u1, u2 = u[..., 0::2], u[..., 1::2]
    return np.stack([u1 * cos - u2 * sin, u1 * sin + u2 * cos], axis=-1).reshape(u.shape)


def rmsnorm(u, w):
    return u * (1.0 / np.sqrt(np.mean(u * u, axis=-1, keepdims=True) + EPS)) * w


def setup_inputs():
    s = mx_kscale(D)
    return {"x": bf(np.random.standard_normal((B, T, D)) * s),
            "wq": bf(np.random.standard_normal((H * DH, D)) / np.sqrt(D) / s),
            "wkv": bf(np.random.standard_normal((2 * DH, D)) * 2.0 / np.sqrt(D) / s),
            "q_norm_w": bf(1.0 + 0.1 * np.random.standard_normal(DH)),
            "k_norm_w": bf(1.0 + 0.1 * np.random.standard_normal(DH))}


def reference(x, wq, wkv, q_norm_w, k_norm_w):
    xq = mxq(f64(x), 2, "e5m2")
    q = xq @ mxq(f64(wq), 1, "e5m2").T
    kv = xq @ mxq(f64(wkv), 1, "e5m2").T
    k, v = kv[..., :DH], kv[..., DH:]
    q = q.reshape(B, T, H, DH).transpose(0, 2, 1, 3)
    q_rot = rmsnorm(rope(q), f64(q_norm_w))
    k_rot = rmsnorm(rope(k), f64(k_norm_w))
    return q_rot, k_rot, v

@@ -1,0 +1,260 @@
+import math
+from contextlib import ExitStack
+
+import concourse.mybir as mybir
+from concourse.masks import make_identity
+
+FLOPS = 2 * 1024 * 512 * 3072
+
+F32 = mybir.dt.float32
+BF16 = mybir.dt.bfloat16
+I32 = mybir.dt.int32
+U32 = mybir.dt.uint32
+U8 = mybir.dt.uint8
+E5X4 = mybir.dt.float8_e5m2_x4
+ALU = mybir.AluOpType
+ACT = mybir.ActivationFunctionType
+
+P = 128
+T = 1024
+D = 512
+NT = T // P
+PAIRS = D // 2
+EPS = 1.1920929e-07
+TWO_PI = 2.0 * math.pi
+STEP = 10000.0 ** (-1.0 / PAIRS)
+G_TILES = (0, 1, 2, 3)
+
+
+def tile_attention_pa_kernel(tc, x, wq, wkv, q_norm_w, k_norm_w, out_0, out_1, out_2):
+    nc = tc.nc
+    with ExitStack() as ctx:
+        const = ctx.enter_context(tc.tile_pool(name="const", bufs=1))
+        mmp = ctx.enter_context(tc.tile_pool(name="mmp", bufs=4))
+        outp = ctx.enter_context(tc.tile_pool(name="outp", bufs=6))
+        rkp = ctx.enter_context(tc.tile_pool(name="rkp", bufs=2))
+        vop = ctx.enter_context(tc.tile_pool(name="vop", bufs=2))
+        jp = ctx.enter_context(tc.tile_pool(name="jp", bufs=2))
+        ps_t = ctx.enter_context(tc.psum_pool(name="ps_t", bufs=2))
+        ps_s = ctx.enter_context(tc.psum_pool(name="ps_s", bufs=2))
+        ps_v = ctx.enter_context(tc.psum_pool(name="ps_v", bufs=3))
+        ps_w = ctx.enter_context(tc.psum_pool(name="ps_w", bufs=1))
+
+        ident = const.tile([P, P], F32, name="ident")
+        ones_bf = const.tile([P, P], BF16, name="ones_bf")
+        wrow = const.tile([P, 2 * D], BF16, name="wrow")
+        x_sb = const.tile([P, NT, D], BF16, name="x_sb")
+        w_sb = const.tile([P, 24, D], BF16, name="w_sb")
+        gx = const.tile([P, 4 * T], BF16, name="gx", align_bytes=64)
+        gw = const.tile([P, 4 * 3072], BF16, name="gw", align_bytes=64)
+        x_codes = const.tile([P, T], U32, name="x_codes", align_bytes=64)
+        x_scales = const.tile([P, T], U8, name="x_scales", align_bytes=64)
+        w_codes = const.tile([P, 3072], U32, name="w_codes", align_bytes=64)
+        w_scales = const.tile([P, 3072], U8, name="w_scales", align_bytes=64)
+        one = const.tile([P, 1], F32, name="one")
+        warm = const.tile([P, 1], F32, name="warm")
+        turns = const.tile([P, PAIRS], F32, name="turns")
+        tcol = const.tile([P, NT], F32, name="tcol")
+        phi = const.tile([P, NT, PAIRS], F32, name="phi")
+        kint = const.tile([P, NT, PAIRS], I32, name="kint")
+        frac = const.tile([P, NT, PAIRS], F32, name="frac")
+        afrac = const.tile([P, NT, PAIRS], F32, name="afrac")
+        planes = const.tile([P, NT, 3, PAIRS], F32, name="planes")
+        tq = const.tile([P, NT, 2, D], F32, name="tq")
+        wq_sb = const.tile([P, D], F32, name="wq_sb")
+        ms = const.tile([P, NT, 8], F32, name="ms")
+        mse = const.tile([P, NT, 8], F32, name="mse")
+        rstd = const.tile([P, NT, 8], F32, name="rstd")
+        nh = const.tile([P, 8], F32, name="nh")
+
+        nc.vector.memset(one[:], 1.0)
+        nc.vector.memset(wrow[:], 0.0)
+        nc.vector.memset(ones_bf[:], 1.0)
+        nc.scalar.activation(out=warm[:], in_=one[:], func=ACT.Sin)
+        nc.gpsimd.iota(tcol[:], pattern=[[P, NT]], base=0, channel_multiplier=1,
+                       allow_small_or_imprecise_dtypes=True)
+        make_identity(nc, ident[:])
+        nc.gpsimd.memset(nh[:], -0.5)
+
+        xv = x.flatten_outer_dims().rearrange("(a p) k -> p a k", p=P)
+        wqv = wq.rearrange("(j p) k -> p j k", p=P)
+        wkvv = wkv.rearrange("(j p) k -> p j k", p=P)
+        nc.sync.dma_start(out=x_sb[:, 0:2, :], in_=xv[:, 0:2, :])
+        nc.sync.dma_start(out=wrow[0:1, 0:D], in_=q_norm_w.rearrange("(o d) -> o d", o=1))
+        nc.sync.dma_start(out=wrow[0:1, D:2 * D], in_=k_norm_w.rearrange("(o d) -> o d", o=1))
+        for h in range(4):
+            nc.sync.dma_start(out=w_sb[:, 4 * h:4 * h + 4, :], in_=wqv[:, 4 * h:4 * h + 4, :])
+        for h in range(2):
+            nc.sync.dma_start(out=w_sb[:, 16 + 4 * h:20 + 4 * h, :], in_=wkvv[:, 4 * h:4 * h + 4, :])
+        for c in range(1, 4):
+            nc.sync.dma_start(out=x_sb[:, 2 * c:2 * c + 2, :], in_=xv[:, 2 * c:2 * c + 2, :])
+
+        for j in range(4):
+            nc.vector.tensor_scalar_mul(out=turns[:, j:j + 1], in0=one[:], scalar1=STEP ** j / TWO_PI)
+        w = 4
+        while w < PAIRS:
+            for m in range(1, 4):
+                nc.vector.tensor_scalar_mul(out=turns[:, m * w:(m + 1) * w], in0=turns[:, 0:w],
+                                            scalar1=STEP ** (m * w))
+            w *= 4
+        chunks = ((0, 2), (2, 4), (4, 8))
+        for a0, a1 in chunks:
+            for a in range(a0, a1):
+                nc.vector.tensor_scalar_mul(out=phi[:, a, :], in0=turns[:], scalar1=tcol[:, a:a + 1])
+            nc.vector.tensor_copy(out=kint[:, a0:a1, :], in_=phi[:, a0:a1, :])
+            nc.vector.tensor_tensor(out=frac[:, a0:a1, :], in0=phi[:, a0:a1, :], in1=kint[:, a0:a1, :],
+                                    op=ALU.subtract)
+
+        def trig(a0, a1):
+            nc.scalar.activation(out=afrac[:, a0:a1, :], in_=frac[:, a0:a1, :], func=ACT.Abs)
+            nc.scalar.activation(out=planes[:, a0:a1, 0, :], in_=afrac[:, a0:a1, :], func=ACT.Sin,
+                                 scale=-TWO_PI, bias=math.pi / 2)
+            nc.scalar.activation(out=planes[:, a0:a1, 1, :], in_=frac[:, a0:a1, :], func=ACT.Sin,
+                                 scale=TWO_PI)
+            nc.scalar.activation(out=planes[:, a0:a1, 2, :], in_=afrac[:, a0:a1, :], func=ACT.Sin,
+                                 scale=TWO_PI, bias=-math.pi / 2)
+
+        wqb = ps_v.tile([P, D], F32, tag="v", name="wqb")
+        wkb = ps_w.tile([P, D], F32, name="wkb")
+
+        def gains():
+            nc.tensor.matmul(out=wqb[:], lhsT=ones_bf[:], rhs=wrow[:, 0:D], start=True, stop=True)
+            nc.tensor.matmul(out=wkb[:], lhsT=ones_bf[:], rhs=wrow[:, D:2 * D], start=True, stop=True)
+            nc.scalar.copy(out=wq_sb[:], in_=wqb[:])
+
+        def turn(src, dst, on_vector):
+            tp = ps_t.tile([P, 2, 2, P], F32, tag="tp", name="tp")
+            for rt in range(2):
+                words = src[:, rt, :].bitcast(F32)
+                for u in range(2):
+                    nc.tensor.transpose(tp[:, rt, u, :], words[:, u:PAIRS:2], ident[:])
+            view = tp[:].rearrange("p c u r -> p c r u")
+            if on_vector:
+                nc.vector.tensor_copy(out=dst, in_=view)
+            else:
+                nc.scalar.copy(out=dst, in_=view)
+
+        gxw = gx[:].bitcast(F32).rearrange("p (c r u) -> p c r u", r=P, u=2)
+        gww = gw[:].bitcast(F32).rearrange("p (c r u) -> p c r u", r=P, u=2)
+
+        def prep_x(c, on_vector):
+            turn(x_sb[:, 2 * c:2 * c + 2, :], gxw[:, 2 * c:2 * c + 2, :, :], on_vector)
+            nc.vector.quantize_mx(out=x_codes[:, 256 * c:256 * (c + 1)].bitcast(E5X4),
+                                  scales=x_scales[:, 256 * c:256 * (c + 1)],
+                                  in_=gx[:, 1024 * c:1024 * (c + 1)])
+
+        def prep_w(grp, on_vector):
+            for b in range(2):
+                j = 4 * grp + 2 * b
+                turn(w_sb[:, j:j + 2, :], gww[:, j:j + 2, :, :], on_vector)
+            nc.vector.quantize_mx(out=w_codes[:, D * grp:D * (grp + 1)].bitcast(E5X4),
+                                  scales=w_scales[:, D * grp:D * (grp + 1)],
+                                  in_=gw[:, 4 * D * grp:4 * D * (grp + 1)])
+
+        def build_t(eng, wsrc, a):
+            wv = wsrc[:].rearrange("p (i r) -> p r i", r=2)
+            for r in range(2):
+                eng.tensor_tensor(out=tq[:, a, r, :].rearrange("p (i e) -> p i e", e=2),
+                                  in0=wv[:, r, :].unsqueeze(2).to_broadcast([P, PAIRS, 2]),
+                                  in1=planes[:, a, r:r + 2, :].rearrange("p e i -> p i e"),
+                                  op=ALU.mult)
+
+        def mx(ps, a, grp):
+            nc.tensor.matmul_mx(out=ps[:],
+                                lhsT=x_codes[:, P * a:P * (a + 1)].bitcast(E5X4),
+                                lhsT_scale=x_scales[:, P * a:P * (a + 1)],
+                                rhs=w_codes[:, D * grp:D * (grp + 1)].bitcast(E5X4),
+                                rhs_scale=w_scales[:, D * grp:D * (grp + 1)],
+                                start=True, stop=True)
+
+        def square(a, grp):
+            ps = ps_s.tile([P, D], F32, tag="s", name="ps")
+            mx(ps, a, grp)
+            junk = jp.tile([P, D], BF16, tag="junk", name="junk")
+            nc.scalar.activation(out=junk[:], in_=ps[:], func=ACT.Square, scale=1.0 / math.sqrt(D),
+                                 accum_out=ms[:, a, grp:grp + 1])
+
+        def value(a):
+            ps = ps_s.tile([P, D], F32, tag="s", name="ps")
+            mx(ps, a, 5)
+            vo = vop.tile([P, D], F32, tag="vo", name="vo")
+            nc.scalar.copy(out=vo[:], in_=ps[:])
+            nc.sync.dma_start(out=out_2[0, P * a:P * (a + 1), :], in_=vo[:])
+
+        def norms(a):
+            nc.gpsimd.tensor_scalar(out=mse[:, a, 0:5], in0=ms[:, a, 0:5], scalar1=1.0, scalar2=EPS,
+                                    op0=ALU.mult, op1=ALU.add)
+            nc.gpsimd.tensor_tensor(out=rstd[:, a, 0:5], in0=mse[:, a, 0:5], in1=nh[:, 0:5], op=ALU.pow)
+
+        def combine(dst, mm):
+            mv = mm[:].rearrange("p r (i e) -> p e i r", e=2)
+            nc.gpsimd.tensor_tensor(out=dst[:].rearrange("p (i r) -> p i r", r=2),
+                                    in0=mv[:, 0], in1=mv[:, 1], op=ALU.subtract)
+
+        def rope_q(a, h):
+            ps = ps_v.tile([P, D], F32, tag="v", name="ps")
+            mx(ps, a, h)
+            mm = mmp.tile([P, 2, D], F32, tag="mm", name="mm")
+            nc.vector.scalar_tensor_tensor(out=mm[:], in0=ps[:].unsqueeze(1).to_broadcast([P, 2, D]),
+                                           scalar=rstd[:, a, h:h + 1], in1=tq[:, a, :, :],
+                                           op0=ALU.mult, op1=ALU.mult)
+            o = outp.tile([P, D], F32, tag="o", name="o")
+            combine(o, mm)
+            nc.sync.dma_start(out=out_0[0, h, P * a:P * (a + 1), :], in_=o[:])
+
+        def rope_k(a):
+            ps = ps_v.tile([P, D], F32, tag="v", name="ps")
+            mx(ps, a, 4)
+            mm = mmp.tile([P, 2, D], F32, tag="mm", name="mm")
+            pv = ps[:].rearrange("p (i e) -> p i e", e=2)
+            for r in range(2):
+                nc.vector.tensor_tensor(out=mm[:, r, :].rearrange("p (i e) -> p i e", e=2), in0=pv,
+                                        in1=planes[:, a, r:r + 2, :].rearrange("p e i -> p i e"),
+                                        op=ALU.mult)
+            rk = rkp.tile([P, D], F32, tag="rk", name="rk")
+            combine(rk, mm)
+            o = outp.tile([P, D], F32, tag="o", name="o")
+            nc.vector.scalar_tensor_tensor(out=o[:], in0=rk[:], scalar=rstd[:, a, 4:5], in1=wkb[:],
+                                           op0=ALU.mult, op1=ALU.mult)
+            nc.sync.dma_start(out=out_1[0, P * a:P * (a + 1), :], in_=o[:])
+
+        trig(0, 2)
+        gains()
+        prep_x(0, True)
+        prep_w(0, True)
+        trig(2, 4)
+        build_t(nc.gpsimd, wq_sb, 0)
+        square(0, 0)
+        prep_w(1, False)
+        square(0, 1)
+        build_t(nc.gpsimd, wq_sb, 1)
+        prep_w(2, False)
+        square(0, 2)
+        trig(4, 8)
+        prep_w(3, False)
+        square(0, 3)
+        prep_w(4, False)
+        square(0, 4)
+        norms(0)
+        prep_w(5, False)
+        value(0)
+        for a in range(2, NT):
+            if a in G_TILES:
+                build_t(nc.gpsimd, wq_sb, a)
+            else:
+                build_t(nc.vector, wqb, a)
+        for c in range(1, 4):
+            prep_x(c, False)
+
+        for a in range(NT):
+            for j in range(6):
+                if j < 4:
+                    rope_q(a, j)
+                elif j == 4:
+                    rope_k(a)
+                if a + 1 < NT:
+                    if j < 5:
+                        square(a + 1, j)
+                    else:
+                        value(a + 1)
+                        norms(a + 1)

@@ -23,7 +23,7 @@ PAIRS = D // 2
 EPS = 1.1920929e-07
 TWO_PI = 2.0 * math.pi
 STEP = 10000.0 ** (-1.0 / PAIRS)
-G_TILES = (0, 1, 2, 3)
+G_TILES = ()
 
 
 def tile_attention_pa_kernel(tc, x, wq, wkv, q_norm_w, k_norm_w, out_0, out_1, out_2):
@@ -32,15 +32,16 @@ def tile_attention_pa_kernel(tc, x, wq, wkv, q_norm_w, k_norm_w, out_0, out_1, o
         const = ctx.enter_context(tc.tile_pool(name="const", bufs=1))
         mmp = ctx.enter_context(tc.tile_pool(name="mmp", bufs=4))
         outp = ctx.enter_context(tc.tile_pool(name="outp", bufs=6))
-        rkp = ctx.enter_context(tc.tile_pool(name="rkp", bufs=2))
         vop = ctx.enter_context(tc.tile_pool(name="vop", bufs=2))
         jp = ctx.enter_context(tc.tile_pool(name="jp", bufs=2))
         ps_t = ctx.enter_context(tc.psum_pool(name="ps_t", bufs=2))
         ps_s = ctx.enter_context(tc.psum_pool(name="ps_s", bufs=2))
         ps_v = ctx.enter_context(tc.psum_pool(name="ps_v", bufs=3))
-        ps_w = ctx.enter_context(tc.psum_pool(name="ps_w", bufs=1))
+        ps_k = ctx.enter_context(tc.psum_pool(name="ps_k", bufs=1))
 
         ident = const.tile([P, P], F32, name="ident")
+        nident = const.tile([P, P], F32, name="nident")
+        wk_sb = const.tile([P, D], F32, name="wk_sb")
         ones_bf = const.tile([P, P], BF16, name="ones_bf")
         wrow = const.tile([P, 2 * D], BF16, name="wrow")
         x_sb = const.tile([P, NT, D], BF16, name="x_sb")
@@ -75,17 +76,21 @@ def tile_attention_pa_kernel(tc, x, wq, wkv, q_norm_w, k_norm_w, out_0, out_1, o
                        allow_small_or_imprecise_dtypes=True)
         make_identity(nc, ident[:])
         nc.gpsimd.memset(nh[:], -0.5)
+        nc.gpsimd.tensor_scalar(out=nident[:], in0=ident[:], scalar1=-1.0, scalar2=0.0, op0=ALU.mult, op1=ALU.add)
 
         xv = x.flatten_outer_dims().rearrange("(a p) k -> p a k", p=P)
-        wqv = wq.rearrange("(j p) k -> p j k", p=P)
-        wkvv = wkv.rearrange("(j p) k -> p j k", p=P)
+        wqv = wq.rearrange("(h b p e) k -> h e p b k", h=4, p=P, e=2)
+        wkv2 = wkv.rearrange("(h b p e) k -> h e p b k", h=2, p=P, e=2)
+        wvv = wkv.rearrange("(j p) k -> p j k", p=P)
         nc.sync.dma_start(out=x_sb[:, 0:2, :], in_=xv[:, 0:2, :])
         nc.sync.dma_start(out=wrow[0:1, 0:D], in_=q_norm_w.rearrange("(o d) -> o d", o=1))
         nc.sync.dma_start(out=wrow[0:1, D:2 * D], in_=k_norm_w.rearrange("(o d) -> o d", o=1))
         for h in range(4):
-            nc.sync.dma_start(out=w_sb[:, 4 * h:4 * h + 4, :], in_=wqv[:, 4 * h:4 * h + 4, :])
-        for h in range(2):
-            nc.sync.dma_start(out=w_sb[:, 16 + 4 * h:20 + 4 * h, :], in_=wkvv[:, 4 * h:4 * h + 4, :])
+            for e in range(2):
+                nc.sync.dma_start(out=w_sb[:, 4 * h + 2 * e:4 * h + 2 * e + 2, :], in_=wqv[h, e])
+        for e in range(2):
+            nc.sync.dma_start(out=w_sb[:, 16 + 2 * e:18 + 2 * e, :], in_=wkv2[0, e])
+        nc.sync.dma_start(out=w_sb[:, 20:24, :], in_=wvv[:, 4:8, :])
         for c in range(1, 4):
             nc.sync.dma_start(out=x_sb[:, 2 * c:2 * c + 2, :], in_=xv[:, 2 * c:2 * c + 2, :])
 
@@ -115,12 +120,13 @@ def tile_attention_pa_kernel(tc, x, wq, wkv, q_norm_w, k_norm_w, out_0, out_1, o
                                  scale=TWO_PI, bias=-math.pi / 2)
 
         wqb = ps_v.tile([P, D], F32, tag="v", name="wqb")
-        wkb = ps_w.tile([P, D], F32, name="wkb")
+        wkb = ps_k.tile([P, D], F32, tag="k", name="wkb")
 
         def gains():
             nc.tensor.matmul(out=wqb[:], lhsT=ones_bf[:], rhs=wrow[:, 0:D], start=True, stop=True)
             nc.tensor.matmul(out=wkb[:], lhsT=ones_bf[:], rhs=wrow[:, D:2 * D], start=True, stop=True)
             nc.scalar.copy(out=wq_sb[:], in_=wqb[:])
+            nc.scalar.copy(out=wk_sb[:], in_=wkb[:])
 
         def turn(src, dst, on_vector):
             tp = ps_t.tile([P, 2, 2, P], F32, tag="tp", name="tp")
@@ -152,11 +158,10 @@ def tile_attention_pa_kernel(tc, x, wq, wkv, q_norm_w, k_norm_w, out_0, out_1, o
                                   in_=gw[:, 4 * D * grp:4 * D * (grp + 1)])
 
         def build_t(eng, wsrc, a):
-            wv = wsrc[:].rearrange("p (i r) -> p r i", r=2)
-            for r in range(2):
-                eng.tensor_tensor(out=tq[:, a, r, :].rearrange("p (i e) -> p i e", e=2),
-                                  in0=wv[:, r, :].unsqueeze(2).to_broadcast([P, PAIRS, 2]),
-                                  in1=planes[:, a, r:r + 2, :].rearrange("p e i -> p i e"),
+            for e in range(2):
+                eng.tensor_tensor(out=tq[:, a, e, :].rearrange("p (i r) -> p i r", r=2),
+                                  in0=wsrc[:].rearrange("p (i r) -> p i r", r=2),
+                                  in1=planes[:, a, e:e + 2, :].rearrange("p r i -> p i r"),
                                   op=ALU.mult)
 
         def mx(ps, a, grp):
@@ -187,16 +192,16 @@ def tile_attention_pa_kernel(tc, x, wq, wkv, q_norm_w, k_norm_w, out_0, out_1, o
             nc.gpsimd.tensor_tensor(out=rstd[:, a, 0:5], in0=mse[:, a, 0:5], in1=nh[:, 0:5], op=ALU.pow)
 
         def combine(dst, mm):
-            mv = mm[:].rearrange("p r (i e) -> p e i r", e=2)
-            nc.gpsimd.tensor_tensor(out=dst[:].rearrange("p (i r) -> p i r", r=2),
-                                    in0=mv[:, 0], in1=mv[:, 1], op=ALU.subtract)
+            nc.gpsimd.tensor_tensor(out=dst[:], in0=mm[:, 0, :], in1=mm[:, 1, :], op=ALU.subtract)
 
         def rope_q(a, h):
             ps = ps_v.tile([P, D], F32, tag="v", name="ps")
             mx(ps, a, h)
             mm = mmp.tile([P, 2, D], F32, tag="mm", name="mm")
-            nc.vector.scalar_tensor_tensor(out=mm[:], in0=ps[:].unsqueeze(1).to_broadcast([P, 2, D]),
-                                           scalar=rstd[:, a, h:h + 1], in1=tq[:, a, :, :],
+            nc.vector.scalar_tensor_tensor(out=mm[:].rearrange("p e (i r) -> p (e i) r", r=2),
+                                           in0=ps[:].unsqueeze(2).to_broadcast([P, D, 2]),
+                                           scalar=rstd[:, a, h:h + 1],
+                                           in1=tq[:, a, :, :].rearrange("p e (i r) -> p (e i) r", r=2),
                                            op0=ALU.mult, op1=ALU.mult)
             o = outp.tile([P, D], F32, tag="o", name="o")
             combine(o, mm)
@@ -206,15 +211,19 @@ def tile_attention_pa_kernel(tc, x, wq, wkv, q_norm_w, k_norm_w, out_0, out_1, o
             ps = ps_v.tile([P, D], F32, tag="v", name="ps")
             mx(ps, a, 4)
             mm = mmp.tile([P, 2, D], F32, tag="mm", name="mm")
-            pv = ps[:].rearrange("p (i e) -> p i e", e=2)
-            for r in range(2):
-                nc.vector.tensor_tensor(out=mm[:, r, :].rearrange("p (i e) -> p i e", e=2), in0=pv,
-                                        in1=planes[:, a, r:r + 2, :].rearrange("p e i -> p i e"),
+            for e in range(2):
+                nc.vector.tensor_tensor(out=mm[:, e, :].rearrange("p (i r) -> p i r", r=2),
+                                        in0=ps[:, PAIRS * e:PAIRS * (e + 1)].unsqueeze(2).to_broadcast([P, PAIRS, 2]),
+                                        in1=planes[:, a, e:e + 2, :].rearrange("p r i -> p i r"),
                                         op=ALU.mult)
-            rk = rkp.tile([P, D], F32, tag="rk", name="rk")
-            combine(rk, mm)
+            rk = ps_k.tile([P, D], F32, tag="k", name="rk")
+            nc.tensor.matmul(out=rk[:], lhsT=ident[:], rhs=mm[:, 0, :], start=True, stop=False)
+            nc.tensor.matmul(out=rk[:], lhsT=nident[:], rhs=mm[:, 1, :], start=False, stop=True)
+            return rk
+
+        def finish_k(a, rk):
             o = outp.tile([P, D], F32, tag="o", name="o")
-            nc.vector.scalar_tensor_tensor(out=o[:], in0=rk[:], scalar=rstd[:, a, 4:5], in1=wkb[:],
+            nc.vector.scalar_tensor_tensor(out=o[:], in0=rk[:], scalar=rstd[:, a, 4:5], in1=wk_sb[:],
                                            op0=ALU.mult, op1=ALU.mult)
             nc.sync.dma_start(out=out_1[0, P * a:P * (a + 1), :], in_=o[:])
 
@@ -247,11 +256,14 @@ def tile_attention_pa_kernel(tc, x, wq, wkv, q_norm_w, k_norm_w, out_0, out_1, o
             prep_x(c, False)
 
         for a in range(NT):
+            rk = None
             for j in range(6):
-                if j < 4:
-                    rope_q(a, j)
-                elif j == 4:
-                    rope_k(a)
+                if j == 0:
+                    rk = rope_k(a)
+                elif j < 5:
+                    rope_q(a, j - 1)
+                if j == 2:
+                    finish_k(a, rk)
                 if a + 1 < NT:
                     if j < 5:
                         square(a + 1, j)

@@ -24,6 +24,7 @@ EPS = 1.1920929e-07
 TWO_PI = 2.0 * math.pi
 STEP = 10000.0 ** (-1.0 / PAIRS)
 G_TILES = ()
+PE_HEADS = ()
 
 
 def tile_attention_pa_kernel(tc, x, wq, wkv, q_norm_w, k_norm_w, out_0, out_1, out_2):
@@ -35,11 +36,13 @@ def tile_attention_pa_kernel(tc, x, wq, wkv, q_norm_w, k_norm_w, out_0, out_1, o
         vop = ctx.enter_context(tc.tile_pool(name="vop", bufs=2))
         jp = ctx.enter_context(tc.tile_pool(name="jp", bufs=2))
         ps_t = ctx.enter_context(tc.psum_pool(name="ps_t", bufs=2))
+        ps_w = ctx.enter_context(tc.psum_pool(name="ps_w", bufs=1))
+        ktp = ctx.enter_context(tc.tile_pool(name="ktp", bufs=2))
         ps_s = ctx.enter_context(tc.psum_pool(name="ps_s", bufs=2))
         ps_v = ctx.enter_context(tc.psum_pool(name="ps_v", bufs=3))
-        ps_k = ctx.enter_context(tc.psum_pool(name="ps_k", bufs=1))
 
         ident = const.tile([P, P], F32, name="ident")
+        wk_col = const.tile([P, 4], F32, name="wk_col")
         nident = const.tile([P, P], F32, name="nident")
         wk_sb = const.tile([P, D], F32, name="wk_sb")
         ones_bf = const.tile([P, P], BF16, name="ones_bf")
@@ -63,9 +66,9 @@ def tile_attention_pa_kernel(tc, x, wq, wkv, q_norm_w, k_norm_w, out_0, out_1, o
         planes = const.tile([P, NT, 3, PAIRS], F32, name="planes")
         tq = const.tile([P, NT, 2, D], F32, name="tq")
         wq_sb = const.tile([P, D], F32, name="wq_sb")
-        ms = const.tile([P, NT, 8], F32, name="ms")
-        mse = const.tile([P, NT, 8], F32, name="mse")
-        rstd = const.tile([P, NT, 8], F32, name="rstd")
+        ms = const.tile([P, NT + 1, 8], F32, name="ms")
+        mse = const.tile([P, NT + 1, 8], F32, name="mse")
+        rstd = const.tile([P, NT + 1, 8], F32, name="rstd")
         nh = const.tile([P, 8], F32, name="nh")
 
         nc.vector.memset(one[:], 1.0)
@@ -119,14 +122,18 @@ def tile_attention_pa_kernel(tc, x, wq, wkv, q_norm_w, k_norm_w, out_0, out_1, o
             nc.scalar.activation(out=planes[:, a0:a1, 2, :], in_=afrac[:, a0:a1, :], func=ACT.Sin,
                                  scale=TWO_PI, bias=-math.pi / 2)
 
-        wqb = ps_v.tile([P, D], F32, tag="v", name="wqb")
-        wkb = ps_k.tile([P, D], F32, tag="k", name="wkb")
+        wqb = ps_w.tile([P, D], F32, tag="w", name="wqb")
+        wkb = ps_s.tile([P, D], F32, tag="s", name="wkb")
 
         def gains():
             nc.tensor.matmul(out=wqb[:], lhsT=ones_bf[:], rhs=wrow[:, 0:D], start=True, stop=True)
             nc.tensor.matmul(out=wkb[:], lhsT=ones_bf[:], rhs=wrow[:, D:2 * D], start=True, stop=True)
             nc.scalar.copy(out=wq_sb[:], in_=wqb[:])
             nc.scalar.copy(out=wk_sb[:], in_=wkb[:])
+            wkt = ps_t.tile([P, 4, P], F32, tag="tp", name="wkt")
+            for b in range(4):
+                nc.tensor.transpose(wkt[:, b, :], wk_sb[:, P * b:P * (b + 1)], ident[:])
+            nc.scalar.copy(out=wk_col[:], in_=wkt[:, :, 0])
 
         def turn(src, dst, on_vector):
             tp = ps_t.tile([P, 2, 2, P], F32, tag="tp", name="tp")
@@ -177,7 +184,7 @@ def tile_attention_pa_kernel(tc, x, wq, wkv, q_norm_w, k_norm_w, out_0, out_1, o
             mx(ps, a, grp)
             junk = jp.tile([P, D], BF16, tag="junk", name="junk")
             nc.scalar.activation(out=junk[:], in_=ps[:], func=ACT.Square, scale=1.0 / math.sqrt(D),
-                                 accum_out=ms[:, a, grp:grp + 1])
+                                 accum_out=ms[:, a + grp // 4, grp:grp + 1])
 
         def value(a):
             ps = ps_s.tile([P, D], F32, tag="s", name="ps")
@@ -190,6 +197,10 @@ def tile_attention_pa_kernel(tc, x, wq, wkv, q_norm_w, k_norm_w, out_0, out_1, o
             nc.gpsimd.tensor_scalar(out=mse[:, a, 0:5], in0=ms[:, a, 0:5], scalar1=1.0, scalar2=EPS,
                                     op0=ALU.mult, op1=ALU.add)
             nc.gpsimd.tensor_tensor(out=rstd[:, a, 0:5], in0=mse[:, a, 0:5], in1=nh[:, 0:5], op=ALU.pow)
+
+        def norms1(a, g):
+            nc.scalar.activation(out=mse[:, a, g:g + 1], in_=ms[:, a, g:g + 1], func=ACT.Copy, bias=EPS)
+            nc.gpsimd.tensor_tensor(out=rstd[:, a, g:g + 1], in0=mse[:, a, g:g + 1], in1=nh[:, g:g + 1], op=ALU.pow)
 
         def combine(dst, mm):
             nc.gpsimd.tensor_tensor(out=dst[:], in0=mm[:, 0, :], in1=mm[:, 1, :], op=ALU.subtract)
@@ -204,7 +215,13 @@ def tile_attention_pa_kernel(tc, x, wq, wkv, q_norm_w, k_norm_w, out_0, out_1, o
                                            in1=tq[:, a, :, :].rearrange("p e (i r) -> p (e i) r", r=2),
                                            op0=ALU.mult, op1=ALU.mult)
             o = outp.tile([P, D], F32, tag="o", name="o")
-            combine(o, mm)
+            if h in PE_HEADS:
+                qc = ps_t.tile([P, D], F32, tag="tp", name="qc")
+                nc.tensor.matmul(out=qc[:], lhsT=ident[:], rhs=mm[:, 0, :], start=True, stop=False)
+                nc.tensor.matmul(out=qc[:], lhsT=nident[:], rhs=mm[:, 1, :], start=False, stop=True)
+                nc.scalar.copy(out=o[:], in_=qc[:])
+            else:
+                combine(o, mm)
             nc.sync.dma_start(out=out_0[0, h, P * a:P * (a + 1), :], in_=o[:])
 
         def rope_k(a):
@@ -212,61 +229,85 @@ def tile_attention_pa_kernel(tc, x, wq, wkv, q_norm_w, k_norm_w, out_0, out_1, o
             mx(ps, a, 4)
             mm = mmp.tile([P, 2, D], F32, tag="mm", name="mm")
             for e in range(2):
-                nc.vector.tensor_tensor(out=mm[:, e, :].rearrange("p (i r) -> p i r", r=2),
-                                        in0=ps[:, PAIRS * e:PAIRS * (e + 1)].unsqueeze(2).to_broadcast([P, PAIRS, 2]),
-                                        in1=planes[:, a, e:e + 2, :].rearrange("p r i -> p i r"),
-                                        op=ALU.mult)
-            rk = ps_k.tile([P, D], F32, tag="k", name="rk")
-            nc.tensor.matmul(out=rk[:], lhsT=ident[:], rhs=mm[:, 0, :], start=True, stop=False)
-            nc.tensor.matmul(out=rk[:], lhsT=nident[:], rhs=mm[:, 1, :], start=False, stop=True)
-            return rk
+                nc.vector.scalar_tensor_tensor(out=mm[:, e, :].rearrange("p (i r) -> p i r", r=2),
+                                               in0=ps[:, PAIRS * e:PAIRS * (e + 1)].unsqueeze(2).to_broadcast([P, PAIRS, 2]),
+                                               scalar=1.0 - 2.0 * e,
+                                               in1=planes[:, a, e:e + 2, :].rearrange("p r i -> p i r"),
+                                               op0=ALU.mult, op1=ALU.mult)
+            kt = ps_t.tile([P, 4, P], F32, tag="tp", name="kt")
+            for b in range(4):
+                nc.tensor.matmul(out=kt[:, b, :], lhsT=mm[:, 0, P * b:P * (b + 1)], rhs=ident[:],
+                                 is_transpose=True, start=True, stop=False)
+                nc.tensor.matmul(out=kt[:, b, :], lhsT=mm[:, 1, P * b:P * (b + 1)], rhs=ident[:],
+                                 is_transpose=True, start=False, stop=True)
+            kts = ktp.tile([P, 4, P], F32, tag="kts", name="kts")
+            for b in range(4):
+                nc.scalar.activation(out=kts[:, b, :], in_=kt[:, b, :], func=ACT.Copy, scale=wk_col[:, b:b + 1])
+            return kts
 
-        def finish_k(a, rk):
+        def finish_k(a, kts):
+            ko = ps_t.tile([P, 4, P], F32, tag="tp", name="ko")
+            for b in range(4):
+                nc.tensor.transpose(ko[:, b, :], kts[:, b, :], ident[:])
             o = outp.tile([P, D], F32, tag="o", name="o")
-            nc.vector.scalar_tensor_tensor(out=o[:], in0=rk[:], scalar=rstd[:, a, 4:5], in1=wk_sb[:],
-                                           op0=ALU.mult, op1=ALU.mult)
+            nc.scalar.activation(out=o[:], in_=ko[:].rearrange("p b d -> p (b d)"), func=ACT.Copy,
+                                 scale=rstd[:, a + 1, 4:5])
             nc.sync.dma_start(out=out_1[0, P * a:P * (a + 1), :], in_=o[:])
+
+        G_TABLES = (1,)
+
+        def table(a):
+            if a in G_TABLES:
+                build_t(nc.gpsimd, wq_sb, a)
+            else:
+                build_t(nc.vector, wqb, a)
+
+        def norms_slot(a, g0, g1):
+            nc.scalar.activation(out=mse[:, a, g0:g1], in_=ms[:, a, g0:g1], func=ACT.Copy, bias=EPS)
+            nc.gpsimd.tensor_tensor(out=rstd[:, a, g0:g1], in0=mse[:, a, g0:g1], in1=nh[:, g0:g1], op=ALU.pow)
+
+        def k_tile(a):
+            finish_k(a, rope_k(a))
+            value(a)
 
         trig(0, 2)
         gains()
         prep_x(0, True)
-        prep_w(0, True)
-        trig(2, 4)
-        build_t(nc.gpsimd, wq_sb, 0)
-        square(0, 0)
-        prep_w(1, False)
-        square(0, 1)
-        build_t(nc.gpsimd, wq_sb, 1)
-        prep_w(2, False)
-        square(0, 2)
-        trig(4, 8)
-        prep_w(3, False)
-        square(0, 3)
+        for g in range(4):
+            prep_w(g, g < 1)
+            if g == 0:
+                table(0)
+                table(1)
+            square(0, g)
+            norms_slot(0, g, g + 1)
+            rope_q(0, g)
+            square(1, g)
+            if g == 1:
+                trig(2, 4)
         prep_w(4, False)
         square(0, 4)
-        norms(0)
-        prep_w(5, False)
-        value(0)
-        for a in range(2, NT):
-            if a in G_TILES:
-                build_t(nc.gpsimd, wq_sb, a)
-            else:
-                build_t(nc.vector, wqb, a)
-        for c in range(1, 4):
-            prep_x(c, False)
-
-        for a in range(NT):
-            rk = None
-            for j in range(6):
-                if j == 0:
-                    rk = rope_k(a)
-                elif j < 5:
-                    rope_q(a, j - 1)
-                if j == 2:
-                    finish_k(a, rk)
-                if a + 1 < NT:
-                    if j < 5:
-                        square(a + 1, j)
-                    else:
-                        value(a + 1)
-                        norms(a + 1)
+        norms_slot(1, 0, 5)
+        for a in range(1, NT):
+            if a == 1:
+                prep_x(1, False)
+                table(2)
+                prep_w(5, False)
+            if a == 2:
+                trig(4, 8)
+                prep_x(2, False)
+                prep_x(3, False)
+            last = a + 1 == NT
+            for g in range(4):
+                if not last:
+                    square(a + 1, g)
+                if g == (0 if last else 3):
+                    square(a, 4)
+                    norms_slot(a + 1, 4 if last else 0, 5)
+                if last and g == 2:
+                    k_tile(a - 1)
+                    k_tile(a)
+                rope_q(a, g)
+            if a + 2 < NT:
+                table(a + 2)
+            if not last:
+                k_tile(a - 1)

@@ -75,25 +75,27 @@ def tile_attention_pa_kernel(tc, x, wq, wkv, q_norm_w, k_norm_w, out_0, out_1, o
         nc.vector.memset(wrow[:], 0.0)
         nc.vector.memset(ones_bf[:], 1.0)
         nc.scalar.activation(out=warm[:], in_=one[:], func=ACT.Sin)
-        nc.gpsimd.iota(tcol[:], pattern=[[P, NT]], base=0, channel_multiplier=1,
+        nc.gpsimd.iota(tcol[:], pattern=[[1, NT]], base=0, channel_multiplier=NT,
                        allow_small_or_imprecise_dtypes=True)
         make_identity(nc, ident[:])
         nc.gpsimd.memset(nh[:], -0.5)
         nc.gpsimd.tensor_scalar(out=nident[:], in0=ident[:], scalar1=-1.0, scalar2=0.0, op0=ALU.mult, op1=ALU.add)
 
-        xv = x.flatten_outer_dims().rearrange("(a p) k -> p a k", p=P)
-        wqv = wq.rearrange("(h b p e) k -> h e p b k", h=4, p=P, e=2)
-        wkv2 = wkv.rearrange("(h b p e) k -> h e p b k", h=2, p=P, e=2)
-        wvv = wkv.rearrange("(j p) k -> p j k", p=P)
+        xv = x.flatten_outer_dims().rearrange("(p a) k -> p a k", a=NT)
+        q_rows = out_0.rearrange("o h (p a) d -> (o h) a p d", a=NT)
+        k_rows = out_1.rearrange("o (p a) d -> (o a) p d", a=NT)
+        v_rows = out_2.rearrange("o (p a) d -> (o a) p d", a=NT)
+        wqv = wq.rearrange("(h b p e) k -> h p b (e k)", h=4, p=P, e=2)
+        wkv2 = wkv.rearrange("(h b p e) k -> h p b (e k)", h=2, p=P, e=2)
+        wvv = wkv.rearrange("(h p j) k -> h p (j k)", h=2, p=P)
+        w_in = w_sb[:].rearrange("p (g b e) k -> p g b (e k)", b=2, e=2)
         nc.sync.dma_start(out=x_sb[:, 0:2, :], in_=xv[:, 0:2, :])
         nc.sync.dma_start(out=wrow[0:1, 0:D], in_=q_norm_w.rearrange("(o d) -> o d", o=1))
         nc.sync.dma_start(out=wrow[0:1, D:2 * D], in_=k_norm_w.rearrange("(o d) -> o d", o=1))
         for h in range(4):
-            for e in range(2):
-                nc.sync.dma_start(out=w_sb[:, 4 * h + 2 * e:4 * h + 2 * e + 2, :], in_=wqv[h, e])
-        for e in range(2):
-            nc.sync.dma_start(out=w_sb[:, 16 + 2 * e:18 + 2 * e, :], in_=wkv2[0, e])
-        nc.sync.dma_start(out=w_sb[:, 20:24, :], in_=wvv[:, 4:8, :])
+            nc.sync.dma_start(out=w_in[:, h], in_=wqv[h])
+        nc.sync.dma_start(out=w_in[:, 4], in_=wkv2[0])
+        nc.sync.dma_start(out=w_sb[:, 20:24, :].rearrange("p j k -> p (j k)"), in_=wvv[1])
         for c in range(1, 4):
             nc.sync.dma_start(out=x_sb[:, 2 * c:2 * c + 2, :], in_=xv[:, 2 * c:2 * c + 2, :])
 
@@ -150,19 +152,24 @@ def tile_attention_pa_kernel(tc, x, wq, wkv, q_norm_w, k_norm_w, out_0, out_1, o
         gxw = gx[:].bitcast(F32).rearrange("p (c r u) -> p c r u", r=P, u=2)
         gww = gw[:].bitcast(F32).rearrange("p (c r u) -> p c r u", r=P, u=2)
 
-        def prep_x(c, on_vector):
-            turn(x_sb[:, 2 * c:2 * c + 2, :], gxw[:, 2 * c:2 * c + 2, :, :], on_vector)
-            nc.vector.quantize_mx(out=x_codes[:, 256 * c:256 * (c + 1)].bitcast(E5X4),
-                                  scales=x_scales[:, 256 * c:256 * (c + 1)],
-                                  in_=gx[:, 1024 * c:1024 * (c + 1)])
+        def prep_x(c0, c1, on_vector):
+            for c in range(c0, c1):
+                turn(x_sb[:, 2 * c:2 * c + 2, :], gxw[:, 2 * c:2 * c + 2, :, :], on_vector)
+            nc.vector.quantize_mx(out=x_codes[:, 256 * c0:256 * c1].bitcast(E5X4),
+                                  scales=x_scales[:, 256 * c0:256 * c1],
+                                  in_=gx[:, 1024 * c0:1024 * c1])
 
-        def prep_w(grp, on_vector):
-            for b in range(2):
-                j = 4 * grp + 2 * b
-                turn(w_sb[:, j:j + 2, :], gww[:, j:j + 2, :, :], on_vector)
-            nc.vector.quantize_mx(out=w_codes[:, D * grp:D * (grp + 1)].bitcast(E5X4),
-                                  scales=w_scales[:, D * grp:D * (grp + 1)],
-                                  in_=gw[:, 4 * D * grp:4 * D * (grp + 1)])
+        def prep_w(g0, g1, on_vector):
+            for grp in range(g0, g1):
+                for e in range(2):
+                    j = 4 * grp
+                    if grp == 5:
+                        turn(w_sb[:, j + 2 * e:j + 2 * e + 2, :], gww[:, j + 2 * e:j + 2 * e + 2, :, :], on_vector)
+                    else:
+                        turn(w_sb[:, j + e:j + 4:2, :], gww[:, j + 2 * e:j + 2 * e + 2, :, :], on_vector)
+            nc.vector.quantize_mx(out=w_codes[:, D * g0:D * g1].bitcast(E5X4),
+                                  scales=w_scales[:, D * g0:D * g1],
+                                  in_=gw[:, 4 * D * g0:4 * D * g1])
 
         def build_t(eng, wsrc, a):
             for e in range(2):
@@ -190,8 +197,8 @@ def tile_attention_pa_kernel(tc, x, wq, wkv, q_norm_w, k_norm_w, out_0, out_1, o
             ps = ps_s.tile([P, D], F32, tag="s", name="ps")
             mx(ps, a, 5)
             vo = vop.tile([P, D], F32, tag="vo", name="vo")
-            nc.scalar.copy(out=vo[:], in_=ps[:])
-            nc.sync.dma_start(out=out_2[0, P * a:P * (a + 1), :], in_=vo[:])
+            nc.scalar.copy(out=vo[:].rearrange("p (q j) -> p q j", j=4), in_=ps[:].rearrange("p (j q) -> p q j", j=4))
+            nc.sync.dma_start(out=v_rows[a], in_=vo[:])
 
         def norms(a):
             nc.gpsimd.tensor_scalar(out=mse[:, a, 0:5], in0=ms[:, a, 0:5], scalar1=1.0, scalar2=EPS,
@@ -222,7 +229,7 @@ def tile_attention_pa_kernel(tc, x, wq, wkv, q_norm_w, k_norm_w, out_0, out_1, o
                 nc.scalar.copy(out=o[:], in_=qc[:])
             else:
                 combine(o, mm)
-            nc.sync.dma_start(out=out_0[0, h, P * a:P * (a + 1), :], in_=o[:])
+            nc.sync.dma_start(out=q_rows[h, a], in_=o[:])
 
         def rope_k(a):
             ps = ps_v.tile([P, D], F32, tag="v", name="ps")
@@ -252,9 +259,9 @@ def tile_attention_pa_kernel(tc, x, wq, wkv, q_norm_w, k_norm_w, out_0, out_1, o
             o = outp.tile([P, D], F32, tag="o", name="o")
             nc.scalar.activation(out=o[:], in_=ko[:].rearrange("p b d -> p (b d)"), func=ACT.Copy,
                                  scale=rstd[:, a + 1, 4:5])
-            nc.sync.dma_start(out=out_1[0, P * a:P * (a + 1), :], in_=o[:])
+            nc.sync.dma_start(out=k_rows[a], in_=o[:])
 
-        G_TABLES = (1,)
+        G_TABLES = ()
 
         def table(a):
             if a in G_TABLES:
@@ -272,9 +279,9 @@ def tile_attention_pa_kernel(tc, x, wq, wkv, q_norm_w, k_norm_w, out_0, out_1, o
 
         trig(0, 2)
         gains()
-        prep_x(0, True)
+        prep_x(0, 1, True)
         for g in range(4):
-            prep_w(g, g < 1)
+            prep_w(g, g + 1, g < 1)
             if g == 0:
                 table(0)
                 table(1)
@@ -284,18 +291,16 @@ def tile_attention_pa_kernel(tc, x, wq, wkv, q_norm_w, k_norm_w, out_0, out_1, o
             square(1, g)
             if g == 1:
                 trig(2, 4)
-        prep_w(4, False)
+        prep_w(4, 6, False)
         square(0, 4)
         norms_slot(1, 0, 5)
         for a in range(1, NT):
             if a == 1:
-                prep_x(1, False)
+                prep_x(1, 2, False)
                 table(2)
-                prep_w(5, False)
             if a == 2:
                 trig(4, 8)
-                prep_x(2, False)
-                prep_x(3, False)
+                prep_x(2, 4, False)
             last = a + 1 == NT
             for g in range(4):
                 if not last:

@@ -11,308 +11,284 @@ BF16 = mybir.dt.bfloat16
 I32 = mybir.dt.int32
 U32 = mybir.dt.uint32
 U8 = mybir.dt.uint8
-E5X4 = mybir.dt.float8_e5m2_x4
+E5M2_X4 = mybir.dt.float8_e5m2_x4
 ALU = mybir.AluOpType
 ACT = mybir.ActivationFunctionType
 
 P = 128
-T = 1024
+TOKENS = 1024
 D = 512
-NT = T // P
+TILES = TOKENS // P
 PAIRS = D // 2
+HEADS = 4
+KEY = 4
+VALUE = 5
+GROUPS = 6
 EPS = 1.1920929e-07
 TWO_PI = 2.0 * math.pi
 STEP = 10000.0 ** (-1.0 / PAIRS)
-G_TILES = ()
-PE_HEADS = ()
 
 
 def tile_attention_pa_kernel(tc, x, wq, wkv, q_norm_w, k_norm_w, out_0, out_1, out_2):
     nc = tc.nc
     with ExitStack() as ctx:
-        const = ctx.enter_context(tc.tile_pool(name="const", bufs=1))
-        mmp = ctx.enter_context(tc.tile_pool(name="mmp", bufs=4))
-        outp = ctx.enter_context(tc.tile_pool(name="outp", bufs=6))
-        vop = ctx.enter_context(tc.tile_pool(name="vop", bufs=2))
-        jp = ctx.enter_context(tc.tile_pool(name="jp", bufs=2))
-        ps_t = ctx.enter_context(tc.psum_pool(name="ps_t", bufs=2))
-        ps_w = ctx.enter_context(tc.psum_pool(name="ps_w", bufs=1))
-        ktp = ctx.enter_context(tc.tile_pool(name="ktp", bufs=2))
-        ps_s = ctx.enter_context(tc.psum_pool(name="ps_s", bufs=2))
-        ps_v = ctx.enter_context(tc.psum_pool(name="ps_v", bufs=3))
+        keep = ctx.enter_context(tc.tile_pool(name="keep", bufs=1))
+        products = ctx.enter_context(tc.tile_pool(name="products", bufs=4))
+        results = ctx.enter_context(tc.tile_pool(name="results", bufs=6))
+        values = ctx.enter_context(tc.tile_pool(name="values", bufs=2))
+        squares = ctx.enter_context(tc.tile_pool(name="squares", bufs=2))
+        turned_k = ctx.enter_context(tc.tile_pool(name="turned_k", bufs=2))
+        ps_turn = ctx.enter_context(tc.psum_pool(name="ps_turn", bufs=2))
+        ps_gain = ctx.enter_context(tc.psum_pool(name="ps_gain", bufs=1))
+        ps_scalar = ctx.enter_context(tc.psum_pool(name="ps_scalar", bufs=2))
+        ps_vector = ctx.enter_context(tc.psum_pool(name="ps_vector", bufs=3))
 
-        ident = const.tile([P, P], F32, name="ident")
-        wk_col = const.tile([P, 4], F32, name="wk_col")
-        nident = const.tile([P, P], F32, name="nident")
-        wk_sb = const.tile([P, D], F32, name="wk_sb")
-        ones_bf = const.tile([P, P], BF16, name="ones_bf")
-        wrow = const.tile([P, 2 * D], BF16, name="wrow")
-        x_sb = const.tile([P, NT, D], BF16, name="x_sb")
-        w_sb = const.tile([P, 24, D], BF16, name="w_sb")
-        gx = const.tile([P, 4 * T], BF16, name="gx", align_bytes=64)
-        gw = const.tile([P, 4 * 3072], BF16, name="gw", align_bytes=64)
-        x_codes = const.tile([P, T], U32, name="x_codes", align_bytes=64)
-        x_scales = const.tile([P, T], U8, name="x_scales", align_bytes=64)
-        w_codes = const.tile([P, 3072], U32, name="w_codes", align_bytes=64)
-        w_scales = const.tile([P, 3072], U8, name="w_scales", align_bytes=64)
-        one = const.tile([P, 1], F32, name="one")
-        warm = const.tile([P, 1], F32, name="warm")
-        turns = const.tile([P, PAIRS], F32, name="turns")
-        tcol = const.tile([P, NT], F32, name="tcol")
-        phi = const.tile([P, NT, PAIRS], F32, name="phi")
-        kint = const.tile([P, NT, PAIRS], I32, name="kint")
-        frac = const.tile([P, NT, PAIRS], F32, name="frac")
-        afrac = const.tile([P, NT, PAIRS], F32, name="afrac")
-        planes = const.tile([P, NT, 3, PAIRS], F32, name="planes")
-        tq = const.tile([P, NT, 2, D], F32, name="tq")
-        wq_sb = const.tile([P, D], F32, name="wq_sb")
-        ms = const.tile([P, NT + 1, 8], F32, name="ms")
-        mse = const.tile([P, NT + 1, 8], F32, name="mse")
-        rstd = const.tile([P, NT + 1, 8], F32, name="rstd")
-        nh = const.tile([P, 8], F32, name="nh")
+        ident = keep.tile([P, P], F32, name="ident")
+        ones = keep.tile([P, P], BF16, name="ones")
+        gain_rows = keep.tile([P, 2 * D], BF16, name="gain_rows")
+        k_gain = keep.tile([P, D], F32, name="k_gain")
+        k_gain_col = keep.tile([P, D // P], F32, name="k_gain_col")
+        x_rows = keep.tile([P, TILES, D], BF16, name="x_rows")
+        w_rows = keep.tile([P, 4 * GROUPS, D], BF16, name="w_rows")
+        x_grouped = keep.tile([P, 4 * TOKENS], BF16, name="x_grouped", align_bytes=64)
+        w_grouped = keep.tile([P, 4 * GROUPS * D], BF16, name="w_grouped", align_bytes=64)
+        x_codes = keep.tile([P, TOKENS], U32, name="x_codes", align_bytes=64)
+        x_scales = keep.tile([P, TOKENS], U8, name="x_scales", align_bytes=64)
+        w_codes = keep.tile([P, GROUPS * D], U32, name="w_codes", align_bytes=64)
+        w_scales = keep.tile([P, GROUPS * D], U8, name="w_scales", align_bytes=64)
+        one = keep.tile([P, 1], F32, name="one")
+        warm = keep.tile([P, 1], F32, name="warm")
+        turns = keep.tile([P, PAIRS], F32, name="turns")
+        token = keep.tile([P, TILES], F32, name="token")
+        angle = keep.tile([P, TILES, PAIRS], F32, name="angle")
+        whole = keep.tile([P, TILES, PAIRS], I32, name="whole")
+        frac = keep.tile([P, TILES, PAIRS], F32, name="frac")
+        abs_frac = keep.tile([P, TILES, PAIRS], F32, name="abs_frac")
+        trig = keep.tile([P, TILES, 3, PAIRS], F32, name="trig")
+        q_table = keep.tile([P, TILES, 2, D], F32, name="q_table")
+        mean_sq = keep.tile([P, TILES + 1, 8], F32, name="mean_sq")
+        mean_eps = keep.tile([P, TILES + 1, 8], F32, name="mean_eps")
+        rstd = keep.tile([P, TILES + 1, 8], F32, name="rstd")
+        minus_half = keep.tile([P, 8], F32, name="minus_half")
 
         nc.vector.memset(one[:], 1.0)
-        nc.vector.memset(wrow[:], 0.0)
-        nc.vector.memset(ones_bf[:], 1.0)
+        nc.vector.memset(gain_rows[:], 0.0)
+        nc.vector.memset(ones[:], 1.0)
         nc.scalar.activation(out=warm[:], in_=one[:], func=ACT.Sin)
-        nc.gpsimd.iota(tcol[:], pattern=[[1, NT]], base=0, channel_multiplier=NT,
+        nc.gpsimd.iota(token[:], pattern=[[1, TILES]], base=0, channel_multiplier=TILES,
                        allow_small_or_imprecise_dtypes=True)
         make_identity(nc, ident[:])
-        nc.gpsimd.memset(nh[:], -0.5)
-        nc.gpsimd.tensor_scalar(out=nident[:], in0=ident[:], scalar1=-1.0, scalar2=0.0, op0=ALU.mult, op1=ALU.add)
+        nc.gpsimd.memset(minus_half[:], -0.5)
 
-        xv = x.flatten_outer_dims().rearrange("(p a) k -> p a k", a=NT)
-        q_rows = out_0.rearrange("o h (p a) d -> (o h) a p d", a=NT)
-        k_rows = out_1.rearrange("o (p a) d -> (o a) p d", a=NT)
-        v_rows = out_2.rearrange("o (p a) d -> (o a) p d", a=NT)
-        wqv = wq.rearrange("(h b p e) k -> h p b (e k)", h=4, p=P, e=2)
-        wkv2 = wkv.rearrange("(h b p e) k -> h p b (e k)", h=2, p=P, e=2)
-        wvv = wkv.rearrange("(h p j) k -> h p (j k)", h=2, p=P)
-        w_in = w_sb[:].rearrange("p (g b e) k -> p g b (e k)", b=2, e=2)
-        nc.sync.dma_start(out=x_sb[:, 0:2, :], in_=xv[:, 0:2, :])
-        nc.sync.dma_start(out=wrow[0:1, 0:D], in_=q_norm_w.rearrange("(o d) -> o d", o=1))
-        nc.sync.dma_start(out=wrow[0:1, D:2 * D], in_=k_norm_w.rearrange("(o d) -> o d", o=1))
-        for h in range(4):
-            nc.sync.dma_start(out=w_in[:, h], in_=wqv[h])
-        nc.sync.dma_start(out=w_in[:, 4], in_=wkv2[0])
-        nc.sync.dma_start(out=w_sb[:, 20:24, :].rearrange("p j k -> p (j k)"), in_=wvv[1])
-        for c in range(1, 4):
-            nc.sync.dma_start(out=x_sb[:, 2 * c:2 * c + 2, :], in_=xv[:, 2 * c:2 * c + 2, :])
+        x_view = x.flatten_outer_dims().rearrange("(p a) k -> p a k", a=TILES)
+        q_view = wq.rearrange("(h b p e) k -> h p b (e k)", h=HEADS, p=P, e=2)
+        k_view = wkv.rearrange("(h b p e) k -> h p b (e k)", h=2, p=P, e=2)
+        v_view = wkv.rearrange("(h p j) k -> h p (j k)", h=2, p=P)
+        w_slots = w_rows[:].rearrange("p (g b e) k -> p g b (e k)", b=2, e=2)
+        q_out = out_0.rearrange("o h (p a) d -> (o h) a p d", a=TILES)
+        k_out = out_1.rearrange("o (p a) d -> (o a) p d", a=TILES)
+        v_out = out_2.rearrange("o (p a) d -> (o a) p d", a=TILES)
+        nc.sync.dma_start(out=x_rows[:, 0:2, :], in_=x_view[:, 0:2, :])
+        nc.sync.dma_start(out=gain_rows[0:1, 0:D], in_=q_norm_w.rearrange("(o d) -> o d", o=1))
+        nc.sync.dma_start(out=gain_rows[0:1, D:2 * D], in_=k_norm_w.rearrange("(o d) -> o d", o=1))
+        for h in range(HEADS):
+            nc.sync.dma_start(out=w_slots[:, h], in_=q_view[h])
+        nc.sync.dma_start(out=w_slots[:, KEY], in_=k_view[0])
+        nc.sync.dma_start(out=w_rows[:, 4 * VALUE:4 * VALUE + 4, :].rearrange("p j k -> p (j k)"), in_=v_view[1])
+        for a in range(2, TILES, 2):
+            nc.sync.dma_start(out=x_rows[:, a:a + 2, :], in_=x_view[:, a:a + 2, :])
 
-        for j in range(4):
-            nc.vector.tensor_scalar_mul(out=turns[:, j:j + 1], in0=one[:], scalar1=STEP ** j / TWO_PI)
-        w = 4
-        while w < PAIRS:
+        for i in range(4):
+            nc.vector.tensor_scalar_mul(out=turns[:, i:i + 1], in0=one[:], scalar1=STEP ** i / TWO_PI)
+        width = 4
+        while width < PAIRS:
             for m in range(1, 4):
-                nc.vector.tensor_scalar_mul(out=turns[:, m * w:(m + 1) * w], in0=turns[:, 0:w],
-                                            scalar1=STEP ** (m * w))
-            w *= 4
-        chunks = ((0, 2), (2, 4), (4, 8))
-        for a0, a1 in chunks:
+                nc.vector.tensor_scalar_mul(out=turns[:, m * width:(m + 1) * width], in0=turns[:, 0:width],
+                                            scalar1=STEP ** (m * width))
+            width *= 4
+        for a0, a1 in ((0, 2), (2, 4), (4, TILES)):
             for a in range(a0, a1):
-                nc.vector.tensor_scalar_mul(out=phi[:, a, :], in0=turns[:], scalar1=tcol[:, a:a + 1])
-            nc.vector.tensor_copy(out=kint[:, a0:a1, :], in_=phi[:, a0:a1, :])
-            nc.vector.tensor_tensor(out=frac[:, a0:a1, :], in0=phi[:, a0:a1, :], in1=kint[:, a0:a1, :],
+                nc.vector.tensor_scalar_mul(out=angle[:, a, :], in0=turns[:], scalar1=token[:, a:a + 1])
+            nc.vector.tensor_copy(out=whole[:, a0:a1, :], in_=angle[:, a0:a1, :])
+            nc.vector.tensor_tensor(out=frac[:, a0:a1, :], in0=angle[:, a0:a1, :], in1=whole[:, a0:a1, :],
                                     op=ALU.subtract)
 
-        def trig(a0, a1):
-            nc.scalar.activation(out=afrac[:, a0:a1, :], in_=frac[:, a0:a1, :], func=ACT.Abs)
-            nc.scalar.activation(out=planes[:, a0:a1, 0, :], in_=afrac[:, a0:a1, :], func=ACT.Sin,
+        def make_trig(a0, a1):
+            nc.scalar.activation(out=abs_frac[:, a0:a1, :], in_=frac[:, a0:a1, :], func=ACT.Abs)
+            nc.scalar.activation(out=trig[:, a0:a1, 0, :], in_=abs_frac[:, a0:a1, :], func=ACT.Sin,
                                  scale=-TWO_PI, bias=math.pi / 2)
-            nc.scalar.activation(out=planes[:, a0:a1, 1, :], in_=frac[:, a0:a1, :], func=ACT.Sin,
+            nc.scalar.activation(out=trig[:, a0:a1, 1, :], in_=frac[:, a0:a1, :], func=ACT.Sin,
                                  scale=TWO_PI)
-            nc.scalar.activation(out=planes[:, a0:a1, 2, :], in_=afrac[:, a0:a1, :], func=ACT.Sin,
+            nc.scalar.activation(out=trig[:, a0:a1, 2, :], in_=abs_frac[:, a0:a1, :], func=ACT.Sin,
                                  scale=TWO_PI, bias=-math.pi / 2)
 
-        wqb = ps_w.tile([P, D], F32, tag="w", name="wqb")
-        wkb = ps_s.tile([P, D], F32, tag="s", name="wkb")
+        q_gain = ps_gain.tile([P, D], F32, name="q_gain")
 
-        def gains():
-            nc.tensor.matmul(out=wqb[:], lhsT=ones_bf[:], rhs=wrow[:, 0:D], start=True, stop=True)
-            nc.tensor.matmul(out=wkb[:], lhsT=ones_bf[:], rhs=wrow[:, D:2 * D], start=True, stop=True)
-            nc.scalar.copy(out=wq_sb[:], in_=wqb[:])
-            nc.scalar.copy(out=wk_sb[:], in_=wkb[:])
-            wkt = ps_t.tile([P, 4, P], F32, tag="tp", name="wkt")
-            for b in range(4):
-                nc.tensor.transpose(wkt[:, b, :], wk_sb[:, P * b:P * (b + 1)], ident[:])
-            nc.scalar.copy(out=wk_col[:], in_=wkt[:, :, 0])
+        def spread_q_gain():
+            nc.tensor.matmul(out=q_gain[:], lhsT=ones[:], rhs=gain_rows[:, 0:D], start=True, stop=True)
 
-        def turn(src, dst, on_vector):
-            tp = ps_t.tile([P, 2, 2, P], F32, tag="tp", name="tp")
-            for rt in range(2):
-                words = src[:, rt, :].bitcast(F32)
+        def spread_k_gain():
+            spread = ps_scalar.tile([P, D], F32, tag="bank", name="spread")
+            nc.tensor.matmul(out=spread[:], lhsT=ones[:], rhs=gain_rows[:, D:2 * D], start=True, stop=True)
+            nc.scalar.copy(out=k_gain[:], in_=spread[:])
+            turned = ps_turn.tile([P, D // P, P], F32, tag="bank", name="turned")
+            for b in range(D // P):
+                nc.tensor.transpose(turned[:, b, :], k_gain[:, P * b:P * (b + 1)], ident[:])
+            nc.scalar.copy(out=k_gain_col[:], in_=turned[:, :, 0])
+
+        def turn(rows, grouped, on_vector):
+            bank = ps_turn.tile([P, 2, 2, P], F32, tag="bank", name="bank")
+            for c in range(2):
+                words = rows[:, c, :].bitcast(F32)
                 for u in range(2):
-                    nc.tensor.transpose(tp[:, rt, u, :], words[:, u:PAIRS:2], ident[:])
-            view = tp[:].rearrange("p c u r -> p c r u")
+                    nc.tensor.transpose(bank[:, c, u, :], words[:, u:PAIRS:2], ident[:])
+            view = bank[:].rearrange("p c u r -> p c r u")
             if on_vector:
-                nc.vector.tensor_copy(out=dst, in_=view)
+                nc.vector.tensor_copy(out=grouped, in_=view)
             else:
-                nc.scalar.copy(out=dst, in_=view)
+                nc.scalar.copy(out=grouped, in_=view)
 
-        gxw = gx[:].bitcast(F32).rearrange("p (c r u) -> p c r u", r=P, u=2)
-        gww = gw[:].bitcast(F32).rearrange("p (c r u) -> p c r u", r=P, u=2)
+        x_words = x_grouped[:].bitcast(F32).rearrange("p (c r u) -> p c r u", r=P, u=2)
+        w_words = w_grouped[:].bitcast(F32).rearrange("p (c r u) -> p c r u", r=P, u=2)
 
-        def prep_x(c0, c1, on_vector):
-            for c in range(c0, c1):
-                turn(x_sb[:, 2 * c:2 * c + 2, :], gxw[:, 2 * c:2 * c + 2, :, :], on_vector)
-            nc.vector.quantize_mx(out=x_codes[:, 256 * c0:256 * c1].bitcast(E5X4),
-                                  scales=x_scales[:, 256 * c0:256 * c1],
-                                  in_=gx[:, 1024 * c0:1024 * c1])
+        def prepare_x(a0, a1, on_vector):
+            for a in range(a0, a1, 2):
+                turn(x_rows[:, a:a + 2, :], x_words[:, a:a + 2, :, :], on_vector)
+            nc.vector.quantize_mx(out=x_codes[:, P * a0:P * a1].bitcast(E5M2_X4),
+                                  scales=x_scales[:, P * a0:P * a1],
+                                  in_=x_grouped[:, 4 * P * a0:4 * P * a1])
 
-        def prep_w(g0, g1, on_vector):
-            for grp in range(g0, g1):
-                for e in range(2):
-                    j = 4 * grp
-                    if grp == 5:
-                        turn(w_sb[:, j + 2 * e:j + 2 * e + 2, :], gww[:, j + 2 * e:j + 2 * e + 2, :, :], on_vector)
+        def prepare_w(g0, g1, on_vector):
+            for g in range(g0, g1):
+                for half in range(2):
+                    first = 4 * g + 2 * half
+                    if g == VALUE:
+                        rows = w_rows[:, first:first + 2, :]
                     else:
-                        turn(w_sb[:, j + e:j + 4:2, :], gww[:, j + 2 * e:j + 2 * e + 2, :, :], on_vector)
-            nc.vector.quantize_mx(out=w_codes[:, D * g0:D * g1].bitcast(E5X4),
+                        rows = w_rows[:, 4 * g + half:4 * g + 4:2, :]
+                    turn(rows, w_words[:, first:first + 2, :, :], on_vector)
+            nc.vector.quantize_mx(out=w_codes[:, D * g0:D * g1].bitcast(E5M2_X4),
                                   scales=w_scales[:, D * g0:D * g1],
-                                  in_=gw[:, 4 * D * g0:4 * D * g1])
+                                  in_=w_grouped[:, 4 * D * g0:4 * D * g1])
 
-        def build_t(eng, wsrc, a):
-            for e in range(2):
-                eng.tensor_tensor(out=tq[:, a, e, :].rearrange("p (i r) -> p i r", r=2),
-                                  in0=wsrc[:].rearrange("p (i r) -> p i r", r=2),
-                                  in1=planes[:, a, e:e + 2, :].rearrange("p r i -> p i r"),
-                                  op=ALU.mult)
-
-        def mx(ps, a, grp):
-            nc.tensor.matmul_mx(out=ps[:],
-                                lhsT=x_codes[:, P * a:P * (a + 1)].bitcast(E5X4),
+        def project(bank, a, g):
+            nc.tensor.matmul_mx(out=bank[:],
+                                lhsT=x_codes[:, P * a:P * (a + 1)].bitcast(E5M2_X4),
                                 lhsT_scale=x_scales[:, P * a:P * (a + 1)],
-                                rhs=w_codes[:, D * grp:D * (grp + 1)].bitcast(E5X4),
-                                rhs_scale=w_scales[:, D * grp:D * (grp + 1)],
+                                rhs=w_codes[:, D * g:D * (g + 1)].bitcast(E5M2_X4),
+                                rhs_scale=w_scales[:, D * g:D * (g + 1)],
                                 start=True, stop=True)
 
-        def square(a, grp):
-            ps = ps_s.tile([P, D], F32, tag="s", name="ps")
-            mx(ps, a, grp)
-            junk = jp.tile([P, D], BF16, tag="junk", name="junk")
-            nc.scalar.activation(out=junk[:], in_=ps[:], func=ACT.Square, scale=1.0 / math.sqrt(D),
-                                 accum_out=ms[:, a + grp // 4, grp:grp + 1])
+        def mean_square(a, g):
+            bank = ps_scalar.tile([P, D], F32, tag="bank", name="bank")
+            project(bank, a, g)
+            unused = squares.tile([P, D], BF16, name="unused")
+            column_group = a + 1 if g == KEY else a
+            nc.scalar.activation(out=unused[:], in_=bank[:], func=ACT.Square, scale=1.0 / math.sqrt(D),
+                                 accum_out=mean_sq[:, column_group, g:g + 1])
 
-        def value(a):
-            ps = ps_s.tile([P, D], F32, tag="s", name="ps")
-            mx(ps, a, 5)
-            vo = vop.tile([P, D], F32, tag="vo", name="vo")
-            nc.scalar.copy(out=vo[:].rearrange("p (q j) -> p q j", j=4), in_=ps[:].rearrange("p (j q) -> p q j", j=4))
-            nc.sync.dma_start(out=v_rows[a], in_=vo[:])
+        def make_rstd(column_group, g0, g1):
+            nc.scalar.activation(out=mean_eps[:, column_group, g0:g1], in_=mean_sq[:, column_group, g0:g1],
+                                 func=ACT.Copy, bias=EPS)
+            nc.gpsimd.tensor_tensor(out=rstd[:, column_group, g0:g1], in0=mean_eps[:, column_group, g0:g1],
+                                    in1=minus_half[:, g0:g1], op=ALU.pow)
 
-        def norms(a):
-            nc.gpsimd.tensor_scalar(out=mse[:, a, 0:5], in0=ms[:, a, 0:5], scalar1=1.0, scalar2=EPS,
-                                    op0=ALU.mult, op1=ALU.add)
-            nc.gpsimd.tensor_tensor(out=rstd[:, a, 0:5], in0=mse[:, a, 0:5], in1=nh[:, 0:5], op=ALU.pow)
+        def store_v(a):
+            bank = ps_scalar.tile([P, D], F32, tag="bank", name="bank")
+            project(bank, a, VALUE)
+            v = values.tile([P, D], F32, name="v")
+            nc.scalar.copy(out=v[:].rearrange("p (q j) -> p q j", j=4), in_=bank[:].rearrange("p (j q) -> p q j", j=4))
+            nc.sync.dma_start(out=v_out[a], in_=v[:])
 
-        def norms1(a, g):
-            nc.scalar.activation(out=mse[:, a, g:g + 1], in_=ms[:, a, g:g + 1], func=ACT.Copy, bias=EPS)
-            nc.gpsimd.tensor_tensor(out=rstd[:, a, g:g + 1], in0=mse[:, a, g:g + 1], in1=nh[:, g:g + 1], op=ALU.pow)
-
-        def combine(dst, mm):
-            nc.gpsimd.tensor_tensor(out=dst[:], in0=mm[:, 0, :], in1=mm[:, 1, :], op=ALU.subtract)
+        def make_q_table(a):
+            for e in range(2):
+                nc.vector.tensor_tensor(out=q_table[:, a, e, :].rearrange("p (i r) -> p i r", r=2),
+                                        in0=q_gain[:].rearrange("p (i r) -> p i r", r=2),
+                                        in1=trig[:, a, e:e + 2, :].rearrange("p r i -> p i r"),
+                                        op=ALU.mult)
 
         def rope_q(a, h):
-            ps = ps_v.tile([P, D], F32, tag="v", name="ps")
-            mx(ps, a, h)
-            mm = mmp.tile([P, 2, D], F32, tag="mm", name="mm")
-            nc.vector.scalar_tensor_tensor(out=mm[:].rearrange("p e (i r) -> p (e i) r", r=2),
-                                           in0=ps[:].unsqueeze(2).to_broadcast([P, D, 2]),
+            bank = ps_vector.tile([P, D], F32, tag="bank", name="bank")
+            project(bank, a, h)
+            halves = products.tile([P, 2, D], F32, name="halves")
+            nc.vector.scalar_tensor_tensor(out=halves[:].rearrange("p e (i r) -> p (e i) r", r=2),
+                                           in0=bank[:].unsqueeze(2).to_broadcast([P, D, 2]),
                                            scalar=rstd[:, a, h:h + 1],
-                                           in1=tq[:, a, :, :].rearrange("p e (i r) -> p (e i) r", r=2),
+                                           in1=q_table[:, a, :, :].rearrange("p e (i r) -> p (e i) r", r=2),
                                            op0=ALU.mult, op1=ALU.mult)
-            o = outp.tile([P, D], F32, tag="o", name="o")
-            if h in PE_HEADS:
-                qc = ps_t.tile([P, D], F32, tag="tp", name="qc")
-                nc.tensor.matmul(out=qc[:], lhsT=ident[:], rhs=mm[:, 0, :], start=True, stop=False)
-                nc.tensor.matmul(out=qc[:], lhsT=nident[:], rhs=mm[:, 1, :], start=False, stop=True)
-                nc.scalar.copy(out=o[:], in_=qc[:])
-            else:
-                combine(o, mm)
-            nc.sync.dma_start(out=q_rows[h, a], in_=o[:])
+            q = results.tile([P, D], F32, tag="result", name="q")
+            engine = nc.vector if (a == TILES - 1 and h == HEADS - 1) else nc.gpsimd
+            engine.tensor_tensor(out=q[:], in0=halves[:, 0, :], in1=halves[:, 1, :], op=ALU.subtract)
+            nc.sync.dma_start(out=q_out[h, a], in_=q[:])
 
         def rope_k(a):
-            ps = ps_v.tile([P, D], F32, tag="v", name="ps")
-            mx(ps, a, 4)
-            mm = mmp.tile([P, 2, D], F32, tag="mm", name="mm")
+            bank = ps_vector.tile([P, D], F32, tag="bank", name="bank")
+            project(bank, a, KEY)
+            halves = products.tile([P, 2, D], F32, name="halves")
             for e in range(2):
-                nc.vector.scalar_tensor_tensor(out=mm[:, e, :].rearrange("p (i r) -> p i r", r=2),
-                                               in0=ps[:, PAIRS * e:PAIRS * (e + 1)].unsqueeze(2).to_broadcast([P, PAIRS, 2]),
+                nc.vector.scalar_tensor_tensor(out=halves[:, e, :].rearrange("p (i r) -> p i r", r=2),
+                                               in0=bank[:, PAIRS * e:PAIRS * (e + 1)].unsqueeze(2).to_broadcast([P, PAIRS, 2]),
                                                scalar=1.0 - 2.0 * e,
-                                               in1=planes[:, a, e:e + 2, :].rearrange("p r i -> p i r"),
+                                               in1=trig[:, a, e:e + 2, :].rearrange("p r i -> p i r"),
                                                op0=ALU.mult, op1=ALU.mult)
-            kt = ps_t.tile([P, 4, P], F32, tag="tp", name="kt")
-            for b in range(4):
-                nc.tensor.matmul(out=kt[:, b, :], lhsT=mm[:, 0, P * b:P * (b + 1)], rhs=ident[:],
-                                 is_transpose=True, start=True, stop=False)
-                nc.tensor.matmul(out=kt[:, b, :], lhsT=mm[:, 1, P * b:P * (b + 1)], rhs=ident[:],
-                                 is_transpose=True, start=False, stop=True)
-            kts = ktp.tile([P, 4, P], F32, tag="kts", name="kts")
-            for b in range(4):
-                nc.scalar.activation(out=kts[:, b, :], in_=kt[:, b, :], func=ACT.Copy, scale=wk_col[:, b:b + 1])
-            return kts
+            by_feature = ps_turn.tile([P, D // P, P], F32, tag="bank", name="by_feature")
+            for b in range(D // P):
+                for e in range(2):
+                    nc.tensor.matmul(out=by_feature[:, b, :], lhsT=halves[:, e, P * b:P * (b + 1)], rhs=ident[:],
+                                     is_transpose=True, start=(e == 0), stop=(e == 1))
+            gained = turned_k.tile([P, D // P, P], F32, name="gained")
+            for b in range(D // P):
+                nc.scalar.activation(out=gained[:, b, :], in_=by_feature[:, b, :], func=ACT.Copy,
+                                     scale=k_gain_col[:, b:b + 1])
+            by_token = ps_turn.tile([P, D // P, P], F32, tag="bank", name="by_token")
+            for b in range(D // P):
+                nc.tensor.transpose(by_token[:, b, :], gained[:, b, :], ident[:])
+            k = results.tile([P, D], F32, tag="result", name="k")
+            nc.scalar.activation(out=k[:], in_=by_token[:].rearrange("p b d -> p (b d)"), func=ACT.Copy,
+                                 scale=rstd[:, a + 1, KEY:KEY + 1])
+            nc.sync.dma_start(out=k_out[a], in_=k[:])
 
-        def finish_k(a, kts):
-            ko = ps_t.tile([P, 4, P], F32, tag="tp", name="ko")
-            for b in range(4):
-                nc.tensor.transpose(ko[:, b, :], kts[:, b, :], ident[:])
-            o = outp.tile([P, D], F32, tag="o", name="o")
-            nc.scalar.activation(out=o[:], in_=ko[:].rearrange("p b d -> p (b d)"), func=ACT.Copy,
-                                 scale=rstd[:, a + 1, 4:5])
-            nc.sync.dma_start(out=k_rows[a], in_=o[:])
-
-        G_TABLES = ()
-
-        def table(a):
-            if a in G_TABLES:
-                build_t(nc.gpsimd, wq_sb, a)
-            else:
-                build_t(nc.vector, wqb, a)
-
-        def norms_slot(a, g0, g1):
-            nc.scalar.activation(out=mse[:, a, g0:g1], in_=ms[:, a, g0:g1], func=ACT.Copy, bias=EPS)
-            nc.gpsimd.tensor_tensor(out=rstd[:, a, g0:g1], in0=mse[:, a, g0:g1], in1=nh[:, g0:g1], op=ALU.pow)
-
-        def k_tile(a):
-            finish_k(a, rope_k(a))
-            value(a)
-
-        trig(0, 2)
-        gains()
-        prep_x(0, 1, True)
-        for g in range(4):
-            prep_w(g, g + 1, g < 1)
-            if g == 0:
-                table(0)
-                table(1)
-            square(0, g)
-            norms_slot(0, g, g + 1)
-            rope_q(0, g)
-            square(1, g)
-            if g == 1:
-                trig(2, 4)
-        prep_w(4, 6, False)
-        square(0, 4)
-        norms_slot(1, 0, 5)
-        for a in range(1, NT):
+        make_trig(0, 2)
+        spread_q_gain()
+        spread_k_gain()
+        prepare_x(0, 2, True)
+        for h in range(HEADS):
+            prepare_w(h, h + 1, h == 0)
+            if h == 0:
+                make_q_table(0)
+                make_q_table(1)
+            mean_square(0, h)
+            make_rstd(0, h, h + 1)
+            rope_q(0, h)
+            mean_square(1, h)
+            if h == 1:
+                make_trig(2, 4)
+        prepare_w(KEY, KEY + 1, False)
+        mean_square(0, KEY)
+        make_rstd(1, 0, KEY + 1)
+        for a in range(1, TILES):
             if a == 1:
-                prep_x(1, 2, False)
-                table(2)
+                prepare_x(2, 4, False)
+                make_q_table(2)
+                prepare_w(VALUE, GROUPS, False)
             if a == 2:
-                trig(4, 8)
-                prep_x(2, 4, False)
-            last = a + 1 == NT
-            for g in range(4):
+                make_trig(4, TILES)
+                prepare_x(4, 6, False)
+                prepare_x(6, TILES, False)
+            last = a == TILES - 1
+            for h in range(HEADS):
                 if not last:
-                    square(a + 1, g)
-                if g == (0 if last else 3):
-                    square(a, 4)
-                    norms_slot(a + 1, 4 if last else 0, 5)
-                if last and g == 2:
-                    k_tile(a - 1)
-                    k_tile(a)
-                rope_q(a, g)
-            if a + 2 < NT:
-                table(a + 2)
+                    mean_square(a + 1, h)
+                if h == (0 if last else HEADS - 1):
+                    mean_square(a, KEY)
+                    make_rstd(a + 1, KEY if last else 0, KEY + 1)
+                if last and h == 1:
+                    for b in (a - 1, a):
+                        rope_k(b)
+                        store_v(b)
+                rope_q(a, h)
+            if a + 2 < TILES:
+                make_q_table(a + 2)
             if not last:
-                k_tile(a - 1)
+                rope_k(a - 1)
+                store_v(a - 1)

@@ -188,6 +188,10 @@ def tile_attention_pa_kernel(tc, x, wq, wkv, q_norm_w, k_norm_w, out_0, out_1, o
                                  accum_out=mean_sq[:, column_group, g:g + 1])
 
         def make_rstd(column_group, g0, g1):
+            if column_group >= 2:
+                nc.scalar.activation(out=rstd[:, column_group, g0:g1], in_=mean_sq[:, column_group, g0:g1],
+                                     func=ACT.Abs_reciprocal_sqrt, bias=EPS)
+                return
             nc.scalar.activation(out=mean_eps[:, column_group, g0:g1], in_=mean_sq[:, column_group, g0:g1],
                                  func=ACT.Copy, bias=EPS)
             nc.gpsimd.tensor_tensor(out=rstd[:, column_group, g0:g1], in0=mean_eps[:, column_group, g0:g1],
@@ -268,11 +272,11 @@ def tile_attention_pa_kernel(tc, x, wq, wkv, q_norm_w, k_norm_w, out_0, out_1, o
         make_rstd(1, 0, KEY + 1)
         for a in range(1, TILES):
             if a == 1:
+                make_trig(4, TILES)
                 prepare_x(2, 4, False)
                 make_q_table(2)
                 prepare_w(VALUE, GROUPS, False)
             if a == 2:
-                make_trig(4, TILES)
                 prepare_x(4, 6, False)
                 prepare_x(6, TILES, False)
             last = a == TILES - 1

@@ -27,6 +27,7 @@ GROUPS = 6
 EPS = 1.1920929e-07
 TWO_PI = 2.0 * math.pi
 STEP = 10000.0 ** (-1.0 / PAIRS)
+GPSIMD_TABLES = (5, 7)
 
 
 def tile_attention_pa_kernel(tc, x, wq, wkv, q_norm_w, k_norm_w, out_0, out_1, out_2):
@@ -66,6 +67,7 @@ def tile_attention_pa_kernel(tc, x, wq, wkv, q_norm_w, k_norm_w, out_0, out_1, o
         abs_frac = keep.tile([P, TILES, PAIRS], F32, name="abs_frac")
         trig = keep.tile([P, TILES, 3, PAIRS], F32, name="trig")
         q_table = keep.tile([P, TILES, 2, D], F32, name="q_table")
+        gain_planes = keep.tile([P, 2, 2, PAIRS], F32, name="gain_planes")
         mean_sq = keep.tile([P, TILES + 1, 8], F32, name="mean_sq")
         mean_eps = keep.tile([P, TILES + 1, 8], F32, name="mean_eps")
         rstd = keep.tile([P, TILES + 1, 8], F32, name="rstd")
@@ -204,7 +206,17 @@ def tile_attention_pa_kernel(tc, x, wq, wkv, q_norm_w, k_norm_w, out_0, out_1, o
             nc.scalar.copy(out=v[:].rearrange("p (q j) -> p q j", j=4), in_=bank[:].rearrange("p (j q) -> p q j", j=4))
             nc.sync.dma_start(out=v_out[a], in_=v[:])
 
+        def copy_q_gain():
+            for e in range(2):
+                nc.scalar.copy(out=gain_planes[:, :, e, :], in_=q_gain[:].rearrange("p (i r) -> p r i", r=2))
+
         def make_q_table(a):
+            if a in GPSIMD_TABLES:
+                for r in range(2):
+                    nc.gpsimd.tensor_tensor(out=q_table[:, a, r, :],
+                                            in0=gain_planes[:, r, :, :].rearrange("p e i -> p (e i)"),
+                                            in1=trig[:, a, r:r + 2, :].rearrange("p e i -> p (e i)"), op=ALU.mult)
+                return
             for e in range(2):
                 nc.vector.tensor_tensor(out=q_table[:, a, e, :].rearrange("p (i r) -> p i r", r=2),
                                         in0=q_gain[:].rearrange("p (i r) -> p i r", r=2),
@@ -218,7 +230,8 @@ def tile_attention_pa_kernel(tc, x, wq, wkv, q_norm_w, k_norm_w, out_0, out_1, o
             nc.vector.scalar_tensor_tensor(out=halves[:].rearrange("p e (i r) -> p (e i) r", r=2),
                                            in0=bank[:].unsqueeze(2).to_broadcast([P, D, 2]),
                                            scalar=rstd[:, a, h:h + 1],
-                                           in1=q_table[:, a, :, :].rearrange("p e (i r) -> p (e i) r", r=2),
+                                           in1=(q_table[:, a, :, :].rearrange("p r n -> p n r") if a in GPSIMD_TABLES
+                                                else q_table[:, a, :, :].rearrange("p e (i r) -> p (e i) r", r=2)),
                                            op0=ALU.mult, op1=ALU.mult)
             q = results.tile([P, D], F32, tag="result", name="q")
             engine = nc.vector if (a == TILES - 1 and h == HEADS - 1) else nc.gpsimd
@@ -270,6 +283,7 @@ def tile_attention_pa_kernel(tc, x, wq, wkv, q_norm_w, k_norm_w, out_0, out_1, o
         prepare_w(KEY, KEY + 1, False)
         mean_square(0, KEY)
         make_rstd(1, 0, KEY + 1)
+        copy_q_gain()
         for a in range(1, TILES):
             if a == 1:
                 make_trig(4, TILES)

@@ -74,8 +74,8 @@ def tile_attention_pa_kernel(tc, x, wq, wkv, q_norm_w, k_norm_w, out_0, out_1, o
         minus_half = keep.tile([P, 8], F32, name="minus_half")
 
         nc.vector.memset(one[:], 1.0)
-        nc.vector.memset(gain_rows[:], 0.0)
-        nc.vector.memset(ones[:], 1.0)
+        nc.gpsimd.memset(gain_rows[:], 0.0)
+        nc.gpsimd.memset(ones[:], 1.0)
         nc.scalar.activation(out=warm[:], in_=one[:], func=ACT.Sin)
         nc.gpsimd.iota(token[:], pattern=[[1, TILES]], base=0, channel_multiplier=TILES,
                        allow_small_or_imprecise_dtypes=True)
@@ -270,7 +270,7 @@ def tile_attention_pa_kernel(tc, x, wq, wkv, q_norm_w, k_norm_w, out_0, out_1, o
         spread_k_gain()
         prepare_x(0, 2, True)
         for h in range(HEADS):
-            prepare_w(h, h + 1, h == 0)
+            prepare_w(h, h + 1, h <= 1)
             if h == 0:
                 make_q_table(0)
                 make_q_table(1)

@@ -278,11 +278,12 @@ def tile_attention_pa_kernel(tc, x, wq, wkv, q_norm_w, k_norm_w, out_0, out_1, o
             make_rstd(0, h, h + 1)
             rope_q(0, h)
             mean_square(1, h)
+            make_rstd(1, h, h + 1)
             if h == 1:
                 make_trig(2, 4)
         prepare_w(KEY, KEY + 1, False)
         mean_square(0, KEY)
-        make_rstd(1, 0, KEY + 1)
+        make_rstd(1, KEY, KEY + 1)
         copy_q_gain()
         for a in range(1, TILES):
             if a == 1:

@@ -27,16 +27,18 @@ GROUPS = 6
 EPS = 1.1920929e-07
 TWO_PI = 2.0 * math.pi
 STEP = 10000.0 ** (-1.0 / PAIRS)
-GPSIMD_TABLES = (5, 7)
+GPSIMD_TABLES = (0, 1, 5, 7)
+V_COPIES = ((3, 0), (4, 0))
+V_TILES = ((), (), (), (), (0, 1, 2), (3,), (4,), (5, 6, 7))
 
 
 def tile_attention_pa_kernel(tc, x, wq, wkv, q_norm_w, k_norm_w, out_0, out_1, out_2):
     nc = tc.nc
     with ExitStack() as ctx:
         keep = ctx.enter_context(tc.tile_pool(name="keep", bufs=1))
-        products = ctx.enter_context(tc.tile_pool(name="products", bufs=4))
-        results = ctx.enter_context(tc.tile_pool(name="results", bufs=6))
-        values = ctx.enter_context(tc.tile_pool(name="values", bufs=2))
+        products = ctx.enter_context(tc.tile_pool(name="products", bufs=6))
+        results = ctx.enter_context(tc.tile_pool(name="results", bufs=8))
+        values = ctx.enter_context(tc.tile_pool(name="values", bufs=4))
         squares = ctx.enter_context(tc.tile_pool(name="squares", bufs=2))
         turned_k = ctx.enter_context(tc.tile_pool(name="turned_k", bufs=2))
         ps_turn = ctx.enter_context(tc.psum_pool(name="ps_turn", bufs=2))
@@ -67,20 +69,16 @@ def tile_attention_pa_kernel(tc, x, wq, wkv, q_norm_w, k_norm_w, out_0, out_1, o
         abs_frac = keep.tile([P, TILES, PAIRS], F32, name="abs_frac")
         trig = keep.tile([P, TILES, 3, PAIRS], F32, name="trig")
         q_table = keep.tile([P, TILES, 2, D], F32, name="q_table")
-        gain_planes = keep.tile([P, 2, 2, PAIRS], F32, name="gain_planes")
+        gain_planes = keep.tile([P, 2, PAIRS], F32, name="gain_planes")
         mean_sq = keep.tile([P, TILES + 1, 8], F32, name="mean_sq")
         mean_eps = keep.tile([P, TILES + 1, 8], F32, name="mean_eps")
         rstd = keep.tile([P, TILES + 1, 8], F32, name="rstd")
         minus_half = keep.tile([P, 8], F32, name="minus_half")
 
-        nc.vector.memset(one[:], 1.0)
-        nc.gpsimd.memset(gain_rows[:], 0.0)
-        nc.gpsimd.memset(ones[:], 1.0)
-        nc.scalar.activation(out=warm[:], in_=one[:], func=ACT.Sin)
-        nc.gpsimd.iota(token[:], pattern=[[1, TILES]], base=0, channel_multiplier=TILES,
-                       allow_small_or_imprecise_dtypes=True)
-        make_identity(nc, ident[:])
-        nc.gpsimd.memset(minus_half[:], -0.5)
+
+        ctx.enter_context(tc.manual_schedule(engines={mybir.EngineType.PE, mybir.EngineType.DVE,
+                                                      mybir.EngineType.Activation, mybir.EngineType.Pool}))
+        live = {}
 
         x_view = x.flatten_outer_dims().rearrange("(p a) k -> p a k", a=TILES)
         q_view = wq.rearrange("(h b p e) k -> h p b (e k)", h=HEADS, p=P, e=2)
@@ -90,87 +88,120 @@ def tile_attention_pa_kernel(tc, x, wq, wkv, q_norm_w, k_norm_w, out_0, out_1, o
         q_out = out_0.rearrange("o h (p a) d -> (o h) a p d", a=TILES)
         k_out = out_1.rearrange("o (p a) d -> (o a) p d", a=TILES)
         v_out = out_2.rearrange("o (p a) d -> (o a) p d", a=TILES)
-        nc.sync.dma_start(out=x_rows[:, 0:2, :], in_=x_view[:, 0:2, :])
-        nc.sync.dma_start(out=gain_rows[0:1, 0:D], in_=q_norm_w.rearrange("(o d) -> o d", o=1))
-        nc.sync.dma_start(out=gain_rows[0:1, D:2 * D], in_=k_norm_w.rearrange("(o d) -> o d", o=1))
-        for h in range(HEADS):
-            nc.sync.dma_start(out=w_slots[:, h], in_=q_view[h])
-        nc.sync.dma_start(out=w_slots[:, KEY], in_=k_view[0])
-        nc.sync.dma_start(out=w_rows[:, 4 * VALUE:4 * VALUE + 4, :].rearrange("p j k -> p (j k)"), in_=v_view[1])
-        for a in range(2, TILES, 2):
+        x_words = x_grouped[:].bitcast(F32).rearrange("p (c r u) -> p c r u", r=P, u=2)
+        w_words = w_grouped[:].bitcast(F32).rearrange("p (c r u) -> p c r u", r=P, u=2)
+        q_gain = ps_gain.tile([P, D], F32, name="q_gain")
+
+        def load_x(a):
             nc.sync.dma_start(out=x_rows[:, a:a + 2, :], in_=x_view[:, a:a + 2, :])
 
-        for i in range(4):
-            nc.vector.tensor_scalar_mul(out=turns[:, i:i + 1], in0=one[:], scalar1=STEP ** i / TWO_PI)
-        width = 4
-        while width < PAIRS:
-            for m in range(1, 4):
-                nc.vector.tensor_scalar_mul(out=turns[:, m * width:(m + 1) * width], in0=turns[:, 0:width],
-                                            scalar1=STEP ** (m * width))
-            width *= 4
-        for a0, a1 in ((0, 2), (2, 4), (4, TILES)):
+        def load_w(g):
+            if g < HEADS:
+                nc.sync.dma_start(out=w_slots[:, g], in_=q_view[g])
+            elif g == KEY:
+                nc.sync.dma_start(out=w_slots[:, KEY], in_=k_view[0])
+            else:
+                nc.sync.dma_start(out=w_rows[:, 4 * VALUE:4 * VALUE + 4, :].rearrange("p j k -> p (j k)"), in_=v_view[1])
+
+        def make_turns():
+            for i in range(4):
+                nc.vector.tensor_scalar_mul(out=turns[:, i:i + 1], in0=one[:], scalar1=STEP ** i / TWO_PI)
+            width = 4
+            while width < PAIRS:
+                for m in range(1, 4):
+                    nc.vector.tensor_scalar_mul(out=turns[:, m * width:(m + 1) * width], in0=turns[:, 0:width],
+                                                scalar1=STEP ** (m * width))
+                width *= 4
+
+        def angles(a0, a1):
             for a in range(a0, a1):
                 nc.vector.tensor_scalar_mul(out=angle[:, a, :], in0=turns[:], scalar1=token[:, a:a + 1])
             nc.vector.tensor_copy(out=whole[:, a0:a1, :], in_=angle[:, a0:a1, :])
             nc.vector.tensor_tensor(out=frac[:, a0:a1, :], in0=angle[:, a0:a1, :], in1=whole[:, a0:a1, :],
                                     op=ALU.subtract)
 
-        def make_trig(a0, a1):
-            nc.scalar.activation(out=abs_frac[:, a0:a1, :], in_=frac[:, a0:a1, :], func=ACT.Abs)
-            nc.scalar.activation(out=trig[:, a0:a1, 0, :], in_=abs_frac[:, a0:a1, :], func=ACT.Sin,
-                                 scale=-TWO_PI, bias=math.pi / 2)
-            nc.scalar.activation(out=trig[:, a0:a1, 1, :], in_=frac[:, a0:a1, :], func=ACT.Sin,
-                                 scale=TWO_PI)
-            nc.scalar.activation(out=trig[:, a0:a1, 2, :], in_=abs_frac[:, a0:a1, :], func=ACT.Sin,
-                                 scale=TWO_PI, bias=-math.pi / 2)
+        def angles_mul(a0, a1):
+            for a in range(a0, a1):
+                nc.vector.tensor_scalar_mul(out=angle[:, a, :], in0=turns[:], scalar1=token[:, a:a + 1])
 
-        q_gain = ps_gain.tile([P, D], F32, name="q_gain")
+        def angles_whole(a0, a1):
+            nc.vector.tensor_copy(out=whole[:, a0:a1, :], in_=angle[:, a0:a1, :])
+
+        def angles_frac(a0, a1):
+            nc.vector.tensor_tensor(out=frac[:, a0:a1, :], in0=angle[:, a0:a1, :], in1=whole[:, a0:a1, :],
+                                    op=ALU.subtract)
+
+        def trig_abs(a0, a1):
+            nc.scalar.activation(out=abs_frac[:, a0:a1, :], in_=frac[:, a0:a1, :], func=ACT.Abs)
+
+        def trig_plane(a0, a1, plane):
+            if plane == 0:
+                nc.scalar.activation(out=trig[:, a0:a1, 0, :], in_=abs_frac[:, a0:a1, :], func=ACT.Sin,
+                                     scale=-TWO_PI, bias=math.pi / 2)
+            elif plane == 1:
+                nc.scalar.activation(out=trig[:, a0:a1, 1, :], in_=frac[:, a0:a1, :], func=ACT.Sin, scale=TWO_PI)
+            else:
+                nc.scalar.activation(out=trig[:, a0:a1, 2, :], in_=abs_frac[:, a0:a1, :], func=ACT.Sin,
+                                     scale=TWO_PI, bias=-math.pi / 2)
+
+        def make_trig(a0, a1):
+            trig_abs(a0, a1)
+            for plane in range(3):
+                trig_plane(a0, a1, plane)
 
         def spread_q_gain():
             nc.tensor.matmul(out=q_gain[:], lhsT=ones[:], rhs=gain_rows[:, 0:D], start=True, stop=True)
 
-        def spread_k_gain():
+        def spread_k_gain_1():
             spread = ps_scalar.tile([P, D], F32, tag="bank", name="spread")
             nc.tensor.matmul(out=spread[:], lhsT=ones[:], rhs=gain_rows[:, D:2 * D], start=True, stop=True)
             nc.scalar.copy(out=k_gain[:], in_=spread[:])
+
+        def spread_k_gain_2():
             turned = ps_turn.tile([P, D // P, P], F32, tag="bank", name="turned")
             for b in range(D // P):
                 nc.tensor.transpose(turned[:, b, :], k_gain[:, P * b:P * (b + 1)], ident[:])
             nc.scalar.copy(out=k_gain_col[:], in_=turned[:, :, 0])
 
-        def turn(rows, grouped, on_vector):
+        def t_rows(key, rows):
             bank = ps_turn.tile([P, 2, 2, P], F32, tag="bank", name="bank")
             for c in range(2):
                 words = rows[:, c, :].bitcast(F32)
                 for u in range(2):
                     nc.tensor.transpose(bank[:, c, u, :], words[:, u:PAIRS:2], ident[:])
-            view = bank[:].rearrange("p c u r -> p c r u")
+            live[key] = bank
+
+        def c_rows(key, grouped, on_vector):
+            view = live[key][:].rearrange("p c u r -> p c r u")
             if on_vector:
                 nc.vector.tensor_copy(out=grouped, in_=view)
             else:
                 nc.scalar.copy(out=grouped, in_=view)
 
-        x_words = x_grouped[:].bitcast(F32).rearrange("p (c r u) -> p c r u", r=P, u=2)
-        w_words = w_grouped[:].bitcast(F32).rearrange("p (c r u) -> p c r u", r=P, u=2)
+        def t_x(a):
+            t_rows(("x", a), x_rows[:, a:a + 2, :])
 
-        def prepare_x(a0, a1, on_vector):
-            for a in range(a0, a1, 2):
-                turn(x_rows[:, a:a + 2, :], x_words[:, a:a + 2, :, :], on_vector)
-            nc.vector.quantize_mx(out=x_codes[:, P * a0:P * a1].bitcast(E5M2_X4),
-                                  scales=x_scales[:, P * a0:P * a1],
+        def c_x(a, on_vector):
+            c_rows(("x", a), x_words[:, a:a + 2, :, :], on_vector)
+
+        def q_x(a0, a1):
+            nc.vector.quantize_mx(out=x_codes[:, P * a0:P * a1].bitcast(E5M2_X4), scales=x_scales[:, P * a0:P * a1],
                                   in_=x_grouped[:, 4 * P * a0:4 * P * a1])
 
-        def prepare_w(g0, g1, on_vector):
-            for g in range(g0, g1):
-                for half in range(2):
-                    first = 4 * g + 2 * half
-                    if g == VALUE:
-                        rows = w_rows[:, first:first + 2, :]
-                    else:
-                        rows = w_rows[:, 4 * g + half:4 * g + 4:2, :]
-                    turn(rows, w_words[:, first:first + 2, :, :], on_vector)
-            nc.vector.quantize_mx(out=w_codes[:, D * g0:D * g1].bitcast(E5M2_X4),
-                                  scales=w_scales[:, D * g0:D * g1],
+        def t_w(g, half):
+            first = 4 * g + 2 * half
+            if g == VALUE:
+                rows = w_rows[:, first:first + 2, :]
+            else:
+                rows = w_rows[:, 4 * g + half:4 * g + 4:2, :]
+            t_rows(("w", g, half), rows)
+
+        def c_w(g, half, on_vector):
+            first = 4 * g + 2 * half
+            c_rows(("w", g, half), w_words[:, first:first + 2, :, :], on_vector)
+
+        def q_w(g0, g1):
+            nc.vector.quantize_mx(out=w_codes[:, D * g0:D * g1].bitcast(E5M2_X4), scales=w_scales[:, D * g0:D * g1],
                                   in_=w_grouped[:, 4 * D * g0:4 * D * g1])
 
         def project(bank, a, g):
@@ -181,41 +212,52 @@ def tile_attention_pa_kernel(tc, x, wq, wkv, q_norm_w, k_norm_w, out_0, out_1, o
                                 rhs_scale=w_scales[:, D * g:D * (g + 1)],
                                 start=True, stop=True)
 
-        def mean_square(a, g):
-            bank = ps_scalar.tile([P, D], F32, tag="bank", name="bank")
-            project(bank, a, g)
-            unused = squares.tile([P, D], BF16, name="unused")
-            column_group = a + 1 if g == KEY else a
-            nc.scalar.activation(out=unused[:], in_=bank[:], func=ACT.Square, scale=1.0 / math.sqrt(D),
-                                 accum_out=mean_sq[:, column_group, g:g + 1])
+        def ok(a):
+            return 0 <= a < TILES
 
-        def make_rstd(column_group, g0, g1):
-            if column_group >= 2:
-                nc.scalar.activation(out=rstd[:, column_group, g0:g1], in_=mean_sq[:, column_group, g0:g1],
-                                     func=ACT.Abs_reciprocal_sqrt, bias=EPS)
-                return
+        def ms(a, g):
+            if ok(a):
+                bank = ps_scalar.tile([P, D], F32, tag="bank", name="bank")
+                project(bank, a, g)
+                live[("s", a, g)] = bank
+
+        def sq(a, g):
+            if ok(a):
+                unused = squares.tile([P, D], BF16, name="unused")
+                column_group = a + 1 if g == KEY else a
+                nc.scalar.activation(out=unused[:], in_=live[("s", a, g)][:], func=ACT.Square, scale=1.0 / math.sqrt(D),
+                                     accum_out=mean_sq[:, column_group, g:g + 1])
+
+        def rs_pow(column_group, g0, g1):
             nc.scalar.activation(out=mean_eps[:, column_group, g0:g1], in_=mean_sq[:, column_group, g0:g1],
                                  func=ACT.Copy, bias=EPS)
             nc.gpsimd.tensor_tensor(out=rstd[:, column_group, g0:g1], in0=mean_eps[:, column_group, g0:g1],
                                     in1=minus_half[:, g0:g1], op=ALU.pow)
 
-        def store_v(a):
-            bank = ps_scalar.tile([P, D], F32, tag="bank", name="bank")
-            project(bank, a, VALUE)
-            v = values.tile([P, D], F32, name="v")
-            nc.scalar.copy(out=v[:].rearrange("p (q j) -> p q j", j=4), in_=bank[:].rearrange("p (j q) -> p q j", j=4))
-            nc.sync.dma_start(out=v_out[a], in_=v[:])
+        def rs(column_group):
+            if column_group <= TILES:
+                g0 = KEY if column_group == TILES else 0
+                nc.scalar.activation(out=rstd[:, column_group, g0:KEY + 1], in_=mean_sq[:, column_group, g0:KEY + 1],
+                                     func=ACT.Abs_reciprocal_sqrt, bias=EPS)
+
+        def vc(a):
+            if ok(a):
+                v = values.tile([P, D], F32, name="v")
+                nc.scalar.copy(out=v[:].rearrange("p (q j) -> p q j", j=4),
+                               in_=live[("s", a, VALUE)][:].rearrange("p (j q) -> p q j", j=4))
+                nc.sync.dma_start(out=v_out[a], in_=v[:])
 
         def copy_q_gain():
-            for e in range(2):
-                nc.scalar.copy(out=gain_planes[:, :, e, :], in_=q_gain[:].rearrange("p (i r) -> p r i", r=2))
+            nc.scalar.copy(out=gain_planes[:], in_=q_gain[:].rearrange("p (i r) -> p r i", r=2))
 
-        def make_q_table(a):
+        def tb(a):
+            if not ok(a):
+                return
             if a in GPSIMD_TABLES:
                 for r in range(2):
-                    nc.gpsimd.tensor_tensor(out=q_table[:, a, r, :],
-                                            in0=gain_planes[:, r, :, :].rearrange("p e i -> p (e i)"),
-                                            in1=trig[:, a, r:r + 2, :].rearrange("p e i -> p (e i)"), op=ALU.mult)
+                    nc.gpsimd.tensor_tensor(out=q_table[:, a, r, :].rearrange("p (e i) -> p e i", e=2),
+                                            in0=gain_planes[:, r, :].unsqueeze(1).to_broadcast([P, 2, PAIRS]),
+                                            in1=trig[:, a, r:r + 2, :], op=ALU.mult)
                 return
             for e in range(2):
                 nc.vector.tensor_tensor(out=q_table[:, a, e, :].rearrange("p (i r) -> p i r", r=2),
@@ -223,91 +265,286 @@ def tile_attention_pa_kernel(tc, x, wq, wkv, q_norm_w, k_norm_w, out_0, out_1, o
                                         in1=trig[:, a, e:e + 2, :].rearrange("p r i -> p i r"),
                                         op=ALU.mult)
 
-        def rope_q(a, h):
-            bank = ps_vector.tile([P, D], F32, tag="bank", name="bank")
-            project(bank, a, h)
+        def mv(a, g):
+            if ok(a):
+                bank = ps_vector.tile([P, D], F32, tag="bank", name="bank")
+                project(bank, a, g)
+                live[("v", a, g)] = bank
+
+        def p(a, h):
+            if not ok(a):
+                return
             halves = products.tile([P, 2, D], F32, name="halves")
             nc.vector.scalar_tensor_tensor(out=halves[:].rearrange("p e (i r) -> p (e i) r", r=2),
-                                           in0=bank[:].unsqueeze(2).to_broadcast([P, D, 2]),
+                                           in0=live[("v", a, h)][:].unsqueeze(2).to_broadcast([P, D, 2]),
                                            scalar=rstd[:, a, h:h + 1],
                                            in1=(q_table[:, a, :, :].rearrange("p r n -> p n r") if a in GPSIMD_TABLES
                                                 else q_table[:, a, :, :].rearrange("p e (i r) -> p (e i) r", r=2)),
                                            op0=ALU.mult, op1=ALU.mult)
+            live[("h", a, h)] = halves
+
+        def sub(a, h):
+            if not ok(a):
+                return
+            halves = live[("h", a, h)]
             q = results.tile([P, D], F32, tag="result", name="q")
             engine = nc.vector if (a == TILES - 1 and h == HEADS - 1) else nc.gpsimd
             engine.tensor_tensor(out=q[:], in0=halves[:, 0, :], in1=halves[:, 1, :], op=ALU.subtract)
             nc.sync.dma_start(out=q_out[h, a], in_=q[:])
 
-        def rope_k(a):
-            bank = ps_vector.tile([P, D], F32, tag="bank", name="bank")
-            project(bank, a, KEY)
+        def pk(a):
+            if not ok(a):
+                return
             halves = products.tile([P, 2, D], F32, name="halves")
+            bank = live[("v", a, KEY)]
             for e in range(2):
                 nc.vector.scalar_tensor_tensor(out=halves[:, e, :].rearrange("p (i r) -> p i r", r=2),
                                                in0=bank[:, PAIRS * e:PAIRS * (e + 1)].unsqueeze(2).to_broadcast([P, PAIRS, 2]),
                                                scalar=1.0 - 2.0 * e,
                                                in1=trig[:, a, e:e + 2, :].rearrange("p r i -> p i r"),
                                                op0=ALU.mult, op1=ALU.mult)
+            live[("h", a, KEY)] = halves
+
+        def ka(a):
+            if not ok(a):
+                return
+            halves = live[("h", a, KEY)]
             by_feature = ps_turn.tile([P, D // P, P], F32, tag="bank", name="by_feature")
             for b in range(D // P):
                 for e in range(2):
                     nc.tensor.matmul(out=by_feature[:, b, :], lhsT=halves[:, e, P * b:P * (b + 1)], rhs=ident[:],
                                      is_transpose=True, start=(e == 0), stop=(e == 1))
+            live[("f", a)] = by_feature
+
+        def kg(a):
+            if not ok(a):
+                return
             gained = turned_k.tile([P, D // P, P], F32, name="gained")
             for b in range(D // P):
-                nc.scalar.activation(out=gained[:, b, :], in_=by_feature[:, b, :], func=ACT.Copy,
+                nc.scalar.activation(out=gained[:, b, :], in_=live[("f", a)][:, b, :], func=ACT.Copy,
                                      scale=k_gain_col[:, b:b + 1])
+            live[("g", a)] = gained
+
+        def kb(a):
+            if not ok(a):
+                return
             by_token = ps_turn.tile([P, D // P, P], F32, tag="bank", name="by_token")
             for b in range(D // P):
-                nc.tensor.transpose(by_token[:, b, :], gained[:, b, :], ident[:])
+                nc.tensor.transpose(by_token[:, b, :], live[("g", a)][:, b, :], ident[:])
+            live[("t", a)] = by_token
+
+        def kf(a):
+            if not ok(a):
+                return
             k = results.tile([P, D], F32, tag="result", name="k")
-            nc.scalar.activation(out=k[:], in_=by_token[:].rearrange("p b d -> p (b d)"), func=ACT.Copy,
+            nc.scalar.activation(out=k[:], in_=live[("t", a)][:].rearrange("p b d -> p (b d)"), func=ACT.Copy,
                                  scale=rstd[:, a + 1, KEY:KEY + 1])
             nc.sync.dma_start(out=k_out[a], in_=k[:])
 
+        nc.vector.memset(one[:], 1.0)
+        nc.scalar.activation(out=warm[:], in_=one[:], func=ACT.Sin)
+        nc.gpsimd.iota(token[:], pattern=[[1, TILES]], base=0, channel_multiplier=TILES,
+                       allow_small_or_imprecise_dtypes=True)
+        nc.gpsimd.memset(gain_rows[:], 0.0)
+        make_identity(nc, ident[:])
+        nc.gpsimd.memset(ones[:], 1.0)
+        nc.gpsimd.memset(minus_half[:], -0.5)
+        load_x(0)
+        load_w(0)
+        load_w(1)
+        nc.sync.dma_start(out=gain_rows[0:1, 0:D], in_=q_norm_w.rearrange("(o d) -> o d", o=1))
+        nc.sync.dma_start(out=gain_rows[0:1, D:2 * D], in_=k_norm_w.rearrange("(o d) -> o d", o=1))
+        load_w(2)
+        load_w(3)
+        load_x(2)
+        load_w(KEY)
+        load_x(4)
+        load_x(6)
+        load_w(VALUE)
+        make_turns()
+        angles(0, 2)
         make_trig(0, 2)
+        t_x(0)
+        c_x(0, True)
+        q_x(0, 2)
+        t_w(0, 0)
+        t_w(0, 1)
+        c_w(0, 0, True)
+        c_w(0, 1, True)
+        q_w(0, 1)
         spread_q_gain()
-        spread_k_gain()
-        prepare_x(0, 2, True)
-        for h in range(HEADS):
-            prepare_w(h, h + 1, h <= 1)
-            if h == 0:
-                make_q_table(0)
-                make_q_table(1)
-            mean_square(0, h)
-            make_rstd(0, h, h + 1)
-            rope_q(0, h)
-            mean_square(1, h)
-            make_rstd(1, h, h + 1)
-            if h == 1:
-                make_trig(2, 4)
-        prepare_w(KEY, KEY + 1, False)
-        mean_square(0, KEY)
-        make_rstd(1, KEY, KEY + 1)
         copy_q_gain()
+        tb(0)
+        t_w(1, 0)
+        t_w(1, 1)
+        ms(0, 0)
+        mv(0, 0)
+        c_w(1, 0, False)
+        c_w(1, 1, False)
+        angles_mul(2, 4)
+        angles_whole(2, 4)
+        q_w(1, 2)
+        sq(0, 0)
+        rs_pow(0, 0, 1)
+        tb(1)
+        angles_frac(2, 4)
+        angles_mul(4, TILES)
+        for h in range(HEADS):
+            nxt = h + 2
+            if nxt < HEADS:
+                t_w(nxt, 0)
+                t_w(nxt, 1)
+            elif nxt == HEADS:
+                t_x(2)
+                t_w(KEY, 0)
+            else:
+                t_w(KEY, 1)
+            if h + 1 < HEADS:
+                ms(0, h + 1)
+                mv(0, h + 1)
+            ms(1, h)
+            if nxt < HEADS:
+                c_w(nxt, 0, (nxt, 0) in V_COPIES)
+                c_w(nxt, 1, (nxt, 1) in V_COPIES)
+            elif nxt == HEADS:
+                c_x(2, "x2" in V_COPIES)
+                c_w(KEY, 0, (KEY, 0) in V_COPIES)
+            else:
+                c_w(KEY, 1, (KEY, 1) in V_COPIES)
+            if h + 1 < HEADS:
+                sq(0, h + 1)
+                rs_pow(0, h + 1, h + 2)
+            if nxt < HEADS:
+                q_w(nxt, nxt + 1)
+            elif nxt == HEADS:
+                q_x(2, 4)
+            else:
+                q_w(KEY, KEY + 1)
+            p(0, h)
+            sub(0, h)
+            sq(1, h)
+            rs_pow(1, h, h + 1)
+            if h == 0:
+                angles_whole(4, TILES)
+                trig_abs(2, 4)
+            if h == 1:
+                angles_frac(4, TILES)
+                trig_plane(2, 4, 0)
+            if h == 2:
+                trig_plane(2, 4, 1)
+            if h == 3:
+                trig_plane(2, 4, 2)
+        for h in range(3):
+            mv(1, h)
+        ms(2, 0)
+        ms(2, 1)
+        trig_abs(4, TILES)
+        tb(2)
         for a in range(1, TILES):
-            if a == 1:
-                make_trig(4, TILES)
-                prepare_x(2, 4, False)
-                make_q_table(2)
-                prepare_w(VALUE, GROUPS, False)
-            if a == 2:
-                prepare_x(4, 6, False)
-                prepare_x(6, TILES, False)
             last = a == TILES - 1
-            for h in range(HEADS):
-                if not last:
-                    mean_square(a + 1, h)
-                if h == (0 if last else HEADS - 1):
-                    mean_square(a, KEY)
-                    make_rstd(a + 1, KEY if last else 0, KEY + 1)
-                if last and h == 1:
-                    for b in (a - 1, a):
-                        rope_k(b)
-                        store_v(b)
-                rope_q(a, h)
-            if a + 2 < TILES:
-                make_q_table(a + 2)
+            first = a == 1
+            done = 0 if a == 2 else a - 1
+            p(a, 0)
+            if a == 4:
+                q_w(VALUE, GROUPS)
+            sq(a + 1, 0)
+            ms(a + 1, 2)
+            if last:
+                pk(a)
+                mv(a, 2)
+                vc(V_TILES[a][0])
+                ms(V_TILES[a][1], VALUE)
+                ka(a)
+            p(a, 1)
+            sub(a, 0)
+            mv(a, 3)
+            sq(a + 1, 1)
+            ms(a + 1, 3)
+            if first:
+                trig_plane(4, TILES, 0)
+            else:
+                kg(done)
+                kb(done)
+            if last:
+                vc(V_TILES[a][1])
+                ms(V_TILES[a][2], VALUE)
+            sq(a + 1, 2)
+            if first:
+                trig_plane(4, TILES, 1)
+            p(a, 2)
+            sub(a, 1)
             if not last:
-                rope_k(a - 1)
-                store_v(a - 1)
+                mv(0 if first else a, KEY)
+                ms(a, KEY)
+            sq(a + 1, 3)
+            if not first:
+                kf(done)
+            if last:
+                kg(a)
+                kb(a)
+                vc(V_TILES[a][2])
+                kf(a)
+            p(a, 3)
+            if first:
+                trig_plane(4, TILES, 2)
+            if a == 2:
+                kg(1)
+            sub(a, 2)
+            if first:
+                mv(1, KEY)
+                t_x(4)
+            else:
+                mv(a + 1, 0)
+            if not last:
+                sq(a, KEY)
+            if first:
+                ms(0, KEY)
+                sq(0, KEY)
+            if a == 2:
+                kb(1)
+            if first:
+                pk(0)
+                spread_k_gain_1()
+                mv(a + 1, 0)
+            if not last:
+                pk(a)
+                rs(a + 1)
+            if first:
+                nc.scalar.activation(out=rstd[:, 1, KEY:KEY + 1], in_=mean_sq[:, 1, KEY:KEY + 1],
+                                     func=ACT.Abs_reciprocal_sqrt, bias=EPS)
+                spread_k_gain_2()
+            if a == 2:
+                kf(1)
+                t_x(6)
+                c_x(6, False)
+            if a == 3:
+                q_x(6, TILES)
+                t_w(VALUE, 0)
+                c_w(VALUE, 0, False)
+                t_w(VALUE, 1)
+                c_w(VALUE, 1, False)
+            mv(a + 1, 1)
+            if not last:
+                for b in V_TILES[a]:
+                    ms(b, VALUE)
+                    vc(b)
+            sub(a, 3)
+            ms(a + 2, 0)
+            ms(a + 2, 1)
+            if a == TILES - 2:
+                ms(a + 1, KEY)
+                sq(a + 1, KEY)
+                rs(a + 2)
+                ms(V_TILES[a + 1][0], VALUE)
+            tb(a + 2)
+            if first:
+                c_x(4, True)
+                q_x(4, 6)
+            if a == TILES - 2:
+                mv(a + 1, KEY)
+            else:
+                mv(a + 1, 2)
+            if first:
+                ka(0)
+            if not last:
+                ka(a)

@@ -27,9 +27,7 @@ GROUPS = 6
 EPS = 1.1920929e-07
 TWO_PI = 2.0 * math.pi
 STEP = 10000.0 ** (-1.0 / PAIRS)
-GPSIMD_TABLES = (0, 1, 5, 7)
-V_COPIES = ((3, 0), (4, 0))
-V_TILES = ((), (), (), (), (0, 1, 2), (3,), (4,), (5, 6, 7))
+GPSIMD_TABLES = (4, 5, 6, 7)
 
 
 def tile_attention_pa_kernel(tc, x, wq, wkv, q_norm_w, k_norm_w, out_0, out_1, out_2):
@@ -38,7 +36,7 @@ def tile_attention_pa_kernel(tc, x, wq, wkv, q_norm_w, k_norm_w, out_0, out_1, o
         keep = ctx.enter_context(tc.tile_pool(name="keep", bufs=1))
         products = ctx.enter_context(tc.tile_pool(name="products", bufs=6))
         results = ctx.enter_context(tc.tile_pool(name="results", bufs=8))
-        values = ctx.enter_context(tc.tile_pool(name="values", bufs=4))
+        values = ctx.enter_context(tc.tile_pool(name="values", bufs=3))
         squares = ctx.enter_context(tc.tile_pool(name="squares", bufs=2))
         turned_k = ctx.enter_context(tc.tile_pool(name="turned_k", bufs=2))
         ps_turn = ctx.enter_context(tc.psum_pool(name="ps_turn", bufs=2))
@@ -163,8 +161,8 @@ def tile_attention_pa_kernel(tc, x, wq, wkv, q_norm_w, k_norm_w, out_0, out_1, o
                 nc.tensor.transpose(turned[:, b, :], k_gain[:, P * b:P * (b + 1)], ident[:])
             nc.scalar.copy(out=k_gain_col[:], in_=turned[:, :, 0])
 
-        def t_rows(key, rows):
-            bank = ps_turn.tile([P, 2, 2, P], F32, tag="bank", name="bank")
+        def t_rows(key, rows, pool):
+            bank = pool.tile([P, 2, 2, P], F32, tag="bank", name="bank")
             for c in range(2):
                 words = rows[:, c, :].bitcast(F32)
                 for u in range(2):
@@ -178,8 +176,8 @@ def tile_attention_pa_kernel(tc, x, wq, wkv, q_norm_w, k_norm_w, out_0, out_1, o
             else:
                 nc.scalar.copy(out=grouped, in_=view)
 
-        def t_x(a):
-            t_rows(("x", a), x_rows[:, a:a + 2, :])
+        def t_x(a, pool):
+            t_rows(("x", a), x_rows[:, a:a + 2, :], pool)
 
         def c_x(a, on_vector):
             c_rows(("x", a), x_words[:, a:a + 2, :, :], on_vector)
@@ -188,13 +186,13 @@ def tile_attention_pa_kernel(tc, x, wq, wkv, q_norm_w, k_norm_w, out_0, out_1, o
             nc.vector.quantize_mx(out=x_codes[:, P * a0:P * a1].bitcast(E5M2_X4), scales=x_scales[:, P * a0:P * a1],
                                   in_=x_grouped[:, 4 * P * a0:4 * P * a1])
 
-        def t_w(g, half):
+        def t_w(g, half, pool):
             first = 4 * g + 2 * half
             if g == VALUE:
                 rows = w_rows[:, first:first + 2, :]
             else:
                 rows = w_rows[:, 4 * g + half:4 * g + 4:2, :]
-            t_rows(("w", g, half), rows)
+            t_rows(("w", g, half), rows, pool)
 
         def c_w(g, half, on_vector):
             first = 4 * g + 2 * half
@@ -224,9 +222,8 @@ def tile_attention_pa_kernel(tc, x, wq, wkv, q_norm_w, k_norm_w, out_0, out_1, o
         def sq(a, g):
             if ok(a):
                 unused = squares.tile([P, D], BF16, name="unused")
-                column_group = a + 1 if g == KEY else a
                 nc.scalar.activation(out=unused[:], in_=live[("s", a, g)][:], func=ACT.Square, scale=1.0 / math.sqrt(D),
-                                     accum_out=mean_sq[:, column_group, g:g + 1])
+                                     accum_out=mean_sq[:, a, g:g + 1])
 
         def rs_pow(column_group, g0, g1):
             nc.scalar.activation(out=mean_eps[:, column_group, g0:g1], in_=mean_sq[:, column_group, g0:g1],
@@ -234,10 +231,9 @@ def tile_attention_pa_kernel(tc, x, wq, wkv, q_norm_w, k_norm_w, out_0, out_1, o
             nc.gpsimd.tensor_tensor(out=rstd[:, column_group, g0:g1], in0=mean_eps[:, column_group, g0:g1],
                                     in1=minus_half[:, g0:g1], op=ALU.pow)
 
-        def rs(column_group):
-            if column_group <= TILES:
-                g0 = KEY if column_group == TILES else 0
-                nc.scalar.activation(out=rstd[:, column_group, g0:KEY + 1], in_=mean_sq[:, column_group, g0:KEY + 1],
+        def rs(a):
+            if ok(a):
+                nc.scalar.activation(out=rstd[:, a, 0:KEY + 1], in_=mean_sq[:, a, 0:KEY + 1],
                                      func=ACT.Abs_reciprocal_sqrt, bias=EPS)
 
         def vc(a):
@@ -338,213 +334,141 @@ def tile_attention_pa_kernel(tc, x, wq, wkv, q_norm_w, k_norm_w, out_0, out_1, o
                 return
             k = results.tile([P, D], F32, tag="result", name="k")
             nc.scalar.activation(out=k[:], in_=live[("t", a)][:].rearrange("p b d -> p (b d)"), func=ACT.Copy,
-                                 scale=rstd[:, a + 1, KEY:KEY + 1])
+                                 scale=rstd[:, a, KEY:KEY + 1])
             nc.sync.dma_start(out=k_out[a], in_=k[:])
 
         nc.vector.memset(one[:], 1.0)
         nc.scalar.activation(out=warm[:], in_=one[:], func=ACT.Sin)
+        nc.gpsimd.memset(gain_rows[:], 0.0)
         nc.gpsimd.iota(token[:], pattern=[[1, TILES]], base=0, channel_multiplier=TILES,
                        allow_small_or_imprecise_dtypes=True)
-        nc.gpsimd.memset(gain_rows[:], 0.0)
         make_identity(nc, ident[:])
         nc.gpsimd.memset(ones[:], 1.0)
-        nc.gpsimd.memset(minus_half[:], -0.5)
         load_x(0)
-        load_w(0)
-        load_w(1)
+        for g in range(HEADS):
+            load_w(g)
+        load_w(KEY)
         nc.sync.dma_start(out=gain_rows[0:1, 0:D], in_=q_norm_w.rearrange("(o d) -> o d", o=1))
         nc.sync.dma_start(out=gain_rows[0:1, D:2 * D], in_=k_norm_w.rearrange("(o d) -> o d", o=1))
-        load_w(2)
-        load_w(3)
-        load_x(2)
-        load_w(KEY)
-        load_x(4)
-        load_x(6)
+        for a in range(2, TILES, 2):
+            load_x(a)
         load_w(VALUE)
         make_turns()
         angles(0, 2)
         make_trig(0, 2)
-        t_x(0)
+        angles(2, 4)
+        make_trig(2, 4)
+        angles(4, TILES)
+        make_trig(4, TILES)
+        t_x(0, ps_vector)
         c_x(0, True)
         q_x(0, 2)
-        t_w(0, 0)
-        t_w(0, 1)
-        c_w(0, 0, True)
-        c_w(0, 1, True)
-        q_w(0, 1)
+        for g in range(3):
+            t_w(g, 0, ps_vector)
+            c_w(g, 0, True)
+            t_w(g, 1, ps_vector)
+            c_w(g, 1, True)
+            q_w(g, g + 1)
+        t_w(3, 0, ps_vector)
+        t_w(3, 1, ps_scalar)
+        t_w(KEY, 0, ps_turn)
+        t_w(KEY, 1, ps_scalar)
+        c_w(3, 0, True)
+        c_w(3, 1, False)
+        q_w(3, 4)
+        t_x(2, ps_turn)
+        c_w(KEY, 0, False)
+        t_x(4, ps_scalar)
+        c_w(KEY, 1, False)
+        q_w(KEY, KEY + 1)
+        t_x(6, ps_turn)
+        c_x(2, False)
+        q_x(2, 4)
+        t_w(VALUE, 0, ps_scalar)
+        c_x(4, False)
+        t_w(VALUE, 1, ps_turn)
+        c_x(6, False)
+        q_x(4, TILES)
+        c_w(VALUE, 0, False)
+        c_w(VALUE, 1, False)
+        q_w(VALUE, GROUPS)
         spread_q_gain()
         copy_q_gain()
-        tb(0)
-        t_w(1, 0)
-        t_w(1, 1)
-        ms(0, 0)
-        mv(0, 0)
-        c_w(1, 0, False)
-        c_w(1, 1, False)
-        angles_mul(2, 4)
-        angles_whole(2, 4)
-        q_w(1, 2)
-        sq(0, 0)
-        rs_pow(0, 0, 1)
-        tb(1)
-        angles_frac(2, 4)
-        angles_mul(4, TILES)
-        for h in range(HEADS):
-            nxt = h + 2
-            if nxt < HEADS:
-                t_w(nxt, 0)
-                t_w(nxt, 1)
-            elif nxt == HEADS:
-                t_x(2)
-                t_w(KEY, 0)
-            else:
-                t_w(KEY, 1)
-            if h + 1 < HEADS:
-                ms(0, h + 1)
-                mv(0, h + 1)
-            ms(1, h)
-            if nxt < HEADS:
-                c_w(nxt, 0, (nxt, 0) in V_COPIES)
-                c_w(nxt, 1, (nxt, 1) in V_COPIES)
-            elif nxt == HEADS:
-                c_x(2, "x2" in V_COPIES)
-                c_w(KEY, 0, (KEY, 0) in V_COPIES)
-            else:
-                c_w(KEY, 1, (KEY, 1) in V_COPIES)
-            if h + 1 < HEADS:
-                sq(0, h + 1)
-                rs_pow(0, h + 1, h + 2)
-            if nxt < HEADS:
-                q_w(nxt, nxt + 1)
-            elif nxt == HEADS:
-                q_x(2, 4)
-            else:
-                q_w(KEY, KEY + 1)
-            p(0, h)
-            sub(0, h)
-            sq(1, h)
-            rs_pow(1, h, h + 1)
-            if h == 0:
-                angles_whole(4, TILES)
-                trig_abs(2, 4)
-            if h == 1:
-                angles_frac(4, TILES)
-                trig_plane(2, 4, 0)
-            if h == 2:
-                trig_plane(2, 4, 1)
-            if h == 3:
-                trig_plane(2, 4, 2)
+        for g in range(KEY + 1):
+            ms(0, g)
+            sq(0, g)
+        rs(0)
+        for a in range(6):
+            tb(a)
+        ms(1, 0)
+        ms(1, 1)
         for h in range(3):
-            mv(1, h)
-        ms(2, 0)
-        ms(2, 1)
-        trig_abs(4, TILES)
-        tb(2)
-        for a in range(1, TILES):
+            mv(0, h)
+        for a in range(TILES):
             last = a == TILES - 1
-            first = a == 1
-            done = 0 if a == 2 else a - 1
+            if last:
+                pk(a)
+                vc(a)
+                kg(a - 1)
+                mv(a, 2)
+                kb(a - 1)
+                ka(a)
             p(a, 0)
-            if a == 4:
-                q_w(VALUE, GROUPS)
             sq(a + 1, 0)
             ms(a + 1, 2)
             if last:
-                pk(a)
-                mv(a, 2)
-                vc(V_TILES[a][0])
-                ms(V_TILES[a][1], VALUE)
-                ka(a)
+                mv(a, 3)
+                kf(a - 1)
+                kg(a)
+                kb(a)
             p(a, 1)
             sub(a, 0)
-            mv(a, 3)
+            if not last:
+                mv(a, 3)
             sq(a + 1, 1)
             ms(a + 1, 3)
-            if first:
-                trig_plane(4, TILES, 0)
-            else:
-                kg(done)
-                kb(done)
-            if last:
-                vc(V_TILES[a][1])
-                ms(V_TILES[a][2], VALUE)
             sq(a + 1, 2)
-            if first:
-                trig_plane(4, TILES, 1)
+            ms(a + 1, KEY)
+            if last:
+                kf(a)
             p(a, 2)
             sub(a, 1)
             if not last:
-                mv(0 if first else a, KEY)
-                ms(a, KEY)
+                mv(a, KEY)
             sq(a + 1, 3)
-            if not first:
-                kf(done)
-            if last:
-                kg(a)
-                kb(a)
-                vc(V_TILES[a][2])
-                kf(a)
+            if not last:
+                ms(a, VALUE)
             p(a, 3)
-            if first:
-                trig_plane(4, TILES, 2)
-            if a == 2:
-                kg(1)
             sub(a, 2)
-            if first:
-                mv(1, KEY)
-                t_x(4)
+            if a == TILES - 2:
+                mv(a + 1, KEY)
             else:
                 mv(a + 1, 0)
+            sq(a + 1, KEY)
+            rs(a + 1)
             if not last:
-                sq(a, KEY)
-            if first:
-                ms(0, KEY)
-                sq(0, KEY)
-            if a == 2:
-                kb(1)
-            if first:
-                pk(0)
-                spread_k_gain_1()
-                mv(a + 1, 0)
-            if not last:
+                kg(a - 1)
+                kb(a - 1)
                 pk(a)
-                rs(a + 1)
-            if first:
-                nc.scalar.activation(out=rstd[:, 1, KEY:KEY + 1], in_=mean_sq[:, 1, KEY:KEY + 1],
-                                     func=ACT.Abs_reciprocal_sqrt, bias=EPS)
-                spread_k_gain_2()
-            if a == 2:
-                kf(1)
-                t_x(6)
-                c_x(6, False)
-            if a == 3:
-                q_x(6, TILES)
-                t_w(VALUE, 0)
-                c_w(VALUE, 0, False)
-                t_w(VALUE, 1)
-                c_w(VALUE, 1, False)
-            mv(a + 1, 1)
+                vc(a)
+            if a == TILES - 2:
+                mv(a + 1, 0)
+            else:
+                mv(a + 1, 1)
             if not last:
-                for b in V_TILES[a]:
-                    ms(b, VALUE)
-                    vc(b)
+                kf(a - 1)
+            if a == 0:
+                spread_k_gain_1()
+                spread_k_gain_2()
             sub(a, 3)
             ms(a + 2, 0)
             ms(a + 2, 1)
             if a == TILES - 2:
-                ms(a + 1, KEY)
-                sq(a + 1, KEY)
-                rs(a + 2)
-                ms(V_TILES[a + 1][0], VALUE)
-            tb(a + 2)
-            if first:
-                c_x(4, True)
-                q_x(4, 6)
-            if a == TILES - 2:
-                mv(a + 1, KEY)
+                ms(a + 1, VALUE)
+                mv(a + 1, 1)
             else:
                 mv(a + 1, 2)
-            if first:
-                ka(0)
             if not last:
                 ka(a)
+            if a in (1, 3):
+                tb(6 + a // 2)

@@ -354,43 +354,60 @@ def tile_attention_pa_kernel(tc, x, wq, wkv, q_norm_w, k_norm_w, out_0, out_1, o
             load_x(a)
         load_w(VALUE)
         make_turns()
-        angles(0, 2)
-        make_trig(0, 2)
-        angles(2, 4)
-        make_trig(2, 4)
-        angles(4, TILES)
-        make_trig(4, TILES)
+        angles_mul(0, 4)
+        angles_whole(0, 2)
+        angles_mul(4, 6)
+        angles_frac(0, 2)
+        angles_whole(2, 4)
+        angles_mul(6, TILES)
+        angles_frac(2, 4)
+        angles_whole(4, TILES)
         t_x(0, ps_vector)
+        t_w(0, 0, ps_vector)
+        t_w(0, 1, ps_vector)
         c_x(0, True)
+        angles_frac(4, TILES)
+        for a0, a1 in ((0, 2), (2, 4), (4, TILES)):
+            trig_abs(a0, a1)
+            trig_plane(a0, a1, 1)
+            trig_plane(a0, a1, 0)
+            trig_plane(a0, a1, 2)
+        c_w(0, 0, True)
         q_x(0, 2)
-        for g in range(3):
-            t_w(g, 0, ps_vector)
-            c_w(g, 0, True)
-            t_w(g, 1, ps_vector)
-            c_w(g, 1, True)
-            q_w(g, g + 1)
+        t_w(1, 0, ps_vector)
+        c_w(0, 1, True)
+        t_w(1, 1, ps_vector)
+        c_w(1, 0, True)
+        q_w(0, 1)
+        t_w(2, 0, ps_vector)
+        c_w(1, 1, True)
+        t_w(2, 1, ps_vector)
+        c_w(2, 0, True)
+        q_w(1, 2)
         t_w(3, 0, ps_vector)
+        c_w(2, 1, True)
         t_w(3, 1, ps_scalar)
         t_w(KEY, 0, ps_turn)
         t_w(KEY, 1, ps_scalar)
         c_w(3, 0, True)
+        q_w(2, 3)
         c_w(3, 1, False)
-        q_w(3, 4)
         t_x(2, ps_turn)
         c_w(KEY, 0, False)
         t_x(4, ps_scalar)
         c_w(KEY, 1, False)
-        q_w(KEY, KEY + 1)
         t_x(6, ps_turn)
         c_x(2, False)
-        q_x(2, 4)
         t_w(VALUE, 0, ps_scalar)
         c_x(4, False)
         t_w(VALUE, 1, ps_turn)
         c_x(6, False)
-        q_x(4, TILES)
         c_w(VALUE, 0, False)
         c_w(VALUE, 1, False)
+        q_w(3, 4)
+        q_w(KEY, KEY + 1)
+        q_x(2, 4)
+        q_x(4, TILES)
         q_w(VALUE, GROUPS)
         spread_q_gain()
         copy_q_gain()

@@ -28,6 +28,7 @@ EPS = 1.1920929e-07
 TWO_PI = 2.0 * math.pi
 STEP = 10000.0 ** (-1.0 / PAIRS)
 GPSIMD_TABLES = (4, 5, 6, 7)
+REDUCED = sum(1 for i in range(PAIRS) if (TOKENS - 1) * STEP ** i / TWO_PI > 0.5)
 
 
 def tile_attention_pa_kernel(tc, x, wq, wkv, q_norm_w, k_norm_w, out_0, out_1, out_2):
@@ -40,6 +41,7 @@ def tile_attention_pa_kernel(tc, x, wq, wkv, q_norm_w, k_norm_w, out_0, out_1, o
         squares = ctx.enter_context(tc.tile_pool(name="squares", bufs=2))
         turned_k = ctx.enter_context(tc.tile_pool(name="turned_k", bufs=2))
         ps_turn = ctx.enter_context(tc.psum_pool(name="ps_turn", bufs=2))
+        k_products = ctx.enter_context(tc.tile_pool(name="k_products", bufs=3))
         ps_gain = ctx.enter_context(tc.psum_pool(name="ps_gain", bufs=1))
         ps_scalar = ctx.enter_context(tc.psum_pool(name="ps_scalar", bufs=2))
         ps_vector = ctx.enter_context(tc.psum_pool(name="ps_vector", bufs=3))
@@ -61,7 +63,6 @@ def tile_attention_pa_kernel(tc, x, wq, wkv, q_norm_w, k_norm_w, out_0, out_1, o
         warm = keep.tile([P, 1], F32, name="warm")
         turns = keep.tile([P, PAIRS], F32, name="turns")
         token = keep.tile([P, TILES], F32, name="token")
-        angle = keep.tile([P, TILES, PAIRS], F32, name="angle")
         whole = keep.tile([P, TILES, PAIRS], I32, name="whole")
         frac = keep.tile([P, TILES, PAIRS], F32, name="frac")
         abs_frac = keep.tile([P, TILES, PAIRS], F32, name="abs_frac")
@@ -111,23 +112,16 @@ def tile_attention_pa_kernel(tc, x, wq, wkv, q_norm_w, k_norm_w, out_0, out_1, o
                                                 scalar1=STEP ** (m * width))
                 width *= 4
 
-        def angles(a0, a1):
-            for a in range(a0, a1):
-                nc.vector.tensor_scalar_mul(out=angle[:, a, :], in0=turns[:], scalar1=token[:, a:a + 1])
-            nc.vector.tensor_copy(out=whole[:, a0:a1, :], in_=angle[:, a0:a1, :])
-            nc.vector.tensor_tensor(out=frac[:, a0:a1, :], in0=angle[:, a0:a1, :], in1=whole[:, a0:a1, :],
-                                    op=ALU.subtract)
-
         def angles_mul(a0, a1):
             for a in range(a0, a1):
-                nc.vector.tensor_scalar_mul(out=angle[:, a, :], in0=turns[:], scalar1=token[:, a:a + 1])
+                nc.vector.tensor_scalar_mul(out=frac[:, a, :], in0=turns[:], scalar1=token[:, a:a + 1])
 
         def angles_whole(a0, a1):
-            nc.vector.tensor_copy(out=whole[:, a0:a1, :], in_=angle[:, a0:a1, :])
+            nc.vector.tensor_copy(out=whole[:, a0:a1, 0:REDUCED], in_=frac[:, a0:a1, 0:REDUCED])
 
         def angles_frac(a0, a1):
-            nc.vector.tensor_tensor(out=frac[:, a0:a1, :], in0=angle[:, a0:a1, :], in1=whole[:, a0:a1, :],
-                                    op=ALU.subtract)
+            nc.vector.tensor_tensor(out=frac[:, a0:a1, 0:REDUCED], in0=frac[:, a0:a1, 0:REDUCED],
+                                    in1=whole[:, a0:a1, 0:REDUCED], op=ALU.subtract)
 
         def trig_abs(a0, a1):
             nc.scalar.activation(out=abs_frac[:, a0:a1, :], in_=frac[:, a0:a1, :], func=ACT.Abs)
@@ -244,7 +238,9 @@ def tile_attention_pa_kernel(tc, x, wq, wkv, q_norm_w, k_norm_w, out_0, out_1, o
                 nc.sync.dma_start(out=v_out[a], in_=v[:])
 
         def copy_q_gain():
-            nc.scalar.copy(out=gain_planes[:], in_=q_gain[:].rearrange("p (i r) -> p r i", r=2))
+            spread = ps_scalar.tile([P, D], F32, tag="bank", name="spread")
+            nc.tensor.matmul(out=spread[:], lhsT=ones[:], rhs=gain_rows[:, 0:D], start=True, stop=True)
+            nc.scalar.copy(out=gain_planes[:], in_=spread[:].rearrange("p (i r) -> p r i", r=2))
 
         def tb(a):
             if not ok(a):
@@ -291,7 +287,7 @@ def tile_attention_pa_kernel(tc, x, wq, wkv, q_norm_w, k_norm_w, out_0, out_1, o
         def pk(a):
             if not ok(a):
                 return
-            halves = products.tile([P, 2, D], F32, name="halves")
+            halves = k_products.tile([P, 2, D], F32, name="k_halves")
             bank = live[("v", a, KEY)]
             for e in range(2):
                 nc.vector.scalar_tensor_tensor(out=halves[:, e, :].rearrange("p (i r) -> p i r", r=2),
@@ -386,36 +382,33 @@ def tile_attention_pa_kernel(tc, x, wq, wkv, q_norm_w, k_norm_w, out_0, out_1, o
         q_w(1, 2)
         t_w(3, 0, ps_vector)
         c_w(2, 1, True)
-        t_w(3, 1, ps_scalar)
         t_w(KEY, 0, ps_turn)
         t_w(KEY, 1, ps_scalar)
         c_w(3, 0, True)
         q_w(2, 3)
-        c_w(3, 1, False)
+        t_w(3, 1, ps_vector)
+        c_w(3, 1, True)
         t_x(2, ps_turn)
         c_w(KEY, 0, False)
         t_x(4, ps_scalar)
         c_w(KEY, 1, False)
         t_x(6, ps_turn)
         c_x(2, False)
-        t_w(VALUE, 0, ps_scalar)
         c_x(4, False)
-        t_w(VALUE, 1, ps_turn)
         c_x(6, False)
-        c_w(VALUE, 0, False)
-        c_w(VALUE, 1, False)
+        spread_q_gain()
         q_w(3, 4)
         q_w(KEY, KEY + 1)
         q_x(2, 4)
+        tb(0)
         q_x(4, TILES)
-        q_w(VALUE, GROUPS)
-        spread_q_gain()
+        tb(1)
         copy_q_gain()
         for g in range(KEY + 1):
             ms(0, g)
             sq(0, g)
         rs(0)
-        for a in range(6):
+        for a in range(2, 6):
             tb(a)
         ms(1, 0)
         ms(1, 1)
@@ -425,11 +418,13 @@ def tile_attention_pa_kernel(tc, x, wq, wkv, q_norm_w, k_norm_w, out_0, out_1, o
             last = a == TILES - 1
             if last:
                 pk(a)
-                vc(a)
+                vc(a - 1)
+                ms(a, VALUE)
                 kg(a - 1)
                 mv(a, 2)
                 kb(a - 1)
                 ka(a)
+                vc(a)
             p(a, 0)
             sq(a + 1, 0)
             ms(a + 1, 2)
@@ -453,8 +448,10 @@ def tile_attention_pa_kernel(tc, x, wq, wkv, q_norm_w, k_norm_w, out_0, out_1, o
             if not last:
                 mv(a, KEY)
             sq(a + 1, 3)
-            if not last:
-                ms(a, VALUE)
+            if a == 0:
+                t_w(VALUE, 0, ps_scalar)
+            elif not last:
+                ms(a - 1, VALUE)
             p(a, 3)
             sub(a, 2)
             if a == TILES - 2:
@@ -467,7 +464,13 @@ def tile_attention_pa_kernel(tc, x, wq, wkv, q_norm_w, k_norm_w, out_0, out_1, o
                 kg(a - 1)
                 kb(a - 1)
                 pk(a)
-                vc(a)
+            if a == 0:
+                c_w(VALUE, 0, False)
+                t_w(VALUE, 1, ps_scalar)
+                c_w(VALUE, 1, False)
+                q_w(VALUE, GROUPS)
+            elif not last:
+                vc(a - 1)
             if a == TILES - 2:
                 mv(a + 1, 0)
             else:
@@ -481,7 +484,7 @@ def tile_attention_pa_kernel(tc, x, wq, wkv, q_norm_w, k_norm_w, out_0, out_1, o
             ms(a + 2, 0)
             ms(a + 2, 1)
             if a == TILES - 2:
-                ms(a + 1, VALUE)
+                ms(a, VALUE)
                 mv(a + 1, 1)
             else:
                 mv(a + 1, 2)

@@ -65,8 +65,7 @@ def tile_attention_pa_kernel(tc, x, wq, wkv, q_norm_w, k_norm_w, out_0, out_1, o
         token = keep.tile([P, TILES], F32, name="token")
         whole = keep.tile([P, TILES, PAIRS], I32, name="whole")
         frac = keep.tile([P, TILES, PAIRS], F32, name="frac")
-        abs_frac = keep.tile([P, TILES, PAIRS], F32, name="abs_frac")
-        trig = keep.tile([P, TILES, 3, PAIRS], F32, name="trig")
+        trig = keep.tile([P, TILES, 4, PAIRS], F32, name="trig")
         q_table = keep.tile([P, TILES, 2, D], F32, name="q_table")
         gain_planes = keep.tile([P, 2, PAIRS], F32, name="gain_planes")
         mean_sq = keep.tile([P, TILES + 1, 8], F32, name="mean_sq")
@@ -124,22 +123,18 @@ def tile_attention_pa_kernel(tc, x, wq, wkv, q_norm_w, k_norm_w, out_0, out_1, o
                                     in1=whole[:, a0:a1, 0:REDUCED], op=ALU.subtract)
 
         def trig_abs(a0, a1):
-            nc.scalar.activation(out=abs_frac[:, a0:a1, :], in_=frac[:, a0:a1, :], func=ACT.Abs)
+            nc.scalar.activation(out=frac[:, a0:a1, :], in_=frac[:, a0:a1, :], func=ACT.Abs)
 
         def trig_plane(a0, a1, plane):
             if plane == 0:
-                nc.scalar.activation(out=trig[:, a0:a1, 0, :], in_=abs_frac[:, a0:a1, :], func=ACT.Sin,
+                nc.scalar.activation(out=trig[:, a0:a1, 0, :], in_=frac[:, a0:a1, :], func=ACT.Sin,
                                      scale=-TWO_PI, bias=math.pi / 2)
-            elif plane == 1:
-                nc.scalar.activation(out=trig[:, a0:a1, 1, :], in_=frac[:, a0:a1, :], func=ACT.Sin, scale=TWO_PI)
             else:
-                nc.scalar.activation(out=trig[:, a0:a1, 2, :], in_=abs_frac[:, a0:a1, :], func=ACT.Sin,
-                                     scale=TWO_PI, bias=-math.pi / 2)
+                nc.scalar.activation(out=trig[:, a0:a1, 1, :], in_=frac[:, a0:a1, :], func=ACT.Sin, scale=TWO_PI)
 
-        def make_trig(a0, a1):
-            trig_abs(a0, a1)
-            for plane in range(3):
-                trig_plane(a0, a1, plane)
+        def trig_derived(a0, a1, plane):
+            nc.gpsimd.tensor_scalar(out=trig[:, a0:a1, plane, :], in0=trig[:, a0:a1, 3 - plane, :],
+                                    scalar1=2.0 * plane - 5.0, scalar2=0.0, op0=ALU.mult, op1=ALU.add)
 
         def spread_q_gain():
             nc.tensor.matmul(out=q_gain[:], lhsT=ones[:], rhs=gain_rows[:, 0:D], start=True, stop=True)
@@ -249,12 +244,12 @@ def tile_attention_pa_kernel(tc, x, wq, wkv, q_norm_w, k_norm_w, out_0, out_1, o
                 for r in range(2):
                     nc.gpsimd.tensor_tensor(out=q_table[:, a, r, :].rearrange("p (e i) -> p e i", e=2),
                                             in0=gain_planes[:, r, :].unsqueeze(1).to_broadcast([P, 2, PAIRS]),
-                                            in1=trig[:, a, r:r + 2, :], op=ALU.mult)
+                                            in1=trig[:, a, r:4:2, :], op=ALU.mult)
                 return
             for e in range(2):
                 nc.vector.tensor_tensor(out=q_table[:, a, e, :].rearrange("p (i r) -> p i r", r=2),
                                         in0=q_gain[:].rearrange("p (i r) -> p i r", r=2),
-                                        in1=trig[:, a, e:e + 2, :].rearrange("p r i -> p i r"),
+                                        in1=trig[:, a, 2 * e:2 * e + 2, :].rearrange("p r i -> p i r"),
                                         op=ALU.mult)
 
         def mv(a, g):
@@ -281,7 +276,7 @@ def tile_attention_pa_kernel(tc, x, wq, wkv, q_norm_w, k_norm_w, out_0, out_1, o
             halves = live[("h", a, h)]
             q = results.tile([P, D], F32, tag="result", name="q")
             engine = nc.vector if (a == TILES - 1 and h == HEADS - 1) else nc.gpsimd
-            engine.tensor_tensor(out=q[:], in0=halves[:, 0, :], in1=halves[:, 1, :], op=ALU.subtract)
+            engine.tensor_tensor(out=q[:], in0=halves[:, 0, :], in1=halves[:, 1, :], op=ALU.add)
             nc.sync.dma_start(out=q_out[h, a], in_=q[:])
 
         def pk(a):
@@ -289,12 +284,10 @@ def tile_attention_pa_kernel(tc, x, wq, wkv, q_norm_w, k_norm_w, out_0, out_1, o
                 return
             halves = k_products.tile([P, 2, D], F32, name="k_halves")
             bank = live[("v", a, KEY)]
-            for e in range(2):
-                nc.vector.scalar_tensor_tensor(out=halves[:, e, :].rearrange("p (i r) -> p i r", r=2),
-                                               in0=bank[:, PAIRS * e:PAIRS * (e + 1)].unsqueeze(2).to_broadcast([P, PAIRS, 2]),
-                                               scalar=1.0 - 2.0 * e,
-                                               in1=trig[:, a, e:e + 2, :].rearrange("p r i -> p i r"),
-                                               op0=ALU.mult, op1=ALU.mult)
+            nc.vector.tensor_tensor(out=halves[:].rearrange("p e (i r) -> p e i r", r=2),
+                                    in0=bank[:].rearrange("p (e i) -> p e i", e=2).unsqueeze(3).to_broadcast([P, 2, PAIRS, 2]),
+                                    in1=trig[:, a, :, :].rearrange("p (e r) i -> p e i r", e=2),
+                                    op=ALU.mult)
             live[("h", a, KEY)] = halves
 
         def ka(a):
@@ -363,11 +356,21 @@ def tile_attention_pa_kernel(tc, x, wq, wkv, q_norm_w, k_norm_w, out_0, out_1, o
         t_w(0, 1, ps_vector)
         c_x(0, True)
         angles_frac(4, TILES)
-        for a0, a1 in ((0, 2), (2, 4), (4, TILES)):
-            trig_abs(a0, a1)
-            trig_plane(a0, a1, 1)
-            trig_plane(a0, a1, 0)
-            trig_plane(a0, a1, 2)
+        trig_plane(0, 2, 1)
+        trig_abs(0, 2)
+        trig_plane(2, 4, 1)
+        trig_abs(2, 4)
+        trig_plane(0, 2, 0)
+        trig_plane(4, TILES, 1)
+        trig_abs(4, TILES)
+        trig_plane(2, 4, 0)
+        trig_plane(4, TILES, 0)
+        trig_derived(0, 2, 2)
+        trig_derived(2, 4, 2)
+        trig_derived(0, 2, 3)
+        trig_derived(4, TILES, 2)
+        trig_derived(2, 4, 3)
+        trig_derived(4, TILES, 3)
         c_w(0, 0, True)
         q_x(0, 2)
         t_w(1, 0, ps_vector)

@@ -442,6 +442,8 @@ def tile_attention_pa_kernel(tc, x, wq, wkv, q_norm_w, k_norm_w, out_0, out_1, o
                 mv(a, 3)
             sq(a + 1, 1)
             ms(a + 1, 3)
+            if not last:
+                kf(a - 2)
             sq(a + 1, 2)
             ms(a + 1, KEY)
             if last:
@@ -465,7 +467,8 @@ def tile_attention_pa_kernel(tc, x, wq, wkv, q_norm_w, k_norm_w, out_0, out_1, o
             rs(a + 1)
             if not last:
                 kg(a - 1)
-                kb(a - 1)
+                if a == TILES - 2:
+                    kb(a - 1)
                 pk(a)
             if a == 0:
                 c_w(VALUE, 0, False)
@@ -478,7 +481,7 @@ def tile_attention_pa_kernel(tc, x, wq, wkv, q_norm_w, k_norm_w, out_0, out_1, o
                 mv(a + 1, 0)
             else:
                 mv(a + 1, 1)
-            if not last:
+            if a == TILES - 2:
                 kf(a - 1)
             if a == 0:
                 spread_k_gain_1()
@@ -492,6 +495,8 @@ def tile_attention_pa_kernel(tc, x, wq, wkv, q_norm_w, k_norm_w, out_0, out_1, o
             else:
                 mv(a + 1, 2)
             if not last:
+                if a < TILES - 2:
+                    kb(a - 1)
                 ka(a)
             if a in (1, 3):
                 tb(6 + a // 2)

@@ -42,8 +42,7 @@ def tile_attention_pa_kernel(tc, x, wq, wkv, q_norm_w, k_norm_w, out_0, out_1, o
         turned_k = ctx.enter_context(tc.tile_pool(name="turned_k", bufs=2))
         ps_turn = ctx.enter_context(tc.psum_pool(name="ps_turn", bufs=2))
         k_products = ctx.enter_context(tc.tile_pool(name="k_products", bufs=3))
-        ps_gain = ctx.enter_context(tc.psum_pool(name="ps_gain", bufs=1))
-        ps_scalar = ctx.enter_context(tc.psum_pool(name="ps_scalar", bufs=2))
+        ps_scalar = ctx.enter_context(tc.psum_pool(name="ps_scalar", bufs=3))
         ps_vector = ctx.enter_context(tc.psum_pool(name="ps_vector", bufs=3))
 
         ident = keep.tile([P, P], F32, name="ident")
@@ -88,7 +87,6 @@ def tile_attention_pa_kernel(tc, x, wq, wkv, q_norm_w, k_norm_w, out_0, out_1, o
         v_out = out_2.rearrange("o (p a) d -> (o a) p d", a=TILES)
         x_words = x_grouped[:].bitcast(F32).rearrange("p (c r u) -> p c r u", r=P, u=2)
         w_words = w_grouped[:].bitcast(F32).rearrange("p (c r u) -> p c r u", r=P, u=2)
-        q_gain = ps_gain.tile([P, D], F32, name="q_gain")
 
         def load_x(a):
             nc.sync.dma_start(out=x_rows[:, a:a + 2, :], in_=x_view[:, a:a + 2, :])
@@ -137,7 +135,9 @@ def tile_attention_pa_kernel(tc, x, wq, wkv, q_norm_w, k_norm_w, out_0, out_1, o
                                     scalar1=2.0 * plane - 5.0, scalar2=0.0, op0=ALU.mult, op1=ALU.add)
 
         def spread_q_gain():
+            q_gain = ps_scalar.tile([P, D], F32, tag="bank", name="q_gain")
             nc.tensor.matmul(out=q_gain[:], lhsT=ones[:], rhs=gain_rows[:, 0:D], start=True, stop=True)
+            live["q_gain"] = q_gain
 
         def spread_k_gain_1():
             spread = ps_scalar.tile([P, D], F32, tag="bank", name="spread")
@@ -248,7 +248,7 @@ def tile_attention_pa_kernel(tc, x, wq, wkv, q_norm_w, k_norm_w, out_0, out_1, o
                 return
             for e in range(2):
                 nc.vector.tensor_tensor(out=q_table[:, a, e, :].rearrange("p (i r) -> p i r", r=2),
-                                        in0=q_gain[:].rearrange("p (i r) -> p i r", r=2),
+                                        in0=live["q_gain"][:].rearrange("p (i r) -> p i r", r=2),
                                         in1=trig[:, a, 2 * e:2 * e + 2, :].rearrange("p r i -> p i r"),
                                         op=ALU.mult)
 

@@ -139,10 +139,13 @@ def tile_attention_pa_kernel(tc, x, wq, wkv, q_norm_w, k_norm_w, out_0, out_1, o
             nc.tensor.matmul(out=q_gain[:], lhsT=ones[:], rhs=gain_rows[:, 0:D], start=True, stop=True)
             live["q_gain"] = q_gain
 
-        def spread_k_gain_1():
+        def spread_k_gain_1a():
             spread = ps_scalar.tile([P, D], F32, tag="bank", name="spread")
             nc.tensor.matmul(out=spread[:], lhsT=ones[:], rhs=gain_rows[:, D:2 * D], start=True, stop=True)
-            nc.scalar.copy(out=k_gain[:], in_=spread[:])
+            live["k_gain"] = spread
+
+        def spread_k_gain_1b():
+            nc.scalar.copy(out=k_gain[:], in_=live["k_gain"][:])
 
         def spread_k_gain_2():
             turned = ps_turn.tile([P, D // P, P], F32, tag="bank", name="turned")
@@ -202,9 +205,9 @@ def tile_attention_pa_kernel(tc, x, wq, wkv, q_norm_w, k_norm_w, out_0, out_1, o
         def ok(a):
             return 0 <= a < TILES
 
-        def ms(a, g):
+        def ms(a, g, pool=ps_scalar):
             if ok(a):
-                bank = ps_scalar.tile([P, D], F32, tag="bank", name="bank")
+                bank = pool.tile([P, D], F32, tag="bank", name="bank")
                 project(bank, a, g)
                 live[("s", a, g)] = bank
 
@@ -407,16 +410,24 @@ def tile_attention_pa_kernel(tc, x, wq, wkv, q_norm_w, k_norm_w, out_0, out_1, o
         q_x(4, TILES)
         tb(1)
         copy_q_gain()
-        for g in range(KEY + 1):
-            ms(0, g)
-            sq(0, g)
+        ms(0, 0)
+        ms(0, 1, ps_turn)
+        ms(0, 2, ps_turn)
+        ms(0, 3)
+        sq(0, 0)
+        ms(0, KEY)
+        for h in range(3):
+            mv(0, h)
+        sq(0, 1)
+        sq(0, 2)
+        sq(0, 3)
+        ms(1, 0)
+        sq(0, KEY)
+        ms(1, 1)
         rs(0)
         for a in range(2, 6):
             tb(a)
-        ms(1, 0)
-        ms(1, 1)
-        for h in range(3):
-            mv(0, h)
+        ms(1, 2)
         for a in range(TILES):
             last = a == TILES - 1
             if last:
@@ -430,7 +441,7 @@ def tile_attention_pa_kernel(tc, x, wq, wkv, q_norm_w, k_norm_w, out_0, out_1, o
                 vc(a)
             p(a, 0)
             sq(a + 1, 0)
-            ms(a + 1, 2)
+            ms(a + 1, 3)
             if last:
                 mv(a, 3)
                 kf(a - 1)
@@ -438,14 +449,14 @@ def tile_attention_pa_kernel(tc, x, wq, wkv, q_norm_w, k_norm_w, out_0, out_1, o
                 kb(a)
             p(a, 1)
             sub(a, 0)
+            sq(a + 1, 1)
+            ms(a + 1, KEY)
             if not last:
                 mv(a, 3)
-            sq(a + 1, 1)
-            ms(a + 1, 3)
-            if not last:
                 kf(a - 2)
             sq(a + 1, 2)
-            ms(a + 1, KEY)
+            if 0 < a < TILES - 1:
+                ms(a - 1, VALUE)
             if last:
                 kf(a)
             p(a, 2)
@@ -455,16 +466,21 @@ def tile_attention_pa_kernel(tc, x, wq, wkv, q_norm_w, k_norm_w, out_0, out_1, o
             sq(a + 1, 3)
             if a == 0:
                 t_w(VALUE, 0, ps_scalar)
-            elif not last:
-                ms(a - 1, VALUE)
+                t_w(VALUE, 1, ps_scalar)
+            else:
+                ms(a + 2, 0)
             p(a, 3)
             sub(a, 2)
+            sq(a + 1, KEY)
+            if a == 0:
+                spread_k_gain_1a()
+            else:
+                ms(a + 2, 1)
+            rs(a + 1)
             if a == TILES - 2:
                 mv(a + 1, KEY)
             else:
                 mv(a + 1, 0)
-            sq(a + 1, KEY)
-            rs(a + 1)
             if not last:
                 kg(a - 1)
                 if a == TILES - 2:
@@ -472,28 +488,28 @@ def tile_attention_pa_kernel(tc, x, wq, wkv, q_norm_w, k_norm_w, out_0, out_1, o
                 pk(a)
             if a == 0:
                 c_w(VALUE, 0, False)
-                t_w(VALUE, 1, ps_scalar)
+                ms(2, 0)
                 c_w(VALUE, 1, False)
+                ms(2, 1)
                 q_w(VALUE, GROUPS)
+                spread_k_gain_1b()
             elif not last:
                 vc(a - 1)
+            ms(a + 2, 2)
             if a == TILES - 2:
                 mv(a + 1, 0)
             else:
                 mv(a + 1, 1)
             if a == TILES - 2:
                 kf(a - 1)
-            if a == 0:
-                spread_k_gain_1()
-                spread_k_gain_2()
             sub(a, 3)
-            ms(a + 2, 0)
-            ms(a + 2, 1)
             if a == TILES - 2:
                 ms(a, VALUE)
                 mv(a + 1, 1)
             else:
                 mv(a + 1, 2)
+            if a == 0:
+                spread_k_gain_2()
             if not last:
                 if a < TILES - 2:
                     kb(a - 1)

@@ -121,7 +121,7 @@ def tile_attention_pa_kernel(tc, x, wq, wkv, q_norm_w, k_norm_w, out_0, out_1, o
                                     in1=whole[:, a0:a1, 0:REDUCED], op=ALU.subtract)
 
         def trig_abs(a0, a1):
-            nc.scalar.activation(out=frac[:, a0:a1, :], in_=frac[:, a0:a1, :], func=ACT.Abs)
+            nc.scalar.activation(out=frac[:, a0:a1, 0:REDUCED], in_=frac[:, a0:a1, 0:REDUCED], func=ACT.Abs)
 
         def trig_plane(a0, a1, plane):
             if plane == 0:
@@ -223,9 +223,9 @@ def tile_attention_pa_kernel(tc, x, wq, wkv, q_norm_w, k_norm_w, out_0, out_1, o
             nc.gpsimd.tensor_tensor(out=rstd[:, column_group, g0:g1], in0=mean_eps[:, column_group, g0:g1],
                                     in1=minus_half[:, g0:g1], op=ALU.pow)
 
-        def rs(a):
+        def rs(a, g0=0, g1=KEY + 1):
             if ok(a):
-                nc.scalar.activation(out=rstd[:, a, 0:KEY + 1], in_=mean_sq[:, a, 0:KEY + 1],
+                nc.scalar.activation(out=rstd[:, a, g0:g1], in_=mean_sq[:, a, g0:g1],
                                      func=ACT.Abs_reciprocal_sqrt, bias=EPS)
 
         def vc(a):
@@ -249,11 +249,11 @@ def tile_attention_pa_kernel(tc, x, wq, wkv, q_norm_w, k_norm_w, out_0, out_1, o
                                             in0=gain_planes[:, r, :].unsqueeze(1).to_broadcast([P, 2, PAIRS]),
                                             in1=trig[:, a, r:4:2, :], op=ALU.mult)
                 return
-            for e in range(2):
-                nc.vector.tensor_tensor(out=q_table[:, a, e, :].rearrange("p (i r) -> p i r", r=2),
-                                        in0=live["q_gain"][:].rearrange("p (i r) -> p i r", r=2),
-                                        in1=trig[:, a, 2 * e:2 * e + 2, :].rearrange("p r i -> p i r"),
-                                        op=ALU.mult)
+            nc.vector.tensor_tensor(out=q_table[:, a, :, :].rearrange("p e (i r) -> p e i r", r=2),
+                                    in0=live["q_gain"][:].rearrange("p (i r) -> p i r", r=2).unsqueeze(1)
+                                    .to_broadcast([P, 2, PAIRS, 2]),
+                                    in1=trig[:, a, :, :].rearrange("p (e r) i -> p e i r", e=2),
+                                    op=ALU.mult)
 
         def mv(a, g):
             if ok(a):
@@ -403,8 +403,7 @@ def tile_attention_pa_kernel(tc, x, wq, wkv, q_norm_w, k_norm_w, out_0, out_1, o
         c_x(4, False)
         c_x(6, False)
         spread_q_gain()
-        q_w(3, 4)
-        q_w(KEY, KEY + 1)
+        q_w(3, KEY + 1)
         q_x(2, 4)
         tb(0)
         q_x(4, TILES)
@@ -422,9 +421,10 @@ def tile_attention_pa_kernel(tc, x, wq, wkv, q_norm_w, k_norm_w, out_0, out_1, o
         sq(0, 2)
         sq(0, 3)
         ms(1, 0)
+        rs(0, 0, KEY)
         sq(0, KEY)
         ms(1, 1)
-        rs(0)
+        rs(0, KEY, KEY + 1)
         for a in range(2, 6):
             tb(a)
         ms(1, 2)

@@ -379,30 +379,30 @@ def tile_attention_pa_kernel(tc, x, wq, wkv, q_norm_w, k_norm_w, out_0, out_1, o
         t_w(1, 0, ps_vector)
         c_w(0, 1, True)
         t_w(1, 1, ps_vector)
+        t_w(3, 0, ps_scalar)
         c_w(1, 0, True)
         q_w(0, 1)
         t_w(2, 0, ps_vector)
+        t_w(3, 1, ps_turn)
         c_w(1, 1, True)
         t_w(2, 1, ps_vector)
+        t_w(KEY, 0, ps_scalar)
+        t_w(KEY, 1, ps_turn)
+        t_x(2, ps_scalar)
         c_w(2, 0, True)
-        q_w(1, 2)
-        t_w(3, 0, ps_vector)
         c_w(2, 1, True)
-        t_w(KEY, 0, ps_turn)
-        t_w(KEY, 1, ps_scalar)
-        c_w(3, 0, True)
+        q_w(1, 2)
         q_w(2, 3)
-        t_w(3, 1, ps_vector)
-        c_w(3, 1, True)
-        t_x(2, ps_turn)
-        c_w(KEY, 0, False)
+        c_w(3, 0, False)
         t_x(4, ps_scalar)
-        c_w(KEY, 1, False)
+        c_w(3, 1, False)
         t_x(6, ps_turn)
+        c_w(KEY, 0, False)
+        spread_q_gain()
+        c_w(KEY, 1, False)
         c_x(2, False)
         c_x(4, False)
         c_x(6, False)
-        spread_q_gain()
         q_w(3, KEY + 1)
         q_x(2, 4)
         tb(0)

@@ -340,8 +340,8 @@ def tile_attention_pa_kernel(tc, x, wq, wkv, q_norm_w, k_norm_w, out_0, out_1, o
         for g in range(HEADS):
             load_w(g)
         load_w(KEY)
-        nc.sync.dma_start(out=gain_rows[0:1, 0:D], in_=q_norm_w.rearrange("(o d) -> o d", o=1))
-        nc.sync.dma_start(out=gain_rows[0:1, D:2 * D], in_=k_norm_w.rearrange("(o d) -> o d", o=1))
+        nc.scalar.dma_start(out=gain_rows[0:1, 0:D], in_=q_norm_w.rearrange("(o d) -> o d", o=1))
+        nc.scalar.dma_start(out=gain_rows[0:1, D:2 * D], in_=k_norm_w.rearrange("(o d) -> o d", o=1))
         for a in range(2, TILES, 2):
             load_x(a)
         load_w(VALUE)

@@ -235,10 +235,13 @@ def tile_attention_pa_kernel(tc, x, wq, wkv, q_norm_w, k_norm_w, out_0, out_1, o
                                in_=live[("s", a, VALUE)][:].rearrange("p (j q) -> p q j", j=4))
                 nc.sync.dma_start(out=v_out[a], in_=v[:])
 
-        def copy_q_gain():
+        def spread_q_gain_again():
             spread = ps_scalar.tile([P, D], F32, tag="bank", name="spread")
             nc.tensor.matmul(out=spread[:], lhsT=ones[:], rhs=gain_rows[:, 0:D], start=True, stop=True)
-            nc.scalar.copy(out=gain_planes[:], in_=spread[:].rearrange("p (i r) -> p r i", r=2))
+            live["gain"] = spread
+
+        def copy_q_gain():
+            nc.scalar.copy(out=gain_planes[:], in_=live["gain"][:].rearrange("p (i r) -> p r i", r=2))
 
         def tb(a):
             if not ok(a):
@@ -379,6 +382,8 @@ def tile_attention_pa_kernel(tc, x, wq, wkv, q_norm_w, k_norm_w, out_0, out_1, o
         t_w(1, 0, ps_vector)
         c_w(0, 1, True)
         t_w(1, 1, ps_vector)
+        spread_q_gain()
+        spread_q_gain_again()
         t_w(3, 0, ps_scalar)
         c_w(1, 0, True)
         q_w(0, 1)
@@ -386,29 +391,31 @@ def tile_attention_pa_kernel(tc, x, wq, wkv, q_norm_w, k_norm_w, out_0, out_1, o
         t_w(3, 1, ps_turn)
         c_w(1, 1, True)
         t_w(2, 1, ps_vector)
-        t_w(KEY, 0, ps_scalar)
-        t_w(KEY, 1, ps_turn)
-        t_x(2, ps_scalar)
+        t_w(KEY, 0, ps_turn)
         c_w(2, 0, True)
         c_w(2, 1, True)
         q_w(1, 2)
         q_w(2, 3)
+        copy_q_gain()
+        t_w(KEY, 1, ps_scalar)
         c_w(3, 0, False)
-        t_x(4, ps_scalar)
+        t_x(2, ps_scalar)
         c_w(3, 1, False)
-        t_x(6, ps_turn)
+        t_x(4, ps_turn)
         c_w(KEY, 0, False)
-        spread_q_gain()
+        t_x(6, ps_turn)
         c_w(KEY, 1, False)
         c_x(2, False)
         c_x(4, False)
         c_x(6, False)
+        tb(0)
         q_w(3, KEY + 1)
         q_x(2, 4)
-        tb(0)
-        q_x(4, TILES)
         tb(1)
-        copy_q_gain()
+        q_x(4, TILES)
+        tb(4)
+        tb(5)
+        tb(6)
         ms(0, 0)
         ms(0, 1, ps_turn)
         ms(0, 2, ps_turn)
@@ -425,8 +432,8 @@ def tile_attention_pa_kernel(tc, x, wq, wkv, q_norm_w, k_norm_w, out_0, out_1, o
         sq(0, KEY)
         ms(1, 1)
         rs(0, KEY, KEY + 1)
-        for a in range(2, 6):
-            tb(a)
+        tb(2)
+        tb(3)
         ms(1, 2)
         for a in range(TILES):
             last = a == TILES - 1
@@ -514,5 +521,5 @@ def tile_attention_pa_kernel(tc, x, wq, wkv, q_norm_w, k_norm_w, out_0, out_1, o
                 if a < TILES - 2:
                     kb(a - 1)
                 ka(a)
-            if a in (1, 3):
-                tb(6 + a // 2)
+            if a == 2:
+                tb(7)

@@ -131,8 +131,11 @@ def tile_attention_pa_kernel(tc, x, wq, wkv, q_norm_w, k_norm_w, out_0, out_1, o
                 nc.scalar.activation(out=trig[:, a0:a1, 1, :], in_=frac[:, a0:a1, :], func=ACT.Sin, scale=TWO_PI)
 
         def trig_derived(a0, a1, plane):
-            nc.gpsimd.tensor_scalar(out=trig[:, a0:a1, plane, :], in0=trig[:, a0:a1, 3 - plane, :],
-                                    scalar1=2.0 * plane - 5.0, scalar2=0.0, op0=ALU.mult, op1=ALU.add)
+            if plane == 3:
+                nc.sync.dma_start(out=trig[:, a0:a1, 3, :], in_=trig[:, a0:a1, 0, :])
+                return
+            nc.gpsimd.tensor_scalar(out=trig[:, a0:a1, 2, :], in0=trig[:, a0:a1, 1, :],
+                                    scalar1=-1.0, scalar2=0.0, op0=ALU.mult, op1=ALU.add)
 
         def spread_q_gain():
             q_gain = ps_scalar.tile([P, D], F32, tag="bank", name="q_gain")

@@ -246,14 +246,17 @@ def tile_attention_pa_kernel(tc, x, wq, wkv, q_norm_w, k_norm_w, out_0, out_1, o
         def copy_q_gain():
             nc.scalar.copy(out=gain_planes[:], in_=live["gain"][:].rearrange("p (i r) -> p r i", r=2))
 
+        def tbh(a, r):
+            nc.gpsimd.tensor_tensor(out=q_table[:, a, r, :].rearrange("p (e i) -> p e i", e=2),
+                                    in0=gain_planes[:, r, :].unsqueeze(1).to_broadcast([P, 2, PAIRS]),
+                                    in1=trig[:, a, r:4:2, :], op=ALU.mult)
+
         def tb(a):
             if not ok(a):
                 return
             if a in GPSIMD_TABLES:
                 for r in range(2):
-                    nc.gpsimd.tensor_tensor(out=q_table[:, a, r, :].rearrange("p (e i) -> p e i", e=2),
-                                            in0=gain_planes[:, r, :].unsqueeze(1).to_broadcast([P, 2, PAIRS]),
-                                            in1=trig[:, a, r:4:2, :], op=ALU.mult)
+                    tbh(a, r)
                 return
             nc.vector.tensor_tensor(out=q_table[:, a, :, :].rearrange("p e (i r) -> p e i r", r=2),
                                     in0=live["q_gain"][:].rearrange("p (i r) -> p i r", r=2).unsqueeze(1)
@@ -379,14 +382,13 @@ def tile_attention_pa_kernel(tc, x, wq, wkv, q_norm_w, k_norm_w, out_0, out_1, o
         trig_derived(0, 2, 3)
         trig_derived(4, TILES, 2)
         trig_derived(2, 4, 3)
-        trig_derived(4, TILES, 3)
+        for a in range(4, TILES):
+            trig_derived(a, a + 1, 3)
         c_w(0, 0, True)
         q_x(0, 2)
         t_w(1, 0, ps_vector)
         c_w(0, 1, True)
         t_w(1, 1, ps_vector)
-        spread_q_gain()
-        spread_q_gain_again()
         t_w(3, 0, ps_scalar)
         c_w(1, 0, True)
         q_w(0, 1)
@@ -394,6 +396,8 @@ def tile_attention_pa_kernel(tc, x, wq, wkv, q_norm_w, k_norm_w, out_0, out_1, o
         t_w(3, 1, ps_turn)
         c_w(1, 1, True)
         t_w(2, 1, ps_vector)
+        spread_q_gain_again()
+        spread_q_gain()
         t_w(KEY, 0, ps_turn)
         c_w(2, 0, True)
         c_w(2, 1, True)
@@ -416,9 +420,9 @@ def tile_attention_pa_kernel(tc, x, wq, wkv, q_norm_w, k_norm_w, out_0, out_1, o
         q_x(2, 4)
         tb(1)
         q_x(4, TILES)
-        tb(4)
-        tb(5)
-        tb(6)
+        for r in range(2):
+            for a in (4, 5, 6):
+                tbh(a, r)
         ms(0, 0)
         ms(0, 1, ps_turn)
         ms(0, 2, ps_turn)

@@ -46,8 +46,9 @@ def tile_attention_pa_kernel(tc, x, wq, wkv, q_norm_w, k_norm_w, out_0, out_1, o
         ps_vector = ctx.enter_context(tc.psum_pool(name="ps_vector", bufs=3))
 
         ident = keep.tile([P, P], F32, name="ident")
-        ones = keep.tile([P, P], BF16, name="ones")
-        gain_rows = keep.tile([P, 2 * D], BF16, name="gain_rows")
+        ident_bf = keep.tile([P, P], BF16, name="ident_bf")
+        q_gain_cols = keep.tile([P, 4], BF16, name="q_gain_cols")
+        k_gain_cols = keep.tile([P, 4], BF16, name="k_gain_cols")
         k_gain = keep.tile([P, D], F32, name="k_gain")
         k_gain_col = keep.tile([P, D // P], F32, name="k_gain_col")
         x_rows = keep.tile([P, TILES, D], BF16, name="x_rows")
@@ -137,15 +138,20 @@ def tile_attention_pa_kernel(tc, x, wq, wkv, q_norm_w, k_norm_w, out_0, out_1, o
             nc.gpsimd.tensor_scalar(out=trig[:, a0:a1, 2, :], in0=trig[:, a0:a1, 1, :],
                                     scalar1=-1.0, scalar2=0.0, op0=ALU.mult, op1=ALU.add)
 
+        def spread(bank, cols):
+            for c in range(4):
+                nc.tensor.matmul(out=bank[:, c:D:4], lhsT=cols[:, c:c + 1].to_broadcast([P, P]), rhs=ident_bf[:],
+                                 start=True, stop=True)
+
         def spread_q_gain():
             q_gain = ps_scalar.tile([P, D], F32, tag="bank", name="q_gain")
-            nc.tensor.matmul(out=q_gain[:], lhsT=ones[:], rhs=gain_rows[:, 0:D], start=True, stop=True)
+            spread(q_gain, q_gain_cols)
             live["q_gain"] = q_gain
 
         def spread_k_gain_1a():
-            spread = ps_scalar.tile([P, D], F32, tag="bank", name="spread")
-            nc.tensor.matmul(out=spread[:], lhsT=ones[:], rhs=gain_rows[:, D:2 * D], start=True, stop=True)
-            live["k_gain"] = spread
+            bank = ps_scalar.tile([P, D], F32, tag="bank", name="spread")
+            spread(bank, k_gain_cols)
+            live["k_gain"] = bank
 
         def spread_k_gain_1b():
             nc.scalar.copy(out=k_gain[:], in_=live["k_gain"][:])
@@ -239,9 +245,9 @@ def tile_attention_pa_kernel(tc, x, wq, wkv, q_norm_w, k_norm_w, out_0, out_1, o
                 nc.sync.dma_start(out=v_out[a], in_=v[:])
 
         def spread_q_gain_again():
-            spread = ps_scalar.tile([P, D], F32, tag="bank", name="spread")
-            nc.tensor.matmul(out=spread[:], lhsT=ones[:], rhs=gain_rows[:, 0:D], start=True, stop=True)
-            live["gain"] = spread
+            bank = ps_scalar.tile([P, D], F32, tag="bank", name="spread")
+            spread(bank, q_gain_cols)
+            live["gain"] = bank
 
         def copy_q_gain():
             nc.scalar.copy(out=gain_planes[:], in_=live["gain"][:].rearrange("p (i r) -> p r i", r=2))
@@ -339,18 +345,17 @@ def tile_attention_pa_kernel(tc, x, wq, wkv, q_norm_w, k_norm_w, out_0, out_1, o
             nc.sync.dma_start(out=k_out[a], in_=k[:])
 
         nc.vector.memset(one[:], 1.0)
+        nc.scalar.dma_start(out=q_gain_cols[:], in_=q_norm_w.rearrange("(p c) -> p c", c=4))
+        nc.scalar.dma_start(out=k_gain_cols[:], in_=k_norm_w.rearrange("(p c) -> p c", c=4))
         nc.scalar.activation(out=warm[:], in_=one[:], func=ACT.Sin)
-        nc.gpsimd.memset(gain_rows[:], 0.0)
         nc.gpsimd.iota(token[:], pattern=[[1, TILES]], base=0, channel_multiplier=TILES,
                        allow_small_or_imprecise_dtypes=True)
         make_identity(nc, ident[:])
-        nc.gpsimd.memset(ones[:], 1.0)
+        make_identity(nc, ident_bf[:])
         load_x(0)
         for g in range(HEADS):
             load_w(g)
         load_w(KEY)
-        nc.scalar.dma_start(out=gain_rows[0:1, 0:D], in_=q_norm_w.rearrange("(o d) -> o d", o=1))
-        nc.scalar.dma_start(out=gain_rows[0:1, D:2 * D], in_=k_norm_w.rearrange("(o d) -> o d", o=1))
         for a in range(2, TILES, 2):
             load_x(a)
         load_w(VALUE)

@@ -369,6 +369,8 @@ def tile_attention_pa_kernel(tc, x, wq, wkv, q_norm_w, k_norm_w, out_0, out_1, o
         angles_frac(2, 4)
         angles_whole(4, TILES)
         t_x(0, ps_vector)
+        spread_q_gain_again()
+        spread_q_gain()
         t_w(0, 0, ps_vector)
         t_w(0, 1, ps_vector)
         c_x(0, True)
@@ -401,8 +403,6 @@ def tile_attention_pa_kernel(tc, x, wq, wkv, q_norm_w, k_norm_w, out_0, out_1, o
         t_w(3, 1, ps_turn)
         c_w(1, 1, True)
         t_w(2, 1, ps_vector)
-        spread_q_gain_again()
-        spread_q_gain()
         t_w(KEY, 0, ps_turn)
         c_w(2, 0, True)
         c_w(2, 1, True)

@@ -110,6 +110,15 @@ def tile_attention_pa_kernel(tc, x, wq, wkv, q_norm_w, k_norm_w, out_0, out_1, o
                                                 scalar1=STEP ** (m * width))
                 width *= 4
 
+        def seed_angles():
+            for i in range(4):
+                nc.vector.tensor_scalar_mul(out=frac[:, :, i:i + 1], in0=token[:].unsqueeze(2), scalar1=STEP ** i / TWO_PI)
+
+        def widen_angles(a0, a1, width, blocks):
+            for m in blocks:
+                nc.vector.tensor_scalar_mul(out=frac[:, a0:a1, m * width:(m + 1) * width], in0=frac[:, a0:a1, 0:width],
+                                            scalar1=STEP ** (m * width))
+
         def angles_mul(a0, a1):
             for a in range(a0, a1):
                 nc.vector.tensor_scalar_mul(out=frac[:, a, :], in0=turns[:], scalar1=token[:, a:a + 1])
@@ -124,12 +133,12 @@ def tile_attention_pa_kernel(tc, x, wq, wkv, q_norm_w, k_norm_w, out_0, out_1, o
         def trig_abs(a0, a1):
             nc.scalar.activation(out=frac[:, a0:a1, 0:REDUCED], in_=frac[:, a0:a1, 0:REDUCED], func=ACT.Abs)
 
-        def trig_plane(a0, a1, plane):
+        def trig_plane(a0, a1, plane, c0=0, c1=REDUCED):
             if plane == 0:
-                nc.scalar.activation(out=trig[:, a0:a1, 0, :], in_=frac[:, a0:a1, :], func=ACT.Sin,
+                nc.scalar.activation(out=trig[:, a0:a1, 0, c0:c1], in_=frac[:, a0:a1, c0:c1], func=ACT.Sin,
                                      scale=-TWO_PI, bias=math.pi / 2)
             else:
-                nc.scalar.activation(out=trig[:, a0:a1, 1, :], in_=frac[:, a0:a1, :], func=ACT.Sin, scale=TWO_PI)
+                nc.scalar.activation(out=trig[:, a0:a1, 1, c0:c1], in_=frac[:, a0:a1, c0:c1], func=ACT.Sin, scale=TWO_PI)
 
         def trig_derived(a0, a1, plane):
             if plane == 3:
@@ -344,12 +353,11 @@ def tile_attention_pa_kernel(tc, x, wq, wkv, q_norm_w, k_norm_w, out_0, out_1, o
                                  scale=rstd[:, a, KEY:KEY + 1])
             nc.sync.dma_start(out=k_out[a], in_=k[:])
 
-        nc.vector.memset(one[:], 1.0)
-        nc.scalar.dma_start(out=q_gain_cols[:], in_=q_norm_w.rearrange("(p c) -> p c", c=4))
-        nc.scalar.dma_start(out=k_gain_cols[:], in_=k_norm_w.rearrange("(p c) -> p c", c=4))
-        nc.scalar.activation(out=warm[:], in_=one[:], func=ACT.Sin)
         nc.gpsimd.iota(token[:], pattern=[[1, TILES]], base=0, channel_multiplier=TILES,
                        allow_small_or_imprecise_dtypes=True)
+        nc.sync.dma_start(out=q_gain_cols[:], in_=q_norm_w.rearrange("(p c) -> p c", c=4))
+        nc.sync.dma_start(out=k_gain_cols[:], in_=k_norm_w.rearrange("(p c) -> p c", c=4))
+        nc.scalar.activation(out=warm[:], in_=token[:, 0:1], func=ACT.Sin, scale=0.0)
         make_identity(nc, ident[:])
         make_identity(nc, ident_bf[:])
         load_x(0)
@@ -359,22 +367,28 @@ def tile_attention_pa_kernel(tc, x, wq, wkv, q_norm_w, k_norm_w, out_0, out_1, o
         for a in range(2, TILES, 2):
             load_x(a)
         load_w(VALUE)
-        make_turns()
-        angles_mul(0, 4)
+        seed_angles()
+        widen_angles(0, TILES, 4, (1, 2, 3))
+        widen_angles(0, TILES, 16, (1, 2, 3))
+        widen_angles(0, TILES, 64, (2, 3))
+        trig_plane(0, TILES, 1, REDUCED, PAIRS)
+        trig_plane(0, TILES, 0, REDUCED, PAIRS)
+        widen_angles(0, 4, 64, (1,))
+        widen_angles(4, TILES, 64, (1,))
         angles_whole(0, 2)
-        angles_mul(4, 6)
-        angles_frac(0, 2)
         angles_whole(2, 4)
-        angles_mul(6, TILES)
+        angles_frac(0, 2)
         angles_frac(2, 4)
-        angles_whole(4, TILES)
+        angles_whole(4, 6)
+        angles_whole(6, TILES)
+        angles_frac(4, 6)
+        angles_frac(6, TILES)
         t_x(0, ps_vector)
         spread_q_gain_again()
         spread_q_gain()
         t_w(0, 0, ps_vector)
         t_w(0, 1, ps_vector)
         c_x(0, True)
-        angles_frac(4, TILES)
         trig_plane(0, 2, 1)
         trig_abs(0, 2)
         trig_plane(2, 4, 1)

@@ -42,8 +42,8 @@ def tile_attention_pa_kernel(tc, x, wq, wkv, q_norm_w, k_norm_w, out_0, out_1, o
         turned_k = ctx.enter_context(tc.tile_pool(name="turned_k", bufs=2))
         ps_turn = ctx.enter_context(tc.psum_pool(name="ps_turn", bufs=2))
         k_products = ctx.enter_context(tc.tile_pool(name="k_products", bufs=3))
-        ps_scalar = ctx.enter_context(tc.psum_pool(name="ps_scalar", bufs=3))
-        ps_vector = ctx.enter_context(tc.psum_pool(name="ps_vector", bufs=3))
+        ps_rope = ctx.enter_context(tc.psum_pool(name="ps_rope", bufs=5))
+        ps_misc = ctx.enter_context(tc.psum_pool(name="ps_misc", bufs=1))
 
         ident = keep.tile([P, P], F32, name="ident")
         ident_bf = keep.tile([P, P], BF16, name="ident_bf")
@@ -153,12 +153,12 @@ def tile_attention_pa_kernel(tc, x, wq, wkv, q_norm_w, k_norm_w, out_0, out_1, o
                                  start=True, stop=True)
 
         def spread_q_gain():
-            q_gain = ps_scalar.tile([P, D], F32, tag="bank", name="q_gain")
+            q_gain = ps_misc.tile([P, D], F32, tag="bank", name="q_gain")
             spread(q_gain, q_gain_cols)
             live["q_gain"] = q_gain
 
         def spread_k_gain_1a():
-            bank = ps_scalar.tile([P, D], F32, tag="bank", name="spread")
+            bank = ps_turn.tile([P, D], F32, tag="bank", name="spread")
             spread(bank, k_gain_cols)
             live["k_gain"] = bank
 
@@ -223,16 +223,16 @@ def tile_attention_pa_kernel(tc, x, wq, wkv, q_norm_w, k_norm_w, out_0, out_1, o
         def ok(a):
             return 0 <= a < TILES
 
-        def ms(a, g, pool=ps_scalar):
+        def mm(a, g):
             if ok(a):
-                bank = pool.tile([P, D], F32, tag="bank", name="bank")
+                bank = (ps_misc if g == VALUE else ps_rope).tile([P, D], F32, tag="bank", name="bank")
                 project(bank, a, g)
-                live[("s", a, g)] = bank
+                live[("b", a, g)] = bank
 
         def sq(a, g):
             if ok(a):
                 unused = squares.tile([P, D], BF16, name="unused")
-                nc.scalar.activation(out=unused[:], in_=live[("s", a, g)][:], func=ACT.Square, scale=1.0 / math.sqrt(D),
+                nc.scalar.activation(out=unused[:], in_=live[("b", a, g)][:], func=ACT.Square, scale=1.0 / math.sqrt(D),
                                      accum_out=mean_sq[:, a, g:g + 1])
 
         def rs_pow(column_group, g0, g1):
@@ -250,11 +250,11 @@ def tile_attention_pa_kernel(tc, x, wq, wkv, q_norm_w, k_norm_w, out_0, out_1, o
             if ok(a):
                 v = values.tile([P, D], F32, name="v")
                 nc.scalar.copy(out=v[:].rearrange("p (q j) -> p q j", j=4),
-                               in_=live[("s", a, VALUE)][:].rearrange("p (j q) -> p q j", j=4))
+                               in_=live[("b", a, VALUE)][:].rearrange("p (j q) -> p q j", j=4))
                 nc.sync.dma_start(out=v_out[a], in_=v[:])
 
         def spread_q_gain_again():
-            bank = ps_scalar.tile([P, D], F32, tag="bank", name="spread")
+            bank = ps_rope.tile([P, D], F32, tag="bank", name="spread")
             spread(bank, q_gain_cols)
             live["gain"] = bank
 
@@ -279,18 +279,12 @@ def tile_attention_pa_kernel(tc, x, wq, wkv, q_norm_w, k_norm_w, out_0, out_1, o
                                     in1=trig[:, a, :, :].rearrange("p (e r) i -> p e i r", e=2),
                                     op=ALU.mult)
 
-        def mv(a, g):
-            if ok(a):
-                bank = ps_vector.tile([P, D], F32, tag="bank", name="bank")
-                project(bank, a, g)
-                live[("v", a, g)] = bank
-
         def p(a, h):
             if not ok(a):
                 return
             halves = products.tile([P, 2, D], F32, name="halves")
             nc.vector.scalar_tensor_tensor(out=halves[:].rearrange("p e (i r) -> p (e i) r", r=2),
-                                           in0=live[("v", a, h)][:].unsqueeze(2).to_broadcast([P, D, 2]),
+                                           in0=live[("b", a, h)][:].unsqueeze(2).to_broadcast([P, D, 2]),
                                            scalar=rstd[:, a, h:h + 1],
                                            in1=(q_table[:, a, :, :].rearrange("p r n -> p n r") if a in GPSIMD_TABLES
                                                 else q_table[:, a, :, :].rearrange("p e (i r) -> p (e i) r", r=2)),
@@ -310,7 +304,7 @@ def tile_attention_pa_kernel(tc, x, wq, wkv, q_norm_w, k_norm_w, out_0, out_1, o
             if not ok(a):
                 return
             halves = k_products.tile([P, 2, D], F32, name="k_halves")
-            bank = live[("v", a, KEY)]
+            bank = live[("b", a, KEY)]
             nc.vector.tensor_tensor(out=halves[:].rearrange("p e (i r) -> p e i r", r=2),
                                     in0=bank[:].rearrange("p (e i) -> p e i", e=2).unsqueeze(3).to_broadcast([P, 2, PAIRS, 2]),
                                     in1=trig[:, a, :, :].rearrange("p (e r) i -> p e i r", e=2),
@@ -383,11 +377,11 @@ def tile_attention_pa_kernel(tc, x, wq, wkv, q_norm_w, k_norm_w, out_0, out_1, o
         angles_whole(6, TILES)
         angles_frac(4, 6)
         angles_frac(6, TILES)
-        t_x(0, ps_vector)
+        t_x(0, ps_rope)
         spread_q_gain_again()
         spread_q_gain()
-        t_w(0, 0, ps_vector)
-        t_w(0, 1, ps_vector)
+        t_w(0, 0, ps_rope)
+        t_w(0, 1, ps_rope)
         c_x(0, True)
         trig_plane(0, 2, 1)
         trig_abs(0, 2)
@@ -407,25 +401,25 @@ def tile_attention_pa_kernel(tc, x, wq, wkv, q_norm_w, k_norm_w, out_0, out_1, o
             trig_derived(a, a + 1, 3)
         c_w(0, 0, True)
         q_x(0, 2)
-        t_w(1, 0, ps_vector)
+        t_w(1, 0, ps_rope)
         c_w(0, 1, True)
-        t_w(1, 1, ps_vector)
-        t_w(3, 0, ps_scalar)
+        t_w(1, 1, ps_rope)
+        t_w(3, 0, ps_rope)
         c_w(1, 0, True)
         q_w(0, 1)
-        t_w(2, 0, ps_vector)
+        t_w(2, 0, ps_rope)
         t_w(3, 1, ps_turn)
         c_w(1, 1, True)
-        t_w(2, 1, ps_vector)
+        t_w(2, 1, ps_rope)
         t_w(KEY, 0, ps_turn)
         c_w(2, 0, True)
         c_w(2, 1, True)
         q_w(1, 2)
         q_w(2, 3)
         copy_q_gain()
-        t_w(KEY, 1, ps_scalar)
+        t_w(KEY, 1, ps_rope)
         c_w(3, 0, False)
-        t_x(2, ps_scalar)
+        t_x(2, ps_rope)
         c_w(3, 1, False)
         t_x(4, ps_turn)
         c_w(KEY, 0, False)
@@ -442,110 +436,80 @@ def tile_attention_pa_kernel(tc, x, wq, wkv, q_norm_w, k_norm_w, out_0, out_1, o
         for r in range(2):
             for a in (4, 5, 6):
                 tbh(a, r)
-        ms(0, 0)
-        ms(0, 1, ps_turn)
-        ms(0, 2, ps_turn)
-        ms(0, 3)
+        mm(0, 0)
+        mm(0, 1)
+        mm(0, KEY)
+        mm(0, 2)
+        mm(0, 3)
         sq(0, 0)
-        ms(0, KEY)
-        for h in range(3):
-            mv(0, h)
         sq(0, 1)
-        sq(0, 2)
-        sq(0, 3)
-        ms(1, 0)
-        rs(0, 0, KEY)
-        sq(0, KEY)
-        ms(1, 1)
-        rs(0, KEY, KEY + 1)
+        rs(0, 0, 2)
         tb(2)
         tb(3)
-        ms(1, 2)
-        for a in range(TILES):
-            last = a == TILES - 1
-            if last:
-                pk(a)
-                vc(a - 1)
-                ms(a, VALUE)
-                kg(a - 1)
-                mv(a, 2)
-                kb(a - 1)
-                ka(a)
-                vc(a)
+        sq(0, KEY)
+        for a in range(TILES - 1):
+            kg(a - 1)
             p(a, 0)
-            sq(a + 1, 0)
-            ms(a + 1, 3)
-            if last:
-                mv(a, 3)
-                kf(a - 1)
-                kg(a)
-                kb(a)
+            sq(a, 2)
+            mm(a + 1, 0)
+            sq(a, 3)
+            rs(a, 2, KEY + 1)
+            if a == 0:
+                t_w(VALUE, 0, ps_misc)
+                t_w(VALUE, 1, ps_turn)
+                spread_k_gain_1a()
+                c_w(VALUE, 0, False)
+                c_w(VALUE, 1, False)
+                spread_k_gain_1b()
+                spread_k_gain_2()
             p(a, 1)
             sub(a, 0)
-            sq(a + 1, 1)
-            ms(a + 1, KEY)
-            if not last:
-                mv(a, 3)
-                kf(a - 2)
-            sq(a + 1, 2)
-            if 0 < a < TILES - 1:
-                ms(a - 1, VALUE)
-            if last:
-                kf(a)
-            p(a, 2)
+            vc(a - 2)
+            mm(a + 1, 1)
+            sq(a + 1, 0)
+            pk(a)
             sub(a, 1)
-            if not last:
-                mv(a, KEY)
-            sq(a + 1, 3)
-            if a == 0:
-                t_w(VALUE, 0, ps_scalar)
-                t_w(VALUE, 1, ps_scalar)
-            else:
-                ms(a + 2, 0)
+            sq(a + 1, 1)
+            rs(a + 1, 0, 2)
+            mm(a + 1, KEY)
+            kb(a - 1)
+            ka(a)
+            p(a, 2)
+            sq(a + 1, KEY)
+            kf(a - 1)
+            mm(a + 1, 2)
+            if a > 0:
+                mm(a - 1, VALUE)
             p(a, 3)
             sub(a, 2)
-            sq(a + 1, KEY)
+            mm(a + 1, 3)
             if a == 0:
-                spread_k_gain_1a()
-            else:
-                ms(a + 2, 1)
-            rs(a + 1)
-            if a == TILES - 2:
-                mv(a + 1, KEY)
-            else:
-                mv(a + 1, 0)
-            if not last:
-                kg(a - 1)
-                if a == TILES - 2:
-                    kb(a - 1)
-                pk(a)
-            if a == 0:
-                c_w(VALUE, 0, False)
-                ms(2, 0)
-                c_w(VALUE, 1, False)
-                ms(2, 1)
                 q_w(VALUE, GROUPS)
-                spread_k_gain_1b()
-            elif not last:
-                vc(a - 1)
-            ms(a + 2, 2)
-            if a == TILES - 2:
-                mv(a + 1, 0)
-            else:
-                mv(a + 1, 1)
-            if a == TILES - 2:
-                kf(a - 1)
             sub(a, 3)
-            if a == TILES - 2:
-                ms(a, VALUE)
-                mv(a + 1, 1)
-            else:
-                mv(a + 1, 2)
-            if a == 0:
-                spread_k_gain_2()
-            if not last:
-                if a < TILES - 2:
-                    kb(a - 1)
-                ka(a)
             if a == 2:
                 tb(7)
+        a = TILES - 1
+        kg(a - 1)
+        pk(a)
+        sq(a, 2)
+        sq(a, 3)
+        rs(a, 2, KEY + 1)
+        kb(a - 1)
+        ka(a)
+        p(a, 0)
+        vc(a - 2)
+        kf(a - 1)
+        mm(a - 1, VALUE)
+        kg(a)
+        p(a, 1)
+        sub(a, 0)
+        kb(a)
+        vc(a - 1)
+        p(a, 2)
+        sub(a, 1)
+        kf(a)
+        mm(a, VALUE)
+        p(a, 3)
+        sub(a, 2)
+        vc(a)
+        sub(a, 3)

@@ -441,27 +441,30 @@ def tile_attention_pa_kernel(tc, x, wq, wkv, q_norm_w, k_norm_w, out_0, out_1, o
         mm(0, KEY)
         mm(0, 2)
         mm(0, 3)
+        t_w(VALUE, 0, ps_turn)
+        t_w(VALUE, 1, ps_turn)
         sq(0, 0)
         sq(0, 1)
         rs(0, 0, 2)
         tb(2)
         tb(3)
         sq(0, KEY)
+        sq(0, 2)
+        sq(0, 3)
+        rs(0, 2, KEY + 1)
+        c_w(VALUE, 0, False)
+        c_w(VALUE, 1, False)
+        spread_k_gain_1a()
+        spread_k_gain_1b()
+        spread_k_gain_2()
         for a in range(TILES - 1):
             kg(a - 1)
             p(a, 0)
-            sq(a, 2)
             mm(a + 1, 0)
-            sq(a, 3)
-            rs(a, 2, KEY + 1)
-            if a == 0:
-                t_w(VALUE, 0, ps_misc)
-                t_w(VALUE, 1, ps_turn)
-                spread_k_gain_1a()
-                c_w(VALUE, 0, False)
-                c_w(VALUE, 1, False)
-                spread_k_gain_1b()
-                spread_k_gain_2()
+            if a > 0:
+                sq(a, 2)
+                sq(a, 3)
+                rs(a, 2, KEY + 1)
             p(a, 1)
             sub(a, 0)
             vc(a - 2)

@@ -489,7 +489,7 @@ def tile_attention_pa_kernel(tc, x, wq, wkv, q_norm_w, k_norm_w, out_0, out_1, o
             if a == 0:
                 q_w(VALUE, GROUPS)
             sub(a, 3)
-            if a == 2:
+            if a == 0:
                 tb(7)
         a = TILES - 1
         kg(a - 1)

@@ -353,7 +353,7 @@ def tile_attention_pa_kernel(tc, x, wq, wkv, q_norm_w, k_norm_w, out_0, out_1, o
         nc.sync.dma_start(out=k_gain_cols[:], in_=k_norm_w.rearrange("(p c) -> p c", c=4))
         nc.scalar.activation(out=warm[:], in_=token[:, 0:1], func=ACT.Sin, scale=0.0)
         make_identity(nc, ident[:])
-        make_identity(nc, ident_bf[:])
+        nc.scalar.copy(out=ident_bf[:], in_=ident[:])
         load_x(0)
         for g in range(HEADS):
             load_w(g)

import math
from contextlib import ExitStack

import concourse.mybir as mybir
from concourse.masks import make_identity

FLOPS = 2 * 1024 * 512 * 3072

F32 = mybir.dt.float32
BF16 = mybir.dt.bfloat16
I32 = mybir.dt.int32
U32 = mybir.dt.uint32
U8 = mybir.dt.uint8
E5M2_X4 = mybir.dt.float8_e5m2_x4
ALU = mybir.AluOpType
ACT = mybir.ActivationFunctionType

P = 128
TOKENS = 1024
D = 512
TILES = TOKENS // P
PAIRS = D // 2
HEADS = 4
KEY = 4
VALUE = 5
GROUPS = 6
EPS = 1.1920929e-07
TWO_PI = 2.0 * math.pi
STEP = 10000.0 ** (-1.0 / PAIRS)
GPSIMD_TABLES = (4, 5, 6, 7)
REDUCED = sum(1 for i in range(PAIRS) if (TOKENS - 1) * STEP ** i / TWO_PI > 0.5)


def tile_attention_pa_kernel(tc, x, wq, wkv, q_norm_w, k_norm_w, out_0, out_1, out_2):
    nc = tc.nc
    with ExitStack() as ctx:
        keep = ctx.enter_context(tc.tile_pool(name="keep", bufs=1))
        products = ctx.enter_context(tc.tile_pool(name="products", bufs=6))
        results = ctx.enter_context(tc.tile_pool(name="results", bufs=8))
        values = ctx.enter_context(tc.tile_pool(name="values", bufs=3))
        squares = ctx.enter_context(tc.tile_pool(name="squares", bufs=2))
        turned_k = ctx.enter_context(tc.tile_pool(name="turned_k", bufs=2))
        ps_turn = ctx.enter_context(tc.psum_pool(name="ps_turn", bufs=2))
        k_products = ctx.enter_context(tc.tile_pool(name="k_products", bufs=3))
        ps_rope = ctx.enter_context(tc.psum_pool(name="ps_rope", bufs=5))
        ps_misc = ctx.enter_context(tc.psum_pool(name="ps_misc", bufs=1))

        ident = keep.tile([P, P], F32, name="ident")
        ident_bf = keep.tile([P, P], BF16, name="ident_bf")
        q_gain_cols = keep.tile([P, 4], BF16, name="q_gain_cols")
        k_gain_cols = keep.tile([P, 4], BF16, name="k_gain_cols")
        k_gain = keep.tile([P, D], F32, name="k_gain")
        k_gain_col = keep.tile([P, D // P], F32, name="k_gain_col")
        x_rows = keep.tile([P, TILES, D], BF16, name="x_rows")
        w_rows = keep.tile([P, 4 * GROUPS, D], BF16, name="w_rows")
        x_grouped = keep.tile([P, 4 * TOKENS], BF16, name="x_grouped", align_bytes=64)
        w_grouped = keep.tile([P, 4 * GROUPS * D], BF16, name="w_grouped", align_bytes=64)
        x_codes = keep.tile([P, TOKENS], U32, name="x_codes", align_bytes=64)
        x_scales = keep.tile([P, TOKENS], U8, name="x_scales", align_bytes=64)
        w_codes = keep.tile([P, GROUPS * D], U32, name="w_codes", align_bytes=64)
        w_scales = keep.tile([P, GROUPS * D], U8, name="w_scales", align_bytes=64)
        one = keep.tile([P, 1], F32, name="one")
        warm = keep.tile([P, 1], F32, name="warm")
        turns = keep.tile([P, PAIRS], F32, name="turns")
        token = keep.tile([P, TILES], F32, name="token")
        whole = keep.tile([P, TILES, PAIRS], I32, name="whole")
        frac = keep.tile([P, TILES, PAIRS], F32, name="frac")
        trig = keep.tile([P, TILES, 4, PAIRS], F32, name="trig")
        q_table = keep.tile([P, TILES, 2, D], F32, name="q_table")
        gain_planes = keep.tile([P, 2, PAIRS], F32, name="gain_planes")
        mean_sq = keep.tile([P, TILES + 1, 8], F32, name="mean_sq")
        mean_eps = keep.tile([P, TILES + 1, 8], F32, name="mean_eps")
        rstd = keep.tile([P, TILES + 1, 8], F32, name="rstd")
        minus_half = keep.tile([P, 8], F32, name="minus_half")


        ctx.enter_context(tc.manual_schedule(engines={mybir.EngineType.PE, mybir.EngineType.DVE,
                                                      mybir.EngineType.Activation, mybir.EngineType.Pool}))
        live = {}

        x_view = x.flatten_outer_dims().rearrange("(p a) k -> p a k", a=TILES)
        q_view = wq.rearrange("(h b p e) k -> h p b (e k)", h=HEADS, p=P, e=2)
        k_view = wkv.rearrange("(h b p e) k -> h p b (e k)", h=2, p=P, e=2)
        v_view = wkv.rearrange("(h p j) k -> h p (j k)", h=2, p=P)
        w_slots = w_rows[:].rearrange("p (g b e) k -> p g b (e k)", b=2, e=2)
        q_out = out_0.rearrange("o h (p a) d -> (o h) a p d", a=TILES)
        k_out = out_1.rearrange("o (p a) d -> (o a) p d", a=TILES)
        v_out = out_2.rearrange("o (p a) d -> (o a) p d", a=TILES)
        x_words = x_grouped[:].bitcast(F32).rearrange("p (c r u) -> p c r u", r=P, u=2)
        w_words = w_grouped[:].bitcast(F32).rearrange("p (c r u) -> p c r u", r=P, u=2)

        def load_x(a):
            nc.sync.dma_start(out=x_rows[:, a:a + 2, :], in_=x_view[:, a:a + 2, :])

        def load_w(g):
            if g < HEADS:
                nc.sync.dma_start(out=w_slots[:, g], in_=q_view[g])
            elif g == KEY:
                nc.sync.dma_start(out=w_slots[:, KEY], in_=k_view[0])
            else:
                nc.sync.dma_start(out=w_rows[:, 4 * VALUE:4 * VALUE + 4, :].rearrange("p j k -> p (j k)"), in_=v_view[1])

        def make_turns():
            for i in range(4):
                nc.vector.tensor_scalar_mul(out=turns[:, i:i + 1], in0=one[:], scalar1=STEP ** i / TWO_PI)
            width = 4
            while width < PAIRS:
                for m in range(1, 4):
                    nc.vector.tensor_scalar_mul(out=turns[:, m * width:(m + 1) * width], in0=turns[:, 0:width],
                                                scalar1=STEP ** (m * width))
                width *= 4

        def seed_angles():
            for i in range(4):
                nc.vector.tensor_scalar_mul(out=frac[:, :, i:i + 1], in0=token[:].unsqueeze(2), scalar1=STEP ** i / TWO_PI)

        def widen_angles(a0, a1, width, blocks):
            for m in blocks:
                nc.vector.tensor_scalar_mul(out=frac[:, a0:a1, m * width:(m + 1) * width], in0=frac[:, a0:a1, 0:width],
                                            scalar1=STEP ** (m * width))

        def angles_mul(a0, a1):
            for a in range(a0, a1):
                nc.vector.tensor_scalar_mul(out=frac[:, a, :], in0=turns[:], scalar1=token[:, a:a + 1])

        def angles_whole(a0, a1):
            nc.vector.tensor_copy(out=whole[:, a0:a1, 0:REDUCED], in_=frac[:, a0:a1, 0:REDUCED])

        def angles_frac(a0, a1):
            nc.vector.tensor_tensor(out=frac[:, a0:a1, 0:REDUCED], in0=frac[:, a0:a1, 0:REDUCED],
                                    in1=whole[:, a0:a1, 0:REDUCED], op=ALU.subtract)

        def trig_abs(a0, a1):
            nc.scalar.activation(out=frac[:, a0:a1, 0:REDUCED], in_=frac[:, a0:a1, 0:REDUCED], func=ACT.Abs)

        def trig_plane(a0, a1, plane, c0=0, c1=REDUCED):
            if plane == 0:
                nc.scalar.activation(out=trig[:, a0:a1, 0, c0:c1], in_=frac[:, a0:a1, c0:c1], func=ACT.Sin,
                                     scale=-TWO_PI, bias=math.pi / 2)
            else:
                nc.scalar.activation(out=trig[:, a0:a1, 1, c0:c1], in_=frac[:, a0:a1, c0:c1], func=ACT.Sin, scale=TWO_PI)

        def trig_derived(a0, a1, plane):
            if plane == 3:
                nc.sync.dma_start(out=trig[:, a0:a1, 3, :], in_=trig[:, a0:a1, 0, :])
                return
            nc.gpsimd.tensor_scalar(out=trig[:, a0:a1, 2, :], in0=trig[:, a0:a1, 1, :],
                                    scalar1=-1.0, scalar2=0.0, op0=ALU.mult, op1=ALU.add)

        def spread(bank, cols):
            for c in range(4):
                nc.tensor.matmul(out=bank[:, c:D:4], lhsT=cols[:, c:c + 1].to_broadcast([P, P]), rhs=ident_bf[:],
                                 start=True, stop=True)

        def spread_q_gain():
            q_gain = ps_misc.tile([P, D], F32, tag="bank", name="q_gain")
            spread(q_gain, q_gain_cols)
            live["q_gain"] = q_gain

        def spread_k_gain_1a():
            bank = ps_turn.tile([P, D], F32, tag="bank", name="spread")
            spread(bank, k_gain_cols)
            live["k_gain"] = bank

        def spread_k_gain_1b():
            nc.scalar.copy(out=k_gain[:], in_=live["k_gain"][:])

        def spread_k_gain_2():
            turned = ps_turn.tile([P, D // P, P], F32, tag="bank", name="turned")
            for b in range(D // P):
                nc.tensor.transpose(turned[:, b, :], k_gain[:, P * b:P * (b + 1)], ident[:])
            nc.scalar.copy(out=k_gain_col[:], in_=turned[:, :, 0])

        def t_rows(key, rows, pool):
            bank = pool.tile([P, 2, 2, P], F32, tag="bank", name="bank")
            for c in range(2):
                words = rows[:, c, :].bitcast(F32)
                for u in range(2):
                    nc.tensor.transpose(bank[:, c, u, :], words[:, u:PAIRS:2], ident[:])
            live[key] = bank

        def c_rows(key, grouped, on_vector):
            view = live[key][:].rearrange("p c u r -> p c r u")
            if on_vector:
                nc.vector.tensor_copy(out=grouped, in_=view)
            else:
                nc.scalar.copy(out=grouped, in_=view)

        def t_x(a, pool):
            t_rows(("x", a), x_rows[:, a:a + 2, :], pool)

        def c_x(a, on_vector):
            c_rows(("x", a), x_words[:, a:a + 2, :, :], on_vector)

        def q_x(a0, a1):
            nc.vector.quantize_mx(out=x_codes[:, P * a0:P * a1].bitcast(E5M2_X4), scales=x_scales[:, P * a0:P * a1],
                                  in_=x_grouped[:, 4 * P * a0:4 * P * a1])

        def t_w(g, half, pool):
            first = 4 * g + 2 * half
            if g == VALUE:
                rows = w_rows[:, first:first + 2, :]
            else:
                rows = w_rows[:, 4 * g + half:4 * g + 4:2, :]
            t_rows(("w", g, half), rows, pool)

        def c_w(g, half, on_vector):
            first = 4 * g + 2 * half
            c_rows(("w", g, half), w_words[:, first:first + 2, :, :], on_vector)

        def q_w(g0, g1):
            nc.vector.quantize_mx(out=w_codes[:, D * g0:D * g1].bitcast(E5M2_X4), scales=w_scales[:, D * g0:D * g1],
                                  in_=w_grouped[:, 4 * D * g0:4 * D * g1])

        def project(bank, a, g):
            nc.tensor.matmul_mx(out=bank[:],
                                lhsT=x_codes[:, P * a:P * (a + 1)].bitcast(E5M2_X4),
                                lhsT_scale=x_scales[:, P * a:P * (a + 1)],
                                rhs=w_codes[:, D * g:D * (g + 1)].bitcast(E5M2_X4),
                                rhs_scale=w_scales[:, D * g:D * (g + 1)],
                                start=True, stop=True)

        def ok(a):
            return 0 <= a < TILES

        def mm(a, g):
            if ok(a):
                bank = (ps_misc if g == VALUE else ps_rope).tile([P, D], F32, tag="bank", name="bank")
                project(bank, a, g)
                live[("b", a, g)] = bank

        def sq(a, g):
            if ok(a):
                unused = squares.tile([P, D], BF16, name="unused")
                nc.scalar.activation(out=unused[:], in_=live[("b", a, g)][:], func=ACT.Square, scale=1.0 / math.sqrt(D),
                                     accum_out=mean_sq[:, a, g:g + 1])

        def rs_pow(column_group, g0, g1):
            nc.scalar.activation(out=mean_eps[:, column_group, g0:g1], in_=mean_sq[:, column_group, g0:g1],
                                 func=ACT.Copy, bias=EPS)
            nc.gpsimd.tensor_tensor(out=rstd[:, column_group, g0:g1], in0=mean_eps[:, column_group, g0:g1],
                                    in1=minus_half[:, g0:g1], op=ALU.pow)

        def rs(a, g0=0, g1=KEY + 1):
            if ok(a):
                nc.scalar.activation(out=rstd[:, a, g0:g1], in_=mean_sq[:, a, g0:g1],
                                     func=ACT.Abs_reciprocal_sqrt, bias=EPS)

        def vc(a):
            if ok(a):
                v = values.tile([P, D], F32, name="v")
                nc.scalar.copy(out=v[:].rearrange("p (q j) -> p q j", j=4),
                               in_=live[("b", a, VALUE)][:].rearrange("p (j q) -> p q j", j=4))
                nc.sync.dma_start(out=v_out[a], in_=v[:])

        def spread_q_gain_again():
            bank = ps_rope.tile([P, D], F32, tag="bank", name="spread")
            spread(bank, q_gain_cols)
            live["gain"] = bank

        def copy_q_gain():
            nc.scalar.copy(out=gain_planes[:], in_=live["gain"][:].rearrange("p (i r) -> p r i", r=2))

        def tbh(a, r):
            nc.gpsimd.tensor_tensor(out=q_table[:, a, r, :].rearrange("p (e i) -> p e i", e=2),
                                    in0=gain_planes[:, r, :].unsqueeze(1).to_broadcast([P, 2, PAIRS]),
                                    in1=trig[:, a, r:4:2, :], op=ALU.mult)

        def tb(a):
            if not ok(a):
                return
            if a in GPSIMD_TABLES:
                for r in range(2):
                    tbh(a, r)
                return
            nc.vector.tensor_tensor(out=q_table[:, a, :, :].rearrange("p e (i r) -> p e i r", r=2),
                                    in0=live["q_gain"][:].rearrange("p (i r) -> p i r", r=2).unsqueeze(1)
                                    .to_broadcast([P, 2, PAIRS, 2]),
                                    in1=trig[:, a, :, :].rearrange("p (e r) i -> p e i r", e=2),
                                    op=ALU.mult)

        def p(a, h):
            if not ok(a):
                return
            halves = products.tile([P, 2, D], F32, name="halves")
            nc.vector.scalar_tensor_tensor(out=halves[:].rearrange("p e (i r) -> p (e i) r", r=2),
                                           in0=live[("b", a, h)][:].unsqueeze(2).to_broadcast([P, D, 2]),
                                           scalar=rstd[:, a, h:h + 1],
                                           in1=(q_table[:, a, :, :].rearrange("p r n -> p n r") if a in GPSIMD_TABLES
                                                else q_table[:, a, :, :].rearrange("p e (i r) -> p (e i) r", r=2)),
                                           op0=ALU.mult, op1=ALU.mult)
            live[("h", a, h)] = halves

        def sub(a, h):
            if not ok(a):
                return
            halves = live[("h", a, h)]
            q = results.tile([P, D], F32, tag="result", name="q")
            engine = nc.vector if (a == TILES - 1 and h == HEADS - 1) else nc.gpsimd
            engine.tensor_tensor(out=q[:], in0=halves[:, 0, :], in1=halves[:, 1, :], op=ALU.add)
            nc.sync.dma_start(out=q_out[h, a], in_=q[:])

        def pk(a):
            if not ok(a):
                return
            halves = k_products.tile([P, 2, D], F32, name="k_halves")
            bank = live[("b", a, KEY)]
            nc.vector.tensor_tensor(out=halves[:].rearrange("p e (i r) -> p e i r", r=2),
                                    in0=bank[:].rearrange("p (e i) -> p e i", e=2).unsqueeze(3).to_broadcast([P, 2, PAIRS, 2]),
                                    in1=trig[:, a, :, :].rearrange("p (e r) i -> p e i r", e=2),
                                    op=ALU.mult)
            live[("h", a, KEY)] = halves

        def ka(a):
            if not ok(a):
                return
            halves = live[("h", a, KEY)]
            by_feature = ps_turn.tile([P, D // P, P], F32, tag="bank", name="by_feature")
            for b in range(D // P):
                for e in range(2):
                    nc.tensor.matmul(out=by_feature[:, b, :], lhsT=halves[:, e, P * b:P * (b + 1)], rhs=ident[:],
                                     is_transpose=True, start=(e == 0), stop=(e == 1))
            live[("f", a)] = by_feature

        def kg(a):
            if not ok(a):
                return
            gained = turned_k.tile([P, D // P, P], F32, name="gained")
            for b in range(D // P):
                nc.scalar.activation(out=gained[:, b, :], in_=live[("f", a)][:, b, :], func=ACT.Copy,
                                     scale=k_gain_col[:, b:b + 1])
            live[("g", a)] = gained

        def kb(a):
            if not ok(a):
                return
            by_token = ps_turn.tile([P, D // P, P], F32, tag="bank", name="by_token")
            for b in range(D // P):
                nc.tensor.transpose(by_token[:, b, :], live[("g", a)][:, b, :], ident[:])
            live[("t", a)] = by_token

        def kf(a):
            if not ok(a):
                return
            k = results.tile([P, D], F32, tag="result", name="k")
            nc.scalar.activation(out=k[:], in_=live[("t", a)][:].rearrange("p b d -> p (b d)"), func=ACT.Copy,
                                 scale=rstd[:, a, KEY:KEY + 1])
            nc.sync.dma_start(out=k_out[a], in_=k[:])

        nc.gpsimd.iota(token[:], pattern=[[1, TILES]], base=0, channel_multiplier=TILES,
                       allow_small_or_imprecise_dtypes=True)
        nc.sync.dma_start(out=q_gain_cols[:], in_=q_norm_w.rearrange("(p c) -> p c", c=4))
        nc.sync.dma_start(out=k_gain_cols[:], in_=k_norm_w.rearrange("(p c) -> p c", c=4))
        nc.scalar.activation(out=warm[:], in_=token[:, 0:1], func=ACT.Sin, scale=0.0)
        make_identity(nc, ident[:])
        nc.scalar.copy(out=ident_bf[:], in_=ident[:])
        load_x(0)
        for g in range(HEADS):
            load_w(g)
        load_w(KEY)
        for a in range(2, TILES, 2):
            load_x(a)
        load_w(VALUE)
        seed_angles()
        widen_angles(0, TILES, 4, (1, 2, 3))
        widen_angles(0, TILES, 16, (1, 2, 3))
        widen_angles(0, TILES, 64, (2, 3))
        trig_plane(0, TILES, 1, REDUCED, PAIRS)
        trig_plane(0, TILES, 0, REDUCED, PAIRS)
        widen_angles(0, 4, 64, (1,))
        widen_angles(4, TILES, 64, (1,))
        angles_whole(0, 2)
        angles_whole(2, 4)
        angles_frac(0, 2)
        angles_frac(2, 4)
        angles_whole(4, 6)
        angles_whole(6, TILES)
        angles_frac(4, 6)
        angles_frac(6, TILES)
        t_x(0, ps_rope)
        spread_q_gain_again()
        spread_q_gain()
        t_w(0, 0, ps_rope)
        t_w(0, 1, ps_rope)
        c_x(0, True)
        trig_plane(0, 2, 1)
        trig_abs(0, 2)
        trig_plane(2, 4, 1)
        trig_abs(2, 4)
        trig_plane(0, 2, 0)
        trig_plane(4, TILES, 1)
        trig_abs(4, TILES)
        trig_plane(2, 4, 0)
        trig_plane(4, TILES, 0)
        trig_derived(0, 2, 2)
        trig_derived(2, 4, 2)
        trig_derived(0, 2, 3)
        trig_derived(4, TILES, 2)
        trig_derived(2, 4, 3)
        for a in range(4, TILES):
            trig_derived(a, a + 1, 3)
        c_w(0, 0, True)
        q_x(0, 2)
        t_w(1, 0, ps_rope)
        c_w(0, 1, True)
        t_w(1, 1, ps_rope)
        t_w(3, 0, ps_rope)
        c_w(1, 0, True)
        q_w(0, 1)
        t_w(2, 0, ps_rope)
        t_w(3, 1, ps_turn)
        c_w(1, 1, True)
        t_w(2, 1, ps_rope)
        t_w(KEY, 0, ps_turn)
        c_w(2, 0, True)
        c_w(2, 1, True)
        q_w(1, 2)
        q_w(2, 3)
        copy_q_gain()
        t_w(KEY, 1, ps_rope)
        c_w(3, 0, False)
        t_x(2, ps_rope)
        c_w(3, 1, False)
        t_x(4, ps_turn)
        c_w(KEY, 0, False)
        t_x(6, ps_turn)
        c_w(KEY, 1, False)
        c_x(2, False)
        c_x(4, False)
        c_x(6, False)
        tb(0)
        q_w(3, KEY + 1)
        q_x(2, 4)
        tb(1)
        q_x(4, TILES)
        for r in range(2):
            for a in (4, 5, 6):
                tbh(a, r)
        mm(0, 0)
        mm(0, 1)
        mm(0, KEY)
        mm(0, 2)
        mm(0, 3)
        t_w(VALUE, 0, ps_turn)
        t_w(VALUE, 1, ps_turn)
        sq(0, 0)
        sq(0, 1)
        rs(0, 0, 2)
        tb(2)
        tb(3)
        sq(0, KEY)
        sq(0, 2)
        sq(0, 3)
        rs(0, 2, KEY + 1)
        c_w(VALUE, 0, False)
        c_w(VALUE, 1, False)
        spread_k_gain_1a()
        spread_k_gain_1b()
        spread_k_gain_2()
        for a in range(TILES - 1):
            kg(a - 1)
            p(a, 0)
            mm(a + 1, 0)
            if a > 0:
                sq(a, 2)
                sq(a, 3)
                rs(a, 2, KEY + 1)
            p(a, 1)
            sub(a, 0)
            vc(a - 2)
            mm(a + 1, 1)
            sq(a + 1, 0)
            pk(a)
            sub(a, 1)
            sq(a + 1, 1)
            rs(a + 1, 0, 2)
            mm(a + 1, KEY)
            kb(a - 1)
            ka(a)
            p(a, 2)
            sq(a + 1, KEY)
            kf(a - 1)
            mm(a + 1, 2)
            if a > 0:
                mm(a - 1, VALUE)
            p(a, 3)
            sub(a, 2)
            mm(a + 1, 3)
            if a == 0:
                q_w(VALUE, GROUPS)
            sub(a, 3)
            if a == 0:
                tb(7)
        a = TILES - 1
        kg(a - 1)
        pk(a)
        sq(a, 2)
        sq(a, 3)
        rs(a, 2, KEY + 1)
        kb(a - 1)
        ka(a)
        p(a, 0)
        vc(a - 2)
        kf(a - 1)
        mm(a - 1, VALUE)
        kg(a)
        p(a, 1)
        sub(a, 0)
        kb(a)
        vc(a - 1)
        p(a, 2)
        sub(a, 1)
        kf(a)
        mm(a, VALUE)
        p(a, 3)
        sub(a, 2)
        vc(a)
        sub(a, 3)
